import numpy as np
import ml_dtypes


def mxq(x, axis, fmt="e4m3"):
    dtype, down = {"e4m3": (ml_dtypes.float8_e4m3fn, 7), "e5m2": (ml_dtypes.float8_e5m2, 14)}[fmt]
    v = np.moveaxis(np.asarray(x, np.float32).astype(ml_dtypes.bfloat16).astype(np.float64), axis, -1)
    blocks = v.reshape(v.shape[:-1] + (-1, 32))
    amax = np.abs(blocks).max(-1, keepdims=True)
    byte = np.maximum(np.where(amax > 0, np.frexp(amax)[1] - 1 + 127, 0) - down, 1)
    scale = np.exp2(byte - 127.0)
    codes = (blocks / scale).astype(np.float32).astype(dtype).astype(np.float64)
    return np.moveaxis((codes * scale).reshape(v.shape), -1, axis)


WIDE = False


def mx_kscale(k):
    if not WIDE:
        return np.ones(k)
    levels = np.array([10, -10, 5, -5, 0])
    a = np.random.permutation(np.resize(levels, k // 512 * 4)).reshape(k // 512, 4)
    idx = np.arange(k)
    return np.exp2(a[idx // 512, idx % 128 // 32])


BF16 = ml_dtypes.bfloat16


def bf(x):
    return np.asarray(x, np.float32).astype(BF16)


def f64(x):
    return np.asarray(x).astype(np.float64)


B, IN, OUT, G, P = 8192, 512, 128, 5, 3
NB = G + P
LO, HI = -1.0, 1.0


def silu(v):
    return v / (1.0 + np.exp(-v))


def b_splines(x, grid):
    xe = x[..., None]
    bases = np.logical_and(xe >= grid[:, :-1], xe < grid[:, 1:]).astype(np.float64)
    for k in range(1, P + 1):
        left = (xe - grid[:, :-(k + 1)]) / (grid[:, k:-1] - grid[:, :-(k + 1)])
        right = (grid[:, k + 1:] - xe) / (grid[:, k + 1:] - grid[:, 1:-k])
        bases = left * bases[..., :-1] + right * bases[..., 1:]
    return bases


def setup_inputs():
    s = mx_kscale(IN)
    s = s / s.max()
    h = (HI - LO) / G
    g = np.arange(-P, G + P + 1) * h + LO
    return {"x": bf(np.random.uniform(LO, HI, (B, IN)) * s),
            "base_weight": bf(np.random.standard_normal((OUT, IN)) * 2.5 / np.sqrt(IN) / s[None, :]),
            "spline_weight": bf(np.random.standard_normal((OUT, IN, NB))),
            "spline_scaler": bf(np.random.standard_normal((OUT, IN)) * 1.5 / np.sqrt(IN)),
            "grid": bf(np.tile(g[None, :], (IN, 1)))}


def reference(x, base_weight, spline_weight, spline_scaler, grid):
    x, grid = f64(x), f64(grid)
    base_out = mxq(silu(x), 1, "e4m3") @ mxq(f64(base_weight), 1, "e4m3").T
    ssw = f64(spline_weight) * f64(spline_scaler)[..., None]
    bs = b_splines(x, grid).reshape(x.shape[0], -1)
    spline_out = mxq(bs, 1, "e4m3") @ mxq(ssw.reshape(OUT, -1), 1, "e4m3").T
    return base_out + spline_out

@@ -1,0 +1,225 @@
+from contextlib import ExitStack
+
+import concourse.bass as bass
+import concourse.mybir as mybir
+import concourse.tile as tile
+from concourse.masks import make_identity
+
+F32 = mybir.dt.float32
+BF16 = mybir.dt.bfloat16
+U32 = mybir.dt.uint32
+U8 = mybir.dt.uint8
+FP8X4 = mybir.dt.float8_e4m3fn_x4
+ALU = mybir.AluOpType
+ACT = mybir.ActivationFunctionType
+
+P = 128
+B, IN, OUT, NB, NK = 8192, 512, 128, 8, 12
+NG = IN // P
+CH = 1024
+NCH = B // CH
+NPASS = 2 * NG + 1
+FLOPS = 2 * B * (IN + IN * NB) * OUT
+
+DVE_TS = (("W", 1), ("W", 4), ("V", 6))
+
+
+def tile_bsplinekanlayer_t_kernel(tc, x, base_weight, spline_weight, spline_scaler, grid, out):
+    nc = tc.nc
+    with ExitStack() as ctx:
+        const = ctx.enter_context(tc.tile_pool(name="const", bufs=1))
+
+        ident = const.tile([P, P], BF16)
+        make_identity(nc, ident[:])
+
+        g_bf = const.tile([P, NG, NK], BF16)
+        nc.sync.dma_start(out=g_bf[:], in_=grid.rearrange("(g p) k -> p g k", p=P))
+        T = const.tile([P, NG, NK], F32)
+        nc.vector.tensor_copy(out=T[:], in_=g_bf[:])
+        negT = const.tile([P, NG, NK], F32)
+        nc.vector.tensor_scalar(out=negT[:], in0=T[:], scalar1=-1.0, scalar2=None, op0=ALU.mult)
+        D1 = const.tile([P, NG, 11], F32)
+        nc.vector.tensor_tensor(out=D1[:], in0=T[:, :, 1:12], in1=T[:, :, 0:11], op=ALU.subtract)
+        D2 = const.tile([P, NG, 10], F32)
+        nc.vector.tensor_tensor(out=D2[:], in0=T[:, :, 2:12], in1=T[:, :, 0:10], op=ALU.subtract)
+        D3 = const.tile([P, NG, 9], F32)
+        nc.vector.tensor_tensor(out=D3[:], in0=T[:, :, 3:12], in1=T[:, :, 0:9], op=ALU.subtract)
+        D4 = const.tile([P, NG, 8], F32)
+        nc.vector.tensor_tensor(out=D4[:], in0=T[:, :, 4:12], in1=T[:, :, 0:8], op=ALU.subtract)
+
+        def prod(name, factors):
+            acc = const.tile([P, NG, NB], F32, name=name)
+            nc.vector.tensor_tensor(out=acc[:], in0=factors[0], in1=factors[1], op=ALU.mult)
+            for f in factors[2:]:
+                nc.vector.tensor_tensor(out=acc[:], in0=acc[:], in1=f, op=ALU.mult)
+            return acc
+
+        a0d = prod("a0d", [D1[:, :, 0:8], D2[:, :, 0:8], D3[:, :, 0:8]])
+        a0 = const.tile([P, NG, NB], F32)
+        nc.vector.reciprocal(out=a0[:], in_=a0d[:])
+        b0d = prod("b0d", [D3[:, :, 1:9], D2[:, :, 2:10], D1[:, :, 3:11]])
+        b0 = const.tile([P, NG, NB], F32)
+        nc.vector.reciprocal(out=b0[:], in_=b0d[:])
+        nb0 = const.tile([P, NG, NB], F32)
+        nc.vector.tensor_scalar(out=nb0[:], in0=b0[:], scalar1=-1.0, scalar2=None, op0=ALU.mult)
+        a1d = prod("a1d", [D1[:, :, 0:8], D1[:, :, 1:9], D2[:, :, 1:9], D3[:, :, 1:9]])
+        a1r = const.tile([P, NG, NB], F32)
+        nc.vector.reciprocal(out=a1r[:], in_=a1d[:])
+        cV = const.tile([P, NG, NB], F32)
+        nc.vector.tensor_tensor(out=cV[:], in0=a1r[:], in1=D4[:], op=ALU.mult)
+        b1d = prod("b1d", [D3[:, :, 0:8], D2[:, :, 1:9], D1[:, :, 2:10], D1[:, :, 3:11]])
+        b1r = const.tile([P, NG, NB], F32)
+        nc.vector.reciprocal(out=b1r[:], in_=b1d[:])
+        cWp = const.tile([P, NG, NB], F32)
+        nc.vector.tensor_tensor(out=cWp[:], in0=b1r[:], in1=D4[:], op=ALU.mult)
+        cW = const.tile([P, NG, NB], F32)
+        nc.vector.tensor_scalar(out=cW[:], in0=cWp[:], scalar1=-1.0, scalar2=None, op0=ALU.mult)
+
+        wcodes = const.tile([P, NPASS, OUT], U32, align_bytes=64)
+        wscales = const.tile([P, NPASS, OUT], U8, align_bytes=64)
+        with tc.tile_pool(name="wsetup", bufs=1) as wp, tc.psum_pool(name="wps", bufs=2) as wps:
+            sw = wp.tile([P, IN * NB], BF16)
+            nc.sync.dma_start(out=sw[:], in_=spline_weight.rearrange("o i j -> o (i j)"))
+            sc = wp.tile([P, IN], BF16)
+            nc.sync.dma_start(out=sc[:], in_=spline_scaler)
+            bw = wp.tile([P, IN], BF16)
+            nc.sync.dma_start(out=bw[:], in_=base_weight)
+            ssw = wp.tile([P, NB, IN], BF16)
+            nc.vector.tensor_tensor(
+                out=ssw[:],
+                in0=sw[:].rearrange("o (i j) -> o j i", j=NB),
+                in1=sc[:].unsqueeze(1).to_broadcast([P, NB, IN]),
+                op=ALU.mult,
+            )
+            wgrp = wp.tile([P, NPASS, OUT, 4], BF16, align_bytes=64)
+            for g in range(NG):
+                ps_w = wps.tile([P, NB, P], BF16)
+                for j in range(NB):
+                    nc.tensor.transpose(ps_w[:, j, :], ssw[:, j, g * P:(g + 1) * P], ident[:])
+                for h in range(2):
+                    nc.vector.tensor_copy(
+                        out=wgrp[:, 2 * g + h, :, :],
+                        in_=ps_w[:, 4 * h:4 * h + 4, :].rearrange("p t o -> p o t"),
+                    )
+            ps_b = wps.tile([P, NB, P], BF16, tag="ps_w")
+            for t in range(NG):
+                nc.tensor.transpose(ps_b[:, t, :], bw[:, t * P:(t + 1) * P], ident[:])
+            nc.vector.tensor_copy(out=wgrp[:, 2 * NG, :, :], in_=ps_b[:, 0:4, :].rearrange("p t o -> p o t"))
+            nc.vector.quantize_mx(
+                out=wcodes[:, 0:8, :].rearrange("p a o -> p (a o)").bitcast(FP8X4),
+                scales=wscales[:, 0:8, :].rearrange("p a o -> p (a o)"),
+                in_=wgrp[:, 0:8, :, :].rearrange("p a o t -> p (a o t)"),
+            )
+            nc.vector.quantize_mx(
+                out=wcodes[:, 8, :].bitcast(FP8X4),
+                scales=wscales[:, 8, :],
+                in_=wgrp[:, 8, :, :].rearrange("p o t -> p (o t)"),
+            )
+
+        xpool = ctx.enter_context(tc.tile_pool(name="xraw", bufs=2))
+        xtpool = ctx.enter_context(tc.tile_pool(name="xt", bufs=2))
+        vpool = ctx.enter_context(tc.tile_pool(name="vc", bufs=2))
+        sqpool = ctx.enter_context(tc.tile_pool(name="sq", bufs=3))
+        kpool = ctx.enter_context(tc.tile_pool(name="k", bufs=8))
+        tpool = ctx.enter_context(tc.tile_pool(name="vw", bufs=4))
+        lrpool = ctx.enter_context(tc.tile_pool(name="lr", bufs=3))
+        npool = ctx.enter_context(tc.tile_pool(name="np", bufs=2))
+        gpool = ctx.enter_context(tc.tile_pool(name="grp", bufs=3))
+        cpool = ctx.enter_context(tc.tile_pool(name="codes", bufs=1))
+        opool = ctx.enter_context(tc.tile_pool(name="ost", bufs=2))
+        psx = ctx.enter_context(tc.psum_pool(name="psx", bufs=2))
+        psa = ctx.enter_context(tc.psum_pool(name="psa", bufs=2))
+
+        def scaled_relu(kind, j, src, coef):
+            t_vw = tpool.tile([P, CH], F32, tag="vw")
+            if (kind, j) in DVE_TS:
+                nc.vector.tensor_scalar(out=t_vw[:], in0=src[:], scalar1=coef, scalar2=0.0, op0=ALU.mult, op1=ALU.max)
+            else:
+                nc.scalar.activation(out=t_vw[:], in_=src[:], func=ACT.Relu, scale=coef)
+            return t_vw
+
+        for c in range(NCH):
+            xraw = xpool.tile([P, CH // P, IN], BF16)
+            nc.sync.dma_start(out=xraw[:], in_=x[c * CH:(c + 1) * CH, :].rearrange("(n p) i -> p n i", p=P))
+            xT = xtpool.tile([P, NG, CH], BF16)
+            for q in range(CH // 256):
+                ps_x = psx.tile([P, NG, 256], BF16)
+                for g in range(NG):
+                    for u in range(2):
+                        nc.tensor.transpose(
+                            ps_x[:, g, u * P:(u + 1) * P], xraw[:, 2 * q + u, g * P:(g + 1) * P], ident[:]
+                        )
+                nc.vector.tensor_copy(out=xT[:, :, q * 256:(q + 1) * 256], in_=ps_x[:])
+
+            codes = cpool.tile([P, NPASS, CH], U32, align_bytes=64)
+            scales = cpool.tile([P, NPASS, CH], U8, align_bytes=64)
+
+            for g in range(NG):
+                vc = vpool.tile([P, CH], BF16)
+                nc.vector.tensor_scalar(
+                    out=vc[:], in0=xT[:, g, :], scalar1=T[:, g, 0:1], scalar2=T[:, g, 11:12], op0=ALU.max, op1=ALU.min
+                )
+                K = []
+
+                def make_k():
+                    m = len(K)
+                    sq = sqpool.tile([P, CH], F32)
+                    nc.scalar.activation(out=sq[:], in_=vc[:], func=ACT.Square, bias=negT[:, g, m:m + 1], scale=1.0)
+                    k_new = kpool.tile([P, CH], F32, tag="K")
+                    nc.vector.scalar_tensor_tensor(
+                        out=k_new[:], in0=vc[:], scalar=T[:, g, m:m + 1], in1=sq[:], op0=ALU.subtract, op1=ALU.mult
+                    )
+                    K.append(k_new)
+
+                for j in range(NB):
+                    while len(K) < j + 5:
+                        make_k()
+                    if j % 4 == 0:
+                        planes = npool.tile([P, 4, CH], BF16)
+                    tv = scaled_relu("V", j, K[j + 1], cV[:, g, j:j + 1])
+                    left = lrpool.tile([P, CH], BF16)
+                    nc.vector.scalar_tensor_tensor(
+                        out=left[:], in0=K[j][:], scalar=a0[:, g, j:j + 1], in1=tv[:], op0=ALU.mult, op1=ALU.subtract
+                    )
+                    tw = scaled_relu("W", j, K[j + 3], cW[:, g, j:j + 1])
+                    right = lrpool.tile([P, CH], BF16)
+                    nc.vector.scalar_tensor_tensor(
+                        out=right[:], in0=K[j + 4][:], scalar=nb0[:, g, j:j + 1], in1=tw[:], op0=ALU.mult, op1=ALU.subtract
+                    )
+                    nc.vector.tensor_tensor(out=planes[:, j % 4, :], in0=left[:], in1=right[:], op=ALU.max)
+                    if j % 4 == 3:
+                        grouped = gpool.tile([P, CH, 4], BF16, align_bytes=64)
+                        nc.scalar.activation(out=grouped[:], in_=planes[:].rearrange("p t b -> p b t"), func=ACT.Relu)
+                        a = 2 * g + j // 4
+                        nc.vector.quantize_mx(
+                            out=codes[:, a, :].bitcast(FP8X4),
+                            scales=scales[:, a, :],
+                            in_=grouped[:].rearrange("p b t -> p (b t)"),
+                        )
+                if g == 0:
+                    gs = gpool.tile([P, CH, 4], BF16, align_bytes=64, tag="grouped")
+                    nc.scalar.activation(out=gs[:], in_=xT[:].rearrange("p g b -> p b g"), func=ACT.Silu)
+                    nc.vector.quantize_mx(
+                        out=codes[:, 2 * NG, :].bitcast(FP8X4),
+                        scales=scales[:, 2 * NG, :],
+                        in_=gs[:].rearrange("p b t -> p (b t)"),
+                    )
+
+            for q in range(CH // 512):
+                acc = psa.tile([P, 4, OUT], F32)
+                for u in range(4):
+                    cols = slice((4 * q + u) * P, (4 * q + u + 1) * P)
+                    for a in range(NPASS):
+                        nc.tensor.matmul_mx(
+                            out=acc[:, u, :],
+                            lhsT=codes[:, a, cols].bitcast(FP8X4),
+                            lhsT_scale=scales[:, a, cols],
+                            rhs=wcodes[:, a, :].bitcast(FP8X4),
+                            rhs_scale=wscales[:, a, :],
+                            start=(a == 0),
+                            stop=(a == NPASS - 1),
+                        )
+                ost = opool.tile([P, 4, OUT], F32)
+                nc.scalar.copy(out=ost[:], in_=acc[:])
+                r0 = c * CH + q * 512
+                nc.sync.dma_start(out=out[r0:r0 + 512, :].rearrange("(n p) o -> p n o", p=P), in_=ost[:])

@@ -119,12 +119,11 @@ def tile_bsplinekanlayer_t_kernel(tc, x, base_weight, spline_weight, spline_scal
         xpool = ctx.enter_context(tc.tile_pool(name="xraw", bufs=2))
         xtpool = ctx.enter_context(tc.tile_pool(name="xt", bufs=2))
         vpool = ctx.enter_context(tc.tile_pool(name="vc", bufs=2))
-        sqpool = ctx.enter_context(tc.tile_pool(name="sq", bufs=3))
-        kpool = ctx.enter_context(tc.tile_pool(name="k", bufs=8))
-        tpool = ctx.enter_context(tc.tile_pool(name="vw", bufs=4))
-        lrpool = ctx.enter_context(tc.tile_pool(name="lr", bufs=3))
-        npool = ctx.enter_context(tc.tile_pool(name="np", bufs=2))
-        gpool = ctx.enter_context(tc.tile_pool(name="grp", bufs=3))
+        sqpool = ctx.enter_context(tc.tile_pool(name="sq", bufs=4))
+        kpool = ctx.enter_context(tc.tile_pool(name="k", bufs=9))
+        tpool = ctx.enter_context(tc.tile_pool(name="vw", bufs=6))
+        lrpool = ctx.enter_context(tc.tile_pool(name="lr", bufs=2))
+        gpool = ctx.enter_context(tc.tile_pool(name="grp", bufs=2))
         cpool = ctx.enter_context(tc.tile_pool(name="codes", bufs=1))
         opool = ctx.enter_context(tc.tile_pool(name="ost", bufs=2))
         psx = ctx.enter_context(tc.psum_pool(name="psx", bufs=2))
@@ -175,21 +174,24 @@ def tile_bsplinekanlayer_t_kernel(tc, x, base_weight, spline_weight, spline_scal
                     while len(K) < j + 5:
                         make_k()
                     if j % 4 == 0:
-                        planes = npool.tile([P, 4, CH], BF16)
+                        left = lrpool.tile([P, 4, CH], BF16)
+                        right = lrpool.tile([P, 4, CH], BF16)
                     tv = scaled_relu("V", j, K[j + 1], cV[:, g, j:j + 1])
-                    left = lrpool.tile([P, CH], BF16)
                     nc.vector.scalar_tensor_tensor(
-                        out=left[:], in0=K[j][:], scalar=a0[:, g, j:j + 1], in1=tv[:], op0=ALU.mult, op1=ALU.subtract
+                        out=left[:, j % 4, :], in0=K[j][:], scalar=a0[:, g, j:j + 1], in1=tv[:], op0=ALU.mult, op1=ALU.subtract
                     )
                     tw = scaled_relu("W", j, K[j + 3], cW[:, g, j:j + 1])
-                    right = lrpool.tile([P, CH], BF16)
                     nc.vector.scalar_tensor_tensor(
-                        out=right[:], in0=K[j + 4][:], scalar=nb0[:, g, j:j + 1], in1=tw[:], op0=ALU.mult, op1=ALU.subtract
+                        out=right[:, j % 4, :], in0=K[j + 4][:], scalar=nb0[:, g, j:j + 1], in1=tw[:], op0=ALU.mult, op1=ALU.subtract
                     )
-                    nc.vector.tensor_tensor(out=planes[:, j % 4, :], in0=left[:], in1=right[:], op=ALU.max)
                     if j % 4 == 3:
+                        nc.vector.tensor_tensor(out=left[:], in0=left[:], in1=right[:], op=ALU.max)
                         grouped = gpool.tile([P, CH, 4], BF16, align_bytes=64)
-                        nc.scalar.activation(out=grouped[:], in_=planes[:].rearrange("p t b -> p b t"), func=ACT.Relu)
+                        nc.scalar.activation(
+                            out=grouped[:].rearrange("p (c i) t -> p c t i", i=4),
+                            in_=left[:].rearrange("p t (c i) -> p c t i", i=4),
+                            func=ACT.Relu,
+                        )
                         a = 2 * g + j // 4
                         nc.vector.quantize_mx(
                             out=codes[:, a, :].bitcast(FP8X4),
@@ -198,7 +200,11 @@ def tile_bsplinekanlayer_t_kernel(tc, x, base_weight, spline_weight, spline_scal
                         )
                 if g == 0:
                     gs = gpool.tile([P, CH, 4], BF16, align_bytes=64, tag="grouped")
-                    nc.scalar.activation(out=gs[:], in_=xT[:].rearrange("p g b -> p b g"), func=ACT.Silu)
+                    nc.scalar.activation(
+                        out=gs[:].rearrange("p (c i) t -> p c t i", i=4),
+                        in_=xT[:].rearrange("p t (c i) -> p c t i", i=4),
+                        func=ACT.Silu,
+                    )
                     nc.vector.quantize_mx(
                         out=codes[:, 2 * NG, :].bitcast(FP8X4),
                         scales=scales[:, 2 * NG, :],

@@ -21,7 +21,7 @@ NCH = B // CH
 NPASS = 2 * NG + 1
 FLOPS = 2 * B * (IN + IN * NB) * OUT
 
-DVE_TS = (("W", 1), ("W", 4), ("V", 6))
+DVE_TS = (("W", 1), ("V", 5))
 
 
 def tile_bsplinekanlayer_t_kernel(tc, x, base_weight, spline_weight, spline_scaler, grid, out):
@@ -29,11 +29,20 @@ def tile_bsplinekanlayer_t_kernel(tc, x, base_weight, spline_weight, spline_scal
     with ExitStack() as ctx:
         const = ctx.enter_context(tc.tile_pool(name="const", bufs=1))
 
-        ident = const.tile([P, P], BF16)
-        make_identity(nc, ident[:])
+        xpool = ctx.enter_context(tc.tile_pool(name="xraw", bufs=2))
+
+        def load_chunk(c):
+            xraw = xpool.tile([P, CH // P, IN], BF16)
+            nc.sync.dma_start(out=xraw[:], in_=x[c * CH:(c + 1) * CH, :].rearrange("(n p) i -> p n i", p=P))
+            return xraw
 
         g_bf = const.tile([P, NG, NK], BF16)
         nc.sync.dma_start(out=g_bf[:], in_=grid.rearrange("(g p) k -> p g k", p=P))
+        loaded = [load_chunk(0)]
+
+        ident = const.tile([P, P], BF16)
+        make_identity(nc, ident[:])
+
         T = const.tile([P, NG, NK], F32)
         nc.vector.tensor_copy(out=T[:], in_=g_bf[:])
         negT = const.tile([P, NG, NK], F32)
@@ -77,51 +86,50 @@ def tile_bsplinekanlayer_t_kernel(tc, x, base_weight, spline_weight, spline_scal
 
         wcodes = const.tile([P, NPASS, OUT], U32, align_bytes=64)
         wscales = const.tile([P, NPASS, OUT], U8, align_bytes=64)
-        with tc.tile_pool(name="wsetup", bufs=1) as wp, tc.psum_pool(name="wps", bufs=2) as wps:
-            sw = wp.tile([P, IN * NB], BF16)
-            nc.sync.dma_start(out=sw[:], in_=spline_weight.rearrange("o i j -> o (i j)"))
-            sc = wp.tile([P, IN], BF16)
+        sc = const.tile([P, IN], BF16)
+        bw = const.tile([P, IN], BF16)
+        wp = ctx.enter_context(tc.tile_pool(name="wsetup", bufs=2))
+        wps = ctx.enter_context(tc.psum_pool(name="wps", bufs=2))
+
+        def prepare_weights():
             nc.sync.dma_start(out=sc[:], in_=spline_scaler)
-            bw = wp.tile([P, IN], BF16)
             nc.sync.dma_start(out=bw[:], in_=base_weight)
-            ssw = wp.tile([P, NB, IN], BF16)
-            nc.vector.tensor_tensor(
-                out=ssw[:],
-                in0=sw[:].rearrange("o (i j) -> o j i", j=NB),
-                in1=sc[:].unsqueeze(1).to_broadcast([P, NB, IN]),
-                op=ALU.mult,
-            )
-            wgrp = wp.tile([P, NPASS, OUT, 4], BF16, align_bytes=64)
             for g in range(NG):
+                sw = wp.tile([P, P * NB], BF16)
+                nc.sync.dma_start(out=sw[:], in_=spline_weight[:, g * P:(g + 1) * P, :].rearrange("o i j -> o (i j)"))
+                ssw = wp.tile([P, NB, P], BF16)
+                nc.vector.tensor_tensor(
+                    out=ssw[:],
+                    in0=sw[:].rearrange("o (i j) -> o j i", j=NB),
+                    in1=sc[:, g * P:(g + 1) * P].unsqueeze(1).to_broadcast([P, NB, P]),
+                    op=ALU.mult,
+                )
                 ps_w = wps.tile([P, NB, P], BF16)
                 for j in range(NB):
-                    nc.tensor.transpose(ps_w[:, j, :], ssw[:, j, g * P:(g + 1) * P], ident[:])
-                for h in range(2):
-                    nc.vector.tensor_copy(
-                        out=wgrp[:, 2 * g + h, :, :],
-                        in_=ps_w[:, 4 * h:4 * h + 4, :].rearrange("p t o -> p o t"),
-                    )
+                    nc.tensor.transpose(ps_w[:, j, :], ssw[:, j, :], ident[:])
+                wgrp = wp.tile([P, 2, OUT, 4], BF16, align_bytes=64)
+                nc.vector.tensor_copy(out=wgrp[:], in_=ps_w[:].rearrange("p (h t) o -> p h o t", t=4))
+                nc.vector.quantize_mx(
+                    out=wcodes[:, 2 * g:2 * g + 2, :].rearrange("p a o -> p (a o)").bitcast(FP8X4),
+                    scales=wscales[:, 2 * g:2 * g + 2, :].rearrange("p a o -> p (a o)"),
+                    in_=wgrp[:].rearrange("p a o t -> p (a o t)"),
+                )
             ps_b = wps.tile([P, NB, P], BF16, tag="ps_w")
             for t in range(NG):
                 nc.tensor.transpose(ps_b[:, t, :], bw[:, t * P:(t + 1) * P], ident[:])
-            nc.vector.tensor_copy(out=wgrp[:, 2 * NG, :, :], in_=ps_b[:, 0:4, :].rearrange("p t o -> p o t"))
+            bgrp = wp.tile([P, 2, OUT, 4], BF16, align_bytes=64, tag="wgrp")
+            nc.vector.tensor_copy(out=bgrp[:, 0, :, :], in_=ps_b[:, 0:4, :].rearrange("p t o -> p o t"))
             nc.vector.quantize_mx(
-                out=wcodes[:, 0:8, :].rearrange("p a o -> p (a o)").bitcast(FP8X4),
-                scales=wscales[:, 0:8, :].rearrange("p a o -> p (a o)"),
-                in_=wgrp[:, 0:8, :, :].rearrange("p a o t -> p (a o t)"),
-            )
-            nc.vector.quantize_mx(
-                out=wcodes[:, 8, :].bitcast(FP8X4),
-                scales=wscales[:, 8, :],
-                in_=wgrp[:, 8, :, :].rearrange("p o t -> p (o t)"),
+                out=wcodes[:, 2 * NG, :].bitcast(FP8X4),
+                scales=wscales[:, 2 * NG, :],
+                in_=bgrp[:, 0, :, :].rearrange("p o t -> p (o t)"),
             )
 
-        xpool = ctx.enter_context(tc.tile_pool(name="xraw", bufs=2))
         xtpool = ctx.enter_context(tc.tile_pool(name="xt", bufs=2))
         vpool = ctx.enter_context(tc.tile_pool(name="vc", bufs=2))
         sqpool = ctx.enter_context(tc.tile_pool(name="sq", bufs=4))
         kpool = ctx.enter_context(tc.tile_pool(name="k", bufs=9))
-        tpool = ctx.enter_context(tc.tile_pool(name="vw", bufs=6))
+        tpool = ctx.enter_context(tc.tile_pool(name="vw", bufs=5))
         lrpool = ctx.enter_context(tc.tile_pool(name="lr", bufs=2))
         gpool = ctx.enter_context(tc.tile_pool(name="grp", bufs=2))
         cpool = ctx.enter_context(tc.tile_pool(name="codes", bufs=1))
@@ -138,8 +146,9 @@ def tile_bsplinekanlayer_t_kernel(tc, x, base_weight, spline_weight, spline_scal
             return t_vw
 
         for c in range(NCH):
-            xraw = xpool.tile([P, CH // P, IN], BF16)
-            nc.sync.dma_start(out=xraw[:], in_=x[c * CH:(c + 1) * CH, :].rearrange("(n p) i -> p n i", p=P))
+            xraw = loaded[c]
+            if c + 1 < NCH:
+                loaded.append(load_chunk(c + 1))
             xT = xtpool.tile([P, NG, CH], BF16)
             for q in range(CH // 256):
                 ps_x = psx.tile([P, NG, 256], BF16)
@@ -148,7 +157,7 @@ def tile_bsplinekanlayer_t_kernel(tc, x, base_weight, spline_weight, spline_scal
                         nc.tensor.transpose(
                             ps_x[:, g, u * P:(u + 1) * P], xraw[:, 2 * q + u, g * P:(g + 1) * P], ident[:]
                         )
-                nc.vector.tensor_copy(out=xT[:, :, q * 256:(q + 1) * 256], in_=ps_x[:])
+                nc.scalar.copy(out=xT[:, :, q * 256:(q + 1) * 256], in_=ps_x[:])
 
             codes = cpool.tile([P, NPASS, CH], U32, align_bytes=64)
             scales = cpool.tile([P, NPASS, CH], U8, align_bytes=64)
@@ -198,6 +207,8 @@ def tile_bsplinekanlayer_t_kernel(tc, x, base_weight, spline_weight, spline_scal
                             scales=scales[:, a, :],
                             in_=grouped[:].rearrange("p b t -> p (b t)"),
                         )
+                if g == 0 and c == 0:
+                    prepare_weights()
                 if g == 0:
                     gs = gpool.tile([P, CH, 4], BF16, align_bytes=64, tag="grouped")
                     nc.scalar.activation(

@@ -145,7 +145,13 @@ def tile_bsplinekanlayer_t_kernel(tc, x, base_weight, spline_weight, spline_scal
                 nc.scalar.activation(out=t_vw[:], in_=src[:], func=ACT.Relu, scale=coef)
             return t_vw
 
-        for c in range(NCH):
+        LOOKAHEAD = 6
+        groups = [(c, g) for c in range(NCH) for g in range(NG)]
+        chunk_xt = {}
+        chunk_codes = {}
+        state = {}
+
+        def prepare_chunk(c):
             xraw = loaded[c]
             if c + 1 < NCH:
                 loaded.append(load_chunk(c + 1))
@@ -158,85 +164,101 @@ def tile_bsplinekanlayer_t_kernel(tc, x, base_weight, spline_weight, spline_scal
                             ps_x[:, g, u * P:(u + 1) * P], xraw[:, 2 * q + u, g * P:(g + 1) * P], ident[:]
                         )
                 nc.scalar.copy(out=xT[:, :, q * 256:(q + 1) * 256], in_=ps_x[:])
+            chunk_xt[c] = xT
 
-            codes = cpool.tile([P, NPASS, CH], U32, align_bytes=64)
-            scales = cpool.tile([P, NPASS, CH], U8, align_bytes=64)
-
-            for g in range(NG):
+        def make_k(n):
+            c, g = groups[n]
+            if n not in state:
                 vc = vpool.tile([P, CH], BF16)
                 nc.vector.tensor_scalar(
-                    out=vc[:], in0=xT[:, g, :], scalar1=T[:, g, 0:1], scalar2=T[:, g, 11:12], op0=ALU.max, op1=ALU.min
+                    out=vc[:], in0=chunk_xt[c][:, g, :], scalar1=T[:, g, 0:1], scalar2=T[:, g, 11:12],
+                    op0=ALU.max, op1=ALU.min,
                 )
-                K = []
+                state[n] = (vc, [])
+            vc, K = state[n]
+            m = len(K)
+            sq = sqpool.tile([P, CH], F32)
+            nc.scalar.activation(out=sq[:], in_=vc[:], func=ACT.Square, bias=negT[:, g, m:m + 1], scale=1.0)
+            k_new = kpool.tile([P, CH], F32, tag="K")
+            nc.vector.scalar_tensor_tensor(
+                out=k_new[:], in0=vc[:], scalar=T[:, g, m:m + 1], in1=sq[:], op0=ALU.subtract, op1=ALU.mult
+            )
+            K.append(k_new)
 
-                def make_k():
-                    m = len(K)
-                    sq = sqpool.tile([P, CH], F32)
-                    nc.scalar.activation(out=sq[:], in_=vc[:], func=ACT.Square, bias=negT[:, g, m:m + 1], scale=1.0)
-                    k_new = kpool.tile([P, CH], F32, tag="K")
-                    nc.vector.scalar_tensor_tensor(
-                        out=k_new[:], in0=vc[:], scalar=T[:, g, m:m + 1], in1=sq[:], op0=ALU.subtract, op1=ALU.mult
-                    )
-                    K.append(k_new)
+        def cubes_made(n):
+            return len(state[n][1]) if n in state else 0
 
-                for j in range(NB):
-                    while len(K) < j + 5:
-                        make_k()
-                    if j % 4 == 0:
-                        left = lrpool.tile([P, 4, CH], BF16)
-                        right = lrpool.tile([P, 4, CH], BF16)
-                    tv = scaled_relu("V", j, K[j + 1], cV[:, g, j:j + 1])
-                    nc.vector.scalar_tensor_tensor(
-                        out=left[:, j % 4, :], in0=K[j][:], scalar=a0[:, g, j:j + 1], in1=tv[:], op0=ALU.mult, op1=ALU.subtract
-                    )
-                    tw = scaled_relu("W", j, K[j + 3], cW[:, g, j:j + 1])
-                    nc.vector.scalar_tensor_tensor(
-                        out=right[:, j % 4, :], in0=K[j + 4][:], scalar=nb0[:, g, j:j + 1], in1=tw[:], op0=ALU.mult, op1=ALU.subtract
-                    )
-                    if j % 4 == 3:
-                        nc.vector.tensor_tensor(out=left[:], in0=left[:], in1=right[:], op=ALU.max)
-                        grouped = gpool.tile([P, CH, 4], BF16, align_bytes=64)
-                        nc.scalar.activation(
-                            out=grouped[:].rearrange("p (c i) t -> p c t i", i=4),
-                            in_=left[:].rearrange("p t (c i) -> p c t i", i=4),
-                            func=ACT.Relu,
-                        )
-                        a = 2 * g + j // 4
-                        nc.vector.quantize_mx(
-                            out=codes[:, a, :].bitcast(FP8X4),
-                            scales=scales[:, a, :],
-                            in_=grouped[:].rearrange("p b t -> p (b t)"),
-                        )
-                if g == 0 and c == 0:
-                    prepare_weights()
-                if g == 0:
-                    gs = gpool.tile([P, CH, 4], BF16, align_bytes=64, tag="grouped")
+        prepare_chunk(0)
+        for n in range(len(groups)):
+            c, g = groups[n]
+            if g == 0:
+                codes = cpool.tile([P, NPASS, CH], U32, align_bytes=64)
+                scales = cpool.tile([P, NPASS, CH], U8, align_bytes=64)
+            if g == 2 and c + 1 < NCH:
+                prepare_chunk(c + 1)
+            for j in range(NB):
+                want = j + 5 + LOOKAHEAD - 4
+                while cubes_made(n) < min(NK, want):
+                    make_k(n)
+                if n + 1 < len(groups):
+                    while cubes_made(n + 1) < want - NK:
+                        make_k(n + 1)
+                K = state[n][1]
+                if j % 4 == 0:
+                    left = lrpool.tile([P, 4, CH], BF16)
+                    right = lrpool.tile([P, 4, CH], BF16)
+                tv = scaled_relu("V", j, K[j + 1], cV[:, g, j:j + 1])
+                nc.vector.scalar_tensor_tensor(
+                    out=left[:, j % 4, :], in0=K[j][:], scalar=a0[:, g, j:j + 1], in1=tv[:], op0=ALU.mult, op1=ALU.subtract
+                )
+                tw = scaled_relu("W", j, K[j + 3], cW[:, g, j:j + 1])
+                nc.vector.scalar_tensor_tensor(
+                    out=right[:, j % 4, :], in0=K[j + 4][:], scalar=nb0[:, g, j:j + 1], in1=tw[:], op0=ALU.mult, op1=ALU.subtract
+                )
+                if j % 4 == 3:
+                    nc.vector.tensor_tensor(out=left[:], in0=left[:], in1=right[:], op=ALU.max)
+                    grouped = gpool.tile([P, CH, 4], BF16, align_bytes=64)
                     nc.scalar.activation(
-                        out=gs[:].rearrange("p (c i) t -> p c t i", i=4),
-                        in_=xT[:].rearrange("p t (c i) -> p c t i", i=4),
-                        func=ACT.Silu,
+                        out=grouped[:].rearrange("p (c i) t -> p c t i", i=4),
+                        in_=left[:].rearrange("p t (c i) -> p c t i", i=4),
+                        func=ACT.Relu,
                     )
+                    a = 2 * g + j // 4
                     nc.vector.quantize_mx(
-                        out=codes[:, 2 * NG, :].bitcast(FP8X4),
-                        scales=scales[:, 2 * NG, :],
-                        in_=gs[:].rearrange("p b t -> p (b t)"),
+                        out=codes[:, a, :].bitcast(FP8X4),
+                        scales=scales[:, a, :],
+                        in_=grouped[:].rearrange("p b t -> p (b t)"),
                     )
-
-            for q in range(CH // 512):
-                acc = psa.tile([P, 4, OUT], F32)
-                for u in range(4):
-                    cols = slice((4 * q + u) * P, (4 * q + u + 1) * P)
-                    for a in range(NPASS):
-                        nc.tensor.matmul_mx(
-                            out=acc[:, u, :],
-                            lhsT=codes[:, a, cols].bitcast(FP8X4),
-                            lhsT_scale=scales[:, a, cols],
-                            rhs=wcodes[:, a, :].bitcast(FP8X4),
-                            rhs_scale=wscales[:, a, :],
-                            start=(a == 0),
-                            stop=(a == NPASS - 1),
-                        )
-                ost = opool.tile([P, 4, OUT], F32)
-                nc.scalar.copy(out=ost[:], in_=acc[:])
-                r0 = c * CH + q * 512
-                nc.sync.dma_start(out=out[r0:r0 + 512, :].rearrange("(n p) o -> p n o", p=P), in_=ost[:])
+            if g == 0 and c == 0:
+                prepare_weights()
+            if g == 0:
+                gs = gpool.tile([P, CH, 4], BF16, align_bytes=64, tag="grouped")
+                nc.scalar.activation(
+                    out=gs[:].rearrange("p (c i) t -> p c t i", i=4),
+                    in_=chunk_xt[c][:].rearrange("p t (c i) -> p c t i", i=4),
+                    func=ACT.Silu,
+                )
+                nc.vector.quantize_mx(
+                    out=codes[:, 2 * NG, :].bitcast(FP8X4),
+                    scales=scales[:, 2 * NG, :],
+                    in_=gs[:].rearrange("p b t -> p (b t)"),
+                )
+            if g == NG - 1:
+                for q in range(CH // 512):
+                    acc = psa.tile([P, 4, OUT], F32)
+                    for u in range(4):
+                        cols = slice((4 * q + u) * P, (4 * q + u + 1) * P)
+                        for a in range(NPASS):
+                            nc.tensor.matmul_mx(
+                                out=acc[:, u, :],
+                                lhsT=codes[:, a, cols].bitcast(FP8X4),
+                                lhsT_scale=scales[:, a, cols],
+                                rhs=wcodes[:, a, :].bitcast(FP8X4),
+                                rhs_scale=wscales[:, a, :],
+                                start=(a == 0),
+                                stop=(a == NPASS - 1),
+                            )
+                    ost = opool.tile([P, 4, OUT], F32)
+                    nc.scalar.copy(out=ost[:], in_=acc[:])
+                    r0 = c * CH + q * 512
+                    nc.sync.dma_start(out=out[r0:r0 + 512, :].rearrange("(n p) o -> p n o", p=P), in_=ost[:])

@@ -1,8 +1,6 @@
 from contextlib import ExitStack
 
-import concourse.bass as bass
 import concourse.mybir as mybir
-import concourse.tile as tile
 from concourse.masks import make_identity
 
 F32 = mybir.dt.float32
@@ -15,250 +13,299 @@ ACT = mybir.ActivationFunctionType
 
 P = 128
 B, IN, OUT, NB, NK = 8192, 512, 128, 8, 12
-NG = IN // P
-CH = 1024
-NCH = B // CH
-NPASS = 2 * NG + 1
+PACK = IN // P
+CHT = 8
+NCH = B // (P * CHT)
+UT = 2
+UPC = CHT // UT
+NU = NCH * UPC
+UC = UT * IN
+NPASS = NB + 1
 FLOPS = 2 * B * (IN + IN * NB) * OUT
-
-DVE_TS = (("W", 1), ("V", 5))
+IR_ON_VECTOR = (9, 10)
 
 
 def tile_bsplinekanlayer_t_kernel(tc, x, base_weight, spline_weight, spline_scaler, grid, out):
     nc = tc.nc
     with ExitStack() as ctx:
         const = ctx.enter_context(tc.tile_pool(name="const", bufs=1))
-
         xpool = ctx.enter_context(tc.tile_pool(name="xraw", bufs=2))
+        vpool = ctx.enter_context(tc.tile_pool(name="v", bufs=3))
+        sqpool = ctx.enter_context(tc.tile_pool(name="sq", bufs=4))
+        kpool = ctx.enter_context(tc.tile_pool(name="k", bufs=6))
+        ilpool = ctx.enter_context(tc.tile_pool(name="il", bufs=4))
+        irpool = ctx.enter_context(tc.tile_pool(name="ir", bufs=4))
+        lpool = ctx.enter_context(tc.tile_pool(name="lb", bufs=7))
+        gpool = ctx.enter_context(tc.tile_pool(name="grp", bufs=3))
+        gspool = ctx.enter_context(tc.tile_pool(name="gs", bufs=2))
+        cpool = ctx.enter_context(tc.tile_pool(name="codes", bufs=2))
+        opool = ctx.enter_context(tc.tile_pool(name="ost", bufs=3))
+        wp = ctx.enter_context(tc.tile_pool(name="wsetup", bufs=1))
+        pslr = ctx.enter_context(tc.psum_pool(name="pslr", bufs=6))
+        psx = ctx.enter_context(tc.psum_pool(name="psx", bufs=1))
+        psa = ctx.enter_context(tc.psum_pool(name="psa", bufs=1))
+        ctx.enter_context(tc.manual_schedule())
+
+        loaded = {}
 
         def load_chunk(c):
-            xraw = xpool.tile([P, CH // P, IN], BF16)
-            nc.sync.dma_start(out=xraw[:], in_=x[c * CH:(c + 1) * CH, :].rearrange("(n p) i -> p n i", p=P))
-            return xraw
+            xraw = xpool.tile([P, CHT, IN], BF16, name="xraw")
+            nc.sync.dma_start(
+                out=xraw[:], in_=x[c * CHT * P:(c + 1) * CHT * P, :].rearrange("(p n) i -> p n i", n=CHT)
+            )
+            loaded[c] = xraw
 
-        g_bf = const.tile([P, NG, NK], BF16)
-        nc.sync.dma_start(out=g_bf[:], in_=grid.rearrange("(g p) k -> p g k", p=P))
-        loaded = [load_chunk(0)]
+        g_bf = const.tile([P, NK], BF16)
+        nc.sync.dma_start(out=g_bf[:], in_=grid[0, :].partition_broadcast(P))
+        load_chunk(0)
+        sw = wp.tile([P, IN * NB], BF16)
+        sc = wp.tile([P, IN], BF16)
+        bw = wp.tile([P, IN], BF16)
+        nc.sync.dma_start(out=sc[:], in_=spline_scaler)
+        nc.sync.dma_start(out=sw[:], in_=spline_weight.rearrange("o i j -> o (i j)"))
+        nc.sync.dma_start(out=bw[:], in_=base_weight)
 
         ident = const.tile([P, P], BF16)
         make_identity(nc, ident[:])
+        ident_f = const.tile([P, P], F32)
+        make_identity(nc, ident_f[:])
 
-        T = const.tile([P, NG, NK], F32)
+        T = const.tile([P, NK], F32)
         nc.vector.tensor_copy(out=T[:], in_=g_bf[:])
-        negT = const.tile([P, NG, NK], F32)
+        negT = const.tile([P, NK], F32)
         nc.vector.tensor_scalar(out=negT[:], in0=T[:], scalar1=-1.0, scalar2=None, op0=ALU.mult)
-        D1 = const.tile([P, NG, 11], F32)
-        nc.vector.tensor_tensor(out=D1[:], in0=T[:, :, 1:12], in1=T[:, :, 0:11], op=ALU.subtract)
-        D2 = const.tile([P, NG, 10], F32)
-        nc.vector.tensor_tensor(out=D2[:], in0=T[:, :, 2:12], in1=T[:, :, 0:10], op=ALU.subtract)
-        D3 = const.tile([P, NG, 9], F32)
-        nc.vector.tensor_tensor(out=D3[:], in0=T[:, :, 3:12], in1=T[:, :, 0:9], op=ALU.subtract)
-        D4 = const.tile([P, NG, 8], F32)
-        nc.vector.tensor_tensor(out=D4[:], in0=T[:, :, 4:12], in1=T[:, :, 0:8], op=ALU.subtract)
+        D = {}
+        for d in (1, 2, 3, 4):
+            D[d] = const.tile([P, NK - d], F32, name="D%d" % d)
+            nc.vector.tensor_tensor(out=D[d][:], in0=T[:, d:NK], in1=T[:, 0:NK - d], op=ALU.subtract)
 
         def prod(name, factors):
-            acc = const.tile([P, NG, NB], F32, name=name)
+            acc = const.tile([P, NB], F32, name=name)
             nc.vector.tensor_tensor(out=acc[:], in0=factors[0], in1=factors[1], op=ALU.mult)
             for f in factors[2:]:
                 nc.vector.tensor_tensor(out=acc[:], in0=acc[:], in1=f, op=ALU.mult)
             return acc
 
-        a0d = prod("a0d", [D1[:, :, 0:8], D2[:, :, 0:8], D3[:, :, 0:8]])
-        a0 = const.tile([P, NG, NB], F32)
-        nc.vector.reciprocal(out=a0[:], in_=a0d[:])
-        b0d = prod("b0d", [D3[:, :, 1:9], D2[:, :, 2:10], D1[:, :, 3:11]])
-        b0 = const.tile([P, NG, NB], F32)
-        nc.vector.reciprocal(out=b0[:], in_=b0d[:])
-        nb0 = const.tile([P, NG, NB], F32)
-        nc.vector.tensor_scalar(out=nb0[:], in0=b0[:], scalar1=-1.0, scalar2=None, op0=ALU.mult)
-        a1d = prod("a1d", [D1[:, :, 0:8], D1[:, :, 1:9], D2[:, :, 1:9], D3[:, :, 1:9]])
-        a1r = const.tile([P, NG, NB], F32)
-        nc.vector.reciprocal(out=a1r[:], in_=a1d[:])
-        cV = const.tile([P, NG, NB], F32)
-        nc.vector.tensor_tensor(out=cV[:], in0=a1r[:], in1=D4[:], op=ALU.mult)
-        b1d = prod("b1d", [D3[:, :, 0:8], D2[:, :, 1:9], D1[:, :, 2:10], D1[:, :, 3:11]])
-        b1r = const.tile([P, NG, NB], F32)
-        nc.vector.reciprocal(out=b1r[:], in_=b1d[:])
-        cWp = const.tile([P, NG, NB], F32)
-        nc.vector.tensor_tensor(out=cWp[:], in0=b1r[:], in1=D4[:], op=ALU.mult)
-        cW = const.tile([P, NG, NB], F32)
-        nc.vector.tensor_scalar(out=cW[:], in0=cWp[:], scalar1=-1.0, scalar2=None, op0=ALU.mult)
+        def diff(d, j0):
+            return D[d][:, j0:j0 + NB]
+
+        def inverse(name, t):
+            r = const.tile([P, NB], F32, name=name)
+            nc.vector.reciprocal(out=r[:], in_=t[:])
+            return r
+
+        def negated(name, t):
+            r = const.tile([P, NB], F32, name=name)
+            nc.vector.tensor_scalar(out=r[:], in0=t[:], scalar1=-1.0, scalar2=None, op0=ALU.mult)
+            return r
+
+        aL = inverse("aL", prod("aLd", [diff(1, 0), diff(2, 0), diff(3, 0)]))
+        naR = negated("naR", inverse("aR", prod("aRd", [diff(3, 1), diff(2, 2), diff(1, 3)])))
+        rLi = inverse("rLi", prod("rLd", [diff(1, 1), diff(2, 1), diff(3, 1)]))
+        nrL = negated("nrL", prod("rL", [diff(4, 0), diff(2, 0), diff(3, 0), rLi[:]]))
+        rRi = inverse("rRi", prod("rRd", [diff(3, 0), diff(2, 1), diff(1, 2)]))
+        nrR = negated("nrR", prod("rR", [diff(4, 0), diff(3, 1), diff(2, 2), rRi[:]]))
 
         wcodes = const.tile([P, NPASS, OUT], U32, align_bytes=64)
         wscales = const.tile([P, NPASS, OUT], U8, align_bytes=64)
-        sc = const.tile([P, IN], BF16)
-        bw = const.tile([P, IN], BF16)
-        wp = ctx.enter_context(tc.tile_pool(name="wsetup", bufs=2))
-        wps = ctx.enter_context(tc.psum_pool(name="wps", bufs=2))
 
         def prepare_weights():
-            nc.sync.dma_start(out=sc[:], in_=spline_scaler)
-            nc.sync.dma_start(out=bw[:], in_=base_weight)
-            for g in range(NG):
-                sw = wp.tile([P, P * NB], BF16)
-                nc.sync.dma_start(out=sw[:], in_=spline_weight[:, g * P:(g + 1) * P, :].rearrange("o i j -> o (i j)"))
-                ssw = wp.tile([P, NB, P], BF16)
-                nc.vector.tensor_tensor(
-                    out=ssw[:],
-                    in0=sw[:].rearrange("o (i j) -> o j i", j=NB),
-                    in1=sc[:, g * P:(g + 1) * P].unsqueeze(1).to_broadcast([P, NB, P]),
-                    op=ALU.mult,
+            ssw = wp.tile([P, NB, IN], BF16)
+            nc.vector.tensor_tensor(
+                out=ssw[:],
+                in0=sw[:].rearrange("o (i j) -> o j i", j=NB),
+                in1=sc[:].unsqueeze(1).to_broadcast([P, NB, IN]),
+                op=ALU.mult,
+            )
+            wgrp = wp.tile([P, NPASS, OUT, PACK], BF16, align_bytes=64)
+            for h in range(NB // 2):
+                ps_w = pslr.tile([P, 2, PACK, P], BF16, name="ps_w", tag="lr")
+                for jj in range(2):
+                    for t in range(PACK):
+                        nc.tensor.transpose(ps_w[:, jj, t, :], ssw[:, 2 * h + jj, t * P:(t + 1) * P], ident[:])
+                nc.vector.tensor_copy(
+                    out=wgrp[:, 2 * h:2 * h + 2, :, :], in_=ps_w[:].rearrange("p j t o -> p j o t")
                 )
-                ps_w = wps.tile([P, NB, P], BF16)
-                for j in range(NB):
-                    nc.tensor.transpose(ps_w[:, j, :], ssw[:, j, :], ident[:])
-                wgrp = wp.tile([P, 2, OUT, 4], BF16, align_bytes=64)
-                nc.vector.tensor_copy(out=wgrp[:], in_=ps_w[:].rearrange("p (h t) o -> p h o t", t=4))
-                nc.vector.quantize_mx(
-                    out=wcodes[:, 2 * g:2 * g + 2, :].rearrange("p a o -> p (a o)").bitcast(FP8X4),
-                    scales=wscales[:, 2 * g:2 * g + 2, :].rearrange("p a o -> p (a o)"),
-                    in_=wgrp[:].rearrange("p a o t -> p (a o t)"),
-                )
-            ps_b = wps.tile([P, NB, P], BF16, tag="ps_w")
-            for t in range(NG):
+            ps_b = pslr.tile([P, PACK, P], BF16, name="ps_b", tag="lr")
+            for t in range(PACK):
                 nc.tensor.transpose(ps_b[:, t, :], bw[:, t * P:(t + 1) * P], ident[:])
-            bgrp = wp.tile([P, 2, OUT, 4], BF16, align_bytes=64, tag="wgrp")
-            nc.vector.tensor_copy(out=bgrp[:, 0, :, :], in_=ps_b[:, 0:4, :].rearrange("p t o -> p o t"))
+            nc.vector.tensor_copy(out=wgrp[:, NB, :, :], in_=ps_b[:].rearrange("p t o -> p o t"))
             nc.vector.quantize_mx(
-                out=wcodes[:, 2 * NG, :].bitcast(FP8X4),
-                scales=wscales[:, 2 * NG, :],
-                in_=bgrp[:, 0, :, :].rearrange("p o t -> p (o t)"),
+                out=wcodes[:, 0:NB, :].rearrange("p a o -> p (a o)").bitcast(FP8X4),
+                scales=wscales[:, 0:NB, :].rearrange("p a o -> p (a o)"),
+                in_=wgrp[:, 0:NB, :, :].rearrange("p a o t -> p (a o t)"),
+            )
+            nc.vector.quantize_mx(
+                out=wcodes[:, NB, :].bitcast(FP8X4),
+                scales=wscales[:, NB, :],
+                in_=wgrp[:, NB, :, :].rearrange("p o t -> p (o t)"),
             )
 
-        xtpool = ctx.enter_context(tc.tile_pool(name="xt", bufs=2))
-        vpool = ctx.enter_context(tc.tile_pool(name="vc", bufs=2))
-        sqpool = ctx.enter_context(tc.tile_pool(name="sq", bufs=4))
-        kpool = ctx.enter_context(tc.tile_pool(name="k", bufs=9))
-        tpool = ctx.enter_context(tc.tile_pool(name="vw", bufs=5))
-        lrpool = ctx.enter_context(tc.tile_pool(name="lr", bufs=2))
-        gpool = ctx.enter_context(tc.tile_pool(name="grp", bufs=2))
-        cpool = ctx.enter_context(tc.tile_pool(name="codes", bufs=1))
-        opool = ctx.enter_context(tc.tile_pool(name="ost", bufs=2))
-        psx = ctx.enter_context(tc.psum_pool(name="psx", bufs=2))
-        psa = ctx.enter_context(tc.psum_pool(name="psa", bufs=2))
+        V, SQ, K, IL, IR, LPS, RPS, LB, GRP, CODES, SCALES, ACC, GS, XPS = ({} for i in range(14))
 
-        def scaled_relu(kind, j, src, coef):
-            t_vw = tpool.tile([P, CH], F32, tag="vw")
-            if (kind, j) in DVE_TS:
-                nc.vector.tensor_scalar(out=t_vw[:], in0=src[:], scalar1=coef, scalar2=0.0, op0=ALU.mult, op1=ALU.max)
-            else:
-                nc.scalar.activation(out=t_vw[:], in_=src[:], func=ACT.Relu, scale=coef)
-            return t_vw
+        def raw(u):
+            return loaded[u // UPC][:, (u % UPC) * UT:(u % UPC + 1) * UT, :]
 
-        LOOKAHEAD = 6
-        groups = [(c, g) for c in range(NCH) for g in range(NG)]
-        chunk_xt = {}
-        chunk_codes = {}
-        state = {}
+        def clamp(u):
+            v = vpool.tile([P, UC], BF16, name="v")
+            nc.vector.tensor_scalar(
+                out=v[:], in0=raw(u).rearrange("p n i -> p (n i)"), scalar1=T[:, 0:1], scalar2=T[:, NK - 1:NK],
+                op0=ALU.max, op1=ALU.min,
+            )
+            V[u] = v
 
-        def prepare_chunk(c):
-            xraw = loaded[c]
-            if c + 1 < NCH:
-                loaded.append(load_chunk(c + 1))
-            xT = xtpool.tile([P, NG, CH], BF16)
-            for q in range(CH // 256):
-                ps_x = psx.tile([P, NG, 256], BF16)
-                for g in range(NG):
-                    for u in range(2):
-                        nc.tensor.transpose(
-                            ps_x[:, g, u * P:(u + 1) * P], xraw[:, 2 * q + u, g * P:(g + 1) * P], ident[:]
-                        )
-                nc.scalar.copy(out=xT[:, :, q * 256:(q + 1) * 256], in_=ps_x[:])
-            chunk_xt[c] = xT
+        def square(u, m):
+            sq = sqpool.tile([P, UC], F32, name="sq")
+            nc.scalar.activation(out=sq[:], in_=V[u][:], func=ACT.Square, bias=negT[:, m:m + 1], scale=1.0)
+            SQ[u, m] = sq
 
-        def make_k(n):
-            c, g = groups[n]
-            if n not in state:
-                vc = vpool.tile([P, CH], BF16)
-                nc.vector.tensor_scalar(
-                    out=vc[:], in0=chunk_xt[c][:, g, :], scalar1=T[:, g, 0:1], scalar2=T[:, g, 11:12],
-                    op0=ALU.max, op1=ALU.min,
-                )
-                state[n] = (vc, [])
-            vc, K = state[n]
-            m = len(K)
-            sq = sqpool.tile([P, CH], F32)
-            nc.scalar.activation(out=sq[:], in_=vc[:], func=ACT.Square, bias=negT[:, g, m:m + 1], scale=1.0)
-            k_new = kpool.tile([P, CH], F32, tag="K")
+        def cube(u, m):
+            k = kpool.tile([P, UC], F32, name="k")
             nc.vector.scalar_tensor_tensor(
-                out=k_new[:], in0=vc[:], scalar=T[:, g, m:m + 1], in1=sq[:], op0=ALU.subtract, op1=ALU.mult
+                out=k[:], in0=V[u][:], scalar=T[:, m:m + 1], in1=SQ[u, m][:], op0=ALU.subtract, op1=ALU.mult
             )
-            K.append(k_new)
+            K[u, m] = k
 
-        def cubes_made(n):
-            return len(state[n][1]) if n in state else 0
+        def inner_left(u, m):
+            j = m - 1
+            il = ilpool.tile([P, UC], F32, name="il")
+            nc.vector.tensor_scalar(
+                out=il[:], in0=K[u, m][:], scalar1=nrL[:, j:j + 1], scalar2=0.0, op0=ALU.mult, op1=ALU.min
+            )
+            IL[u, m] = il
 
-        prepare_chunk(0)
-        for n in range(len(groups)):
-            c, g = groups[n]
-            if g == 0:
-                codes = cpool.tile([P, NPASS, CH], U32, align_bytes=64)
-                scales = cpool.tile([P, NPASS, CH], U8, align_bytes=64)
-            if g == 2 and c + 1 < NCH:
-                prepare_chunk(c + 1)
-            for j in range(NB):
-                want = j + 5 + LOOKAHEAD - 4
-                while cubes_made(n) < min(NK, want):
-                    make_k(n)
-                if n + 1 < len(groups):
-                    while cubes_made(n + 1) < want - NK:
-                        make_k(n + 1)
-                K = state[n][1]
-                if j % 4 == 0:
-                    left = lrpool.tile([P, 4, CH], BF16)
-                    right = lrpool.tile([P, 4, CH], BF16)
-                tv = scaled_relu("V", j, K[j + 1], cV[:, g, j:j + 1])
-                nc.vector.scalar_tensor_tensor(
-                    out=left[:, j % 4, :], in0=K[j][:], scalar=a0[:, g, j:j + 1], in1=tv[:], op0=ALU.mult, op1=ALU.subtract
+        def inner_right(u, m):
+            j = m - 3
+            ir = irpool.tile([P, UC], F32, name="ir")
+            if m in IR_ON_VECTOR:
+                nc.vector.tensor_scalar(
+                    out=ir[:], in0=K[u, m][:], scalar1=nrR[:, j:j + 1], scalar2=0.0, op0=ALU.mult, op1=ALU.max
                 )
-                tw = scaled_relu("W", j, K[j + 3], cW[:, g, j:j + 1])
-                nc.vector.scalar_tensor_tensor(
-                    out=right[:, j % 4, :], in0=K[j + 4][:], scalar=nb0[:, g, j:j + 1], in1=tw[:], op0=ALU.mult, op1=ALU.subtract
-                )
-                if j % 4 == 3:
-                    nc.vector.tensor_tensor(out=left[:], in0=left[:], in1=right[:], op=ALU.max)
-                    grouped = gpool.tile([P, CH, 4], BF16, align_bytes=64)
-                    nc.scalar.activation(
-                        out=grouped[:].rearrange("p (c i) t -> p c t i", i=4),
-                        in_=left[:].rearrange("p t (c i) -> p c t i", i=4),
-                        func=ACT.Relu,
-                    )
-                    a = 2 * g + j // 4
-                    nc.vector.quantize_mx(
-                        out=codes[:, a, :].bitcast(FP8X4),
-                        scales=scales[:, a, :],
-                        in_=grouped[:].rearrange("p b t -> p (b t)"),
-                    )
-            if g == 0 and c == 0:
-                prepare_weights()
-            if g == 0:
-                gs = gpool.tile([P, CH, 4], BF16, align_bytes=64, tag="grouped")
+            else:
+                nc.scalar.activation(out=ir[:], in_=K[u, m][:], func=ACT.Relu, scale=nrR[:, j:j + 1])
+            IR[u, m] = ir
+
+        def add_transposed(first, second):
+            sums = []
+            for n in range(UT):
+                ps = pslr.tile([P, PACK, P], F32, name="ps", tag="lr")
+                for t in range(PACK):
+                    cols = slice(n * IN + t * P, n * IN + (t + 1) * P)
+                    nc.tensor.matmul(ps[:, t, :], lhsT=first[:, cols], rhs=ident_f[:], start=True, stop=False, is_transpose=True)
+                    nc.tensor.matmul(ps[:, t, :], lhsT=second[:, cols], rhs=ident_f[:], start=False, stop=True, is_transpose=True)
+                sums.append(ps)
+            return sums
+
+        def read_left(u, j):
+            lb = lpool.tile([P, UT, P, PACK], BF16, name="lb")
+            for n in range(UT):
                 nc.scalar.activation(
-                    out=gs[:].rearrange("p (c i) t -> p c t i", i=4),
-                    in_=chunk_xt[c][:].rearrange("p t (c i) -> p c t i", i=4),
-                    func=ACT.Silu,
+                    out=lb[:, n, :, :], in_=LPS[u, j][n][:].rearrange("p t b -> p b t"), func=ACT.Relu,
+                    scale=aL[:, j:j + 1],
                 )
-                nc.vector.quantize_mx(
-                    out=codes[:, 2 * NG, :].bitcast(FP8X4),
-                    scales=scales[:, 2 * NG, :],
-                    in_=gs[:].rearrange("p b t -> p (b t)"),
+            LB[u, j] = lb
+
+        def finish(u, j):
+            grp = gpool.tile([P, UT, P, PACK], BF16, name="grp", align_bytes=64)
+            for n in range(UT):
+                nc.vector.scalar_tensor_tensor(
+                    out=grp[:, n, :, :], in0=RPS[u, j][n][:].rearrange("p t b -> p b t"), scalar=naR[:, j:j + 1],
+                    in1=LB[u, j][:, n, :, :], op0=ALU.mult, op1=ALU.max,
                 )
-            if g == NG - 1:
-                for q in range(CH // 512):
-                    acc = psa.tile([P, 4, OUT], F32)
-                    for u in range(4):
-                        cols = slice((4 * q + u) * P, (4 * q + u + 1) * P)
-                        for a in range(NPASS):
-                            nc.tensor.matmul_mx(
-                                out=acc[:, u, :],
-                                lhsT=codes[:, a, cols].bitcast(FP8X4),
-                                lhsT_scale=scales[:, a, cols],
-                                rhs=wcodes[:, a, :].bitcast(FP8X4),
-                                rhs_scale=wscales[:, a, :],
-                                start=(a == 0),
-                                stop=(a == NPASS - 1),
-                            )
-                    ost = opool.tile([P, 4, OUT], F32)
-                    nc.scalar.copy(out=ost[:], in_=acc[:])
-                    r0 = c * CH + q * 512
-                    nc.sync.dma_start(out=out[r0:r0 + 512, :].rearrange("(n p) o -> p n o", p=P), in_=ost[:])
+            GRP[u, j] = grp
+
+        def quantize(u, a, src):
+            nc.vector.quantize_mx(
+                out=CODES[u][:, a, :, :].rearrange("p n b -> p (n b)").bitcast(FP8X4),
+                scales=SCALES[u][:, a, :, :].rearrange("p n b -> p (n b)"),
+                in_=src[:].rearrange("p n b t -> p (n b t)"),
+            )
+
+        def new_codes(u):
+            codes = cpool.tile([P, NPASS, UT, P], U32, name="codes", align_bytes=64)
+            scales = cpool.tile([P, NPASS, UT, P], U8, name="scales", align_bytes=64)
+            CODES[u] = codes
+            SCALES[u] = scales
+
+        def transpose_raw(u):
+            ps_x = psx.tile([P, UT, PACK, P], BF16, name="ps_x")
+            for n in range(UT):
+                for t in range(PACK):
+                    nc.tensor.transpose(ps_x[:, n, t, :], raw(u)[:, n, t * P:(t + 1) * P], ident[:])
+            XPS[u] = ps_x
+
+        def silu(u):
+            gs = gspool.tile([P, UT, P, PACK], BF16, name="gs", align_bytes=64)
+            nc.scalar.activation(out=gs[:], in_=XPS[u][:].rearrange("p n t b -> p n b t"), func=ACT.Silu)
+            GS[u] = gs
+
+        def multiply(u):
+            acc = psa.tile([P, UT, OUT], F32, name="acc")
+            for n in range(UT):
+                for a in range(NPASS):
+                    nc.tensor.matmul_mx(
+                        out=acc[:, n, :],
+                        lhsT=CODES[u][:, a, n, :].bitcast(FP8X4),
+                        lhsT_scale=SCALES[u][:, a, n, :],
+                        rhs=wcodes[:, a, :].bitcast(FP8X4),
+                        rhs_scale=wscales[:, a, :],
+                        start=(a == 0),
+                        stop=(a == NPASS - 1),
+                    )
+            ACC[u] = acc
+
+        def store(u):
+            ost = opool.tile([P, UT, OUT], F32, name="ost")
+            nc.scalar.copy(out=ost[:], in_=ACC[u][:])
+            c, q = u // UPC, u % UPC
+            rows = out[c * CHT * P:(c + 1) * CHT * P, :].rearrange("(p n) o -> p n o", n=CHT)
+            nc.sync.dma_start(out=rows[:, q * UT:(q + 1) * UT, :], in_=ost[:])
+
+        NS = NU * NK
+
+        def at(s):
+            return (s // NK, s % NK) if 0 <= s < NS else (-1, -1)
+
+        for s in range(-2, NS + NK):
+            u2, m2 = at(s + 2)
+            if m2 == 0:
+                clamp(u2)
+                new_codes(u2)
+                if u2 % UPC == 1 and u2 // UPC + 1 < NCH:
+                    load_chunk(u2 // UPC + 1)
+            if u2 >= 0:
+                square(u2, m2)
+            u1, m1 = at(s + 1)
+            if u1 >= 0:
+                cube(u1, m1)
+            u, m = at(s)
+            if 1 <= m <= NB:
+                inner_left(u, m)
+            if 3 <= m <= NB + 2:
+                inner_right(u, m)
+            if 4 <= m:
+                RPS[u, m - 4] = add_transposed(K[u, m], IR[u, m - 1])
+            if 1 <= m <= NB:
+                LPS[u, m - 1] = add_transposed(K[u, m - 1], IL[u, m])
+            if m == 1:
+                transpose_raw(u)
+            if m == 2:
+                silu(u)
+            up, mp = at(s - 1)
+            if 1 <= mp <= NB:
+                read_left(up, mp - 1)
+            if 4 <= mp:
+                finish(up, mp - 4)
+            if m == 3:
+                quantize(u, NB, GS[u])
+            uq, mq = at(s - 2)
+            if 4 <= mq:
+                quantize(uq, mq - 4, GRP[uq, mq - 4])
+            if s == 6:
+                prepare_weights()
+            um, mm = at(s - 3)
+            if mm == NK - 1:
+                multiply(um)
+            us, ms = at(s - 5)
+            if ms == NK - 1:
+                store(us)

@@ -22,7 +22,8 @@ NU = NCH * UPC
 UC = UT * IN
 NPASS = NB + 1
 FLOPS = 2 * B * (IN + IN * NB) * OUT
-IR_ON_VECTOR = (9, 10)
+NATURAL = (0, 7)
+INNER_ON_VECTOR = (10,)
 
 
 def tile_bsplinekanlayer_t_kernel(tc, x, base_weight, spline_weight, spline_scaler, grid, out):
@@ -30,15 +31,16 @@ def tile_bsplinekanlayer_t_kernel(tc, x, base_weight, spline_weight, spline_scal
     with ExitStack() as ctx:
         const = ctx.enter_context(tc.tile_pool(name="const", bufs=1))
         xpool = ctx.enter_context(tc.tile_pool(name="xraw", bufs=2))
-        vpool = ctx.enter_context(tc.tile_pool(name="v", bufs=3))
+        vpool = ctx.enter_context(tc.tile_pool(name="v", bufs=4))
         sqpool = ctx.enter_context(tc.tile_pool(name="sq", bufs=4))
-        kpool = ctx.enter_context(tc.tile_pool(name="k", bufs=6))
+        kpool = ctx.enter_context(tc.tile_pool(name="k", bufs=8))
         ilpool = ctx.enter_context(tc.tile_pool(name="il", bufs=4))
-        irpool = ctx.enter_context(tc.tile_pool(name="ir", bufs=4))
-        lpool = ctx.enter_context(tc.tile_pool(name="lb", bufs=7))
-        gpool = ctx.enter_context(tc.tile_pool(name="grp", bufs=3))
+        irpool = ctx.enter_context(tc.tile_pool(name="ir", bufs=5))
+        lpool = ctx.enter_context(tc.tile_pool(name="lb", bufs=11))
+        gpool = ctx.enter_context(tc.tile_pool(name="grp", bufs=6))
         gspool = ctx.enter_context(tc.tile_pool(name="gs", bufs=2))
-        cpool = ctx.enter_context(tc.tile_pool(name="codes", bufs=2))
+        cpool = ctx.enter_context(tc.tile_pool(name="codes", bufs=3))
+        npool = ctx.enter_context(tc.tile_pool(name="nat", bufs=2))
         opool = ctx.enter_context(tc.tile_pool(name="ost", bufs=3))
         wp = ctx.enter_context(tc.tile_pool(name="wsetup", bufs=1))
         pslr = ctx.enter_context(tc.psum_pool(name="pslr", bufs=6))
@@ -106,17 +108,30 @@ def tile_bsplinekanlayer_t_kernel(tc, x, base_weight, spline_weight, spline_scal
         rRi = inverse("rRi", prod("rRd", [diff(3, 0), diff(2, 1), diff(1, 2)]))
         nrR = negated("nrR", prod("rR", [diff(4, 0), diff(3, 1), diff(2, 2), rRi[:]]))
 
+        def times(name, p, q):
+            r = const.tile([P, NB], F32, name=name)
+            nc.vector.tensor_tensor(out=r[:], in0=p[:], in1=q[:], op=ALU.mult)
+            return r
+
+        pIL = negated("pIL", times("nIL", aL, nrL))
+        nIR = negated("nIR", times("pIR", naR, nrR))
+
         wcodes = const.tile([P, NPASS, OUT], U32, align_bytes=64)
         wscales = const.tile([P, NPASS, OUT], U8, align_bytes=64)
 
         def prepare_weights():
             ssw = wp.tile([P, NB, IN], BF16)
+            sw_j = sw[:].rearrange("o (i j) -> o j i", j=NB)
             nc.vector.tensor_tensor(
-                out=ssw[:],
-                in0=sw[:].rearrange("o (i j) -> o j i", j=NB),
-                in1=sc[:].unsqueeze(1).to_broadcast([P, NB, IN]),
-                op=ALU.mult,
+                out=ssw[:, 1:NB - 1, :], in0=sw_j[:, 1:NB - 1, :], in1=sc[:].unsqueeze(1).to_broadcast([P, NB - 2, IN]), op=ALU.mult
             )
+            for j in NATURAL:
+                nc.vector.tensor_tensor(
+                    out=ssw[:, j, :].rearrange("o (u e p) -> o u e p", u=2, e=2),
+                    in0=sw_j[:, j, :].rearrange("o (u p e) -> o u e p", u=2, e=2),
+                    in1=sc[:].rearrange("o (u p e) -> o u e p", u=2, e=2),
+                    op=ALU.mult,
+                )
             wgrp = wp.tile([P, NPASS, OUT, PACK], BF16, align_bytes=64)
             for h in range(NB // 2):
                 ps_w = pslr.tile([P, 2, PACK, P], BF16, name="ps_w", tag="lr")
@@ -141,7 +156,7 @@ def tile_bsplinekanlayer_t_kernel(tc, x, base_weight, spline_weight, spline_scal
                 in_=wgrp[:, NB, :, :].rearrange("p o t -> p (o t)"),
             )
 
-        V, SQ, K, IL, IR, LPS, RPS, LB, GRP, CODES, SCALES, ACC, GS, XPS = ({} for i in range(14))
+        V, SQ, K, IL, IR, LPS, RPS, LB, GRP, CODES, SCALES, ACC, GS, XPS, LN, RN, NPS = ({} for i in range(17))
 
         def raw(u):
             return loaded[u // UPC][:, (u % UPC) * UT:(u % UPC + 1) * UT, :]
@@ -169,20 +184,24 @@ def tile_bsplinekanlayer_t_kernel(tc, x, base_weight, spline_weight, spline_scal
         def inner_left(u, m):
             j = m - 1
             il = ilpool.tile([P, UC], F32, name="il")
+            IL[u, m] = il
+            if j in NATURAL:
+                nc.scalar.activation(out=il[:], in_=K[u, m][:], func=ACT.Relu, scale=pIL[:, j:j + 1])
+                return
             nc.vector.tensor_scalar(
                 out=il[:], in0=K[u, m][:], scalar1=nrL[:, j:j + 1], scalar2=0.0, op0=ALU.mult, op1=ALU.min
             )
-            IL[u, m] = il
 
         def inner_right(u, m):
             j = m - 3
             ir = irpool.tile([P, UC], F32, name="ir")
-            if m in IR_ON_VECTOR:
+            scale = (nIR if j in NATURAL else nrR)[:, j:j + 1]
+            if m in INNER_ON_VECTOR:
                 nc.vector.tensor_scalar(
-                    out=ir[:], in0=K[u, m][:], scalar1=nrR[:, j:j + 1], scalar2=0.0, op0=ALU.mult, op1=ALU.max
+                    out=ir[:], in0=K[u, m][:], scalar1=scale, scalar2=0.0, op0=ALU.mult, op1=ALU.max
                 )
             else:
-                nc.scalar.activation(out=ir[:], in_=K[u, m][:], func=ACT.Relu, scale=nrR[:, j:j + 1])
+                nc.scalar.activation(out=ir[:], in_=K[u, m][:], func=ACT.Relu, scale=scale)
             IR[u, m] = ir
 
         def add_transposed(first, second):
@@ -212,6 +231,43 @@ def tile_bsplinekanlayer_t_kernel(tc, x, base_weight, spline_weight, spline_scal
                     out=grp[:, n, :, :], in0=RPS[u, j][n][:].rearrange("p t b -> p b t"), scalar=naR[:, j:j + 1],
                     in1=LB[u, j][:, n, :, :], op0=ALU.mult, op1=ALU.max,
                 )
+            GRP[u, j] = grp
+
+        def natural_left(u, j):
+            ln = npool.tile([P, UC], BF16, name="ln", tag="ln%d" % j)
+            nc.vector.scalar_tensor_tensor(
+                out=ln[:], in0=K[u, j][:], scalar=aL[:, j:j + 1], in1=IL[u, j + 1][:], op0=ALU.mult, op1=ALU.subtract
+            )
+            LN[u, j] = ln
+
+        def natural_right(u, j):
+            rn = npool.tile([P, UC], BF16, name="rn")
+            nc.vector.scalar_tensor_tensor(
+                out=rn[:], in0=K[u, j + 4][:], scalar=naR[:, j:j + 1], in1=IR[u, j + 3][:], op0=ALU.mult, op1=ALU.subtract
+            )
+            RN[u, j] = rn
+
+        def natural_join(u, j):
+            nc.vector.tensor_tensor(out=RN[u, j][:], in0=LN[u, j][:], in1=RN[u, j][:], op=ALU.max)
+
+        def natural_relu(u, j):
+            nc.vector.tensor_scalar(out=RN[u, j][:], in0=RN[u, j][:], scalar1=0.0, scalar2=None, op0=ALU.max)
+
+        def natural_transpose(u, j):
+            words = RN[u, j][:].bitcast(F32)
+            ps_n = pslr.tile([P, UT, 2, P], F32, name="ps_n", tag="lr")
+            for n in range(UT):
+                for h in range(2):
+                    q = 2 * n + h
+                    nc.tensor.transpose(ps_n[:, n, h, :], words[:, q * P:(q + 1) * P], ident_f[:])
+            NPS[u, j] = ps_n
+
+        def natural_copy(u, j):
+            grp = gpool.tile([P, UT, P, PACK], BF16, name="grp", align_bytes=64)
+            nc.scalar.copy(
+                out=grp[:].rearrange("p n b t -> p (n b t)").bitcast(F32).rearrange("p (n b h) -> p n b h", n=UT, h=2),
+                in_=NPS[u, j][:].rearrange("p n h b -> p n b h"),
+            )
             GRP[u, j] = grp
 
         def quantize(u, a, src):
@@ -261,51 +317,82 @@ def tile_bsplinekanlayer_t_kernel(tc, x, base_weight, spline_weight, spline_scal
             rows = out[c * CHT * P:(c + 1) * CHT * P, :].rearrange("(p n) o -> p n o", n=CHT)
             nc.sync.dma_start(out=rows[:, q * UT:(q + 1) * UT, :], in_=ost[:])
 
-        NS = NU * NK
+        HALF = NK // 2
 
-        def at(s):
-            return (s // NK, s % NK) if 0 <= s < NS else (-1, -1)
+        def stream(parity, tau):
+            i = tau // NK
+            return (2 * i + parity, tau % NK) if 0 <= i < NU // 2 else (-1, -1)
 
-        for s in range(-2, NS + NK):
-            u2, m2 = at(s + 2)
-            if m2 == 0:
-                clamp(u2)
-                new_codes(u2)
-                if u2 % UPC == 1 and u2 // UPC + 1 < NCH:
-                    load_chunk(u2 // UPC + 1)
-            if u2 >= 0:
-                square(u2, m2)
-            u1, m1 = at(s + 1)
-            if u1 >= 0:
-                cube(u1, m1)
-            u, m = at(s)
-            if 1 <= m <= NB:
-                inner_left(u, m)
-            if 3 <= m <= NB + 2:
-                inner_right(u, m)
-            if 4 <= m:
-                RPS[u, m - 4] = add_transposed(K[u, m], IR[u, m - 1])
-            if 1 <= m <= NB:
-                LPS[u, m - 1] = add_transposed(K[u, m - 1], IL[u, m])
-            if m == 1:
-                transpose_raw(u)
-            if m == 2:
-                silu(u)
-            up, mp = at(s - 1)
-            if 1 <= mp <= NB:
-                read_left(up, mp - 1)
-            if 4 <= mp:
-                finish(up, mp - 4)
-            if m == 3:
-                quantize(u, NB, GS[u])
-            uq, mq = at(s - 2)
-            if 4 <= mq:
-                quantize(uq, mq - 4, GRP[uq, mq - 4])
-            if s == 6:
+        for tau in range(-2, NU // 2 * NK + HALF + NK):
+            def both(lag):
+                return [stream(0, tau - lag), stream(1, tau - HALF - lag)]
+
+            ahead, now, before, two_ago, three_ago, four_ago = (both(lag) for lag in range(-1, 5))
+            for u, m in both(-2):
+                if m == 0:
+                    clamp(u)
+                    new_codes(u)
+                    if u % UPC == 1 and u // UPC + 1 < NCH:
+                        load_chunk(u // UPC + 1)
+            for u, m in ahead:
+                if m >= 0:
+                    square(u, m)
+            for u, m in now:
+                if 1 <= m <= NB:
+                    inner_left(u, m)
+            for u, m in now:
+                if 3 <= m <= NB + 2:
+                    inner_right(u, m)
+            for u, m in before:
+                if 1 <= m <= NB and m - 1 not in NATURAL:
+                    read_left(u, m - 1)
+                if m == 6:
+                    silu(u)
+            for u, m in before:
+                if m >= 4 and m - 4 not in NATURAL:
+                    finish(u, m - 4)
+            for u, m in now:
+                if m >= 4 and m - 4 in NATURAL:
+                    natural_right(u, m - 4)
+            for u, m in before:
+                if m >= 1 and m - 1 in NATURAL:
+                    natural_left(u, m - 1)
+            for u, m in four_ago:
+                if m >= 4 and m - 4 in NATURAL:
+                    quantize(u, m - 4, GRP[u, m - 4])
+            for u, m in before:
+                if m >= 4 and m - 4 in NATURAL:
+                    natural_join(u, m - 4)
+            for u, m in two_ago:
+                if m >= 4 and m - 4 not in NATURAL:
+                    quantize(u, m - 4, GRP[u, m - 4])
+                if m == 6:
+                    quantize(u, NB, GS[u])
+            for u, m in before:
+                if m >= 4 and m - 4 in NATURAL:
+                    natural_relu(u, m - 4)
+            for u, m in three_ago:
+                if m >= 4 and m - 4 in NATURAL:
+                    natural_copy(u, m - 4)
+            for u, m in ahead:
+                if m >= 0:
+                    cube(u, m)
+            for u, m in now:
+                if m >= 4 and m - 4 not in NATURAL:
+                    RPS[u, m - 4] = add_transposed(K[u, m], IR[u, m - 1])
+            for u, m in two_ago:
+                if m >= 4 and m - 4 in NATURAL:
+                    natural_transpose(u, m - 4)
+            for u, m in now:
+                if 1 <= m <= NB and m - 1 not in NATURAL:
+                    LPS[u, m - 1] = add_transposed(K[u, m - 1], IL[u, m])
+                if m == 6:
+                    transpose_raw(u)
+            if tau == 5:
                 prepare_weights()
-            um, mm = at(s - 3)
-            if mm == NK - 1:
-                multiply(um)
-            us, ms = at(s - 5)
-            if ms == NK - 1:
-                store(us)
+            for u, m in both(5):
+                if m == NK - 1:
+                    multiply(u)
+            for u, m in both(6):
+                if m == NK - 1:
+                    store(u)

@@ -22,27 +22,51 @@ NU = NCH * UPC
 UC = UT * IN
 NPASS = NB + 1
 FLOPS = 2 * B * (IN + IN * NB) * OUT
+NQ = NK // 2
 NATURAL = (0, 7)
-INNER_ON_VECTOR = (10,)
+INNER_ON_SCALAR = (0, 1, 4, 5)
+LEFT, RIGHT = "left", "right"
+
+
+def half(side, j):
+    if side == LEFT:
+        outer, inner, up = j, j + 1, 1
+    else:
+        outer, inner, up = j + 4, j + 3, -1
+    return outer % NQ, up if outer >= NQ else -up, inner % NQ, up if inner >= NQ else -up
+
+
+def wraps(side, j):
+    o, so, i, si = half(side, j)
+    return abs(o - i) == NQ - 1
+
+
+def sum_step(side, j):
+    o, so, i, si = half(side, j)
+    return NQ if wraps(side, j) else max(o, i)
+
+
+def inner_step(side, j):
+    return NQ - 1 if wraps(side, j) else half(side, j)[2]
+
+
+HALVES = [(side, j) for j in range(NB) for side in (LEFT, RIGHT)]
+
+
+def other(side):
+    return RIGHT if side == LEFT else LEFT
 
 
 def tile_bsplinekanlayer_t_kernel(tc, x, base_weight, spline_weight, spline_scaler, grid, out):
     nc = tc.nc
     with ExitStack() as ctx:
-        const = ctx.enter_context(tc.tile_pool(name="const", bufs=1))
-        xpool = ctx.enter_context(tc.tile_pool(name="xraw", bufs=2))
-        vpool = ctx.enter_context(tc.tile_pool(name="v", bufs=4))
-        sqpool = ctx.enter_context(tc.tile_pool(name="sq", bufs=4))
-        kpool = ctx.enter_context(tc.tile_pool(name="k", bufs=8))
-        ilpool = ctx.enter_context(tc.tile_pool(name="il", bufs=4))
-        irpool = ctx.enter_context(tc.tile_pool(name="ir", bufs=5))
-        lpool = ctx.enter_context(tc.tile_pool(name="lb", bufs=11))
-        gpool = ctx.enter_context(tc.tile_pool(name="grp", bufs=6))
-        gspool = ctx.enter_context(tc.tile_pool(name="gs", bufs=2))
-        cpool = ctx.enter_context(tc.tile_pool(name="codes", bufs=3))
-        npool = ctx.enter_context(tc.tile_pool(name="nat", bufs=2))
-        opool = ctx.enter_context(tc.tile_pool(name="ost", bufs=3))
-        wp = ctx.enter_context(tc.tile_pool(name="wsetup", bufs=1))
+        def pool(name, bufs):
+            return ctx.enter_context(tc.tile_pool(name=name, bufs=bufs))
+
+        const, xpool, vpool, apool, sqpool = pool("const", 1), pool("xraw", 2), pool("v", 2), pool("a", 3), pool("sq", 3)
+        kpool, w0pool, ipool, fpool = pool("w", 6), pool("w0", 2), pool("inner", 9), pool("first", 9)
+        npool, gpool, gspool, cpool = pool("nat", 2), pool("grp", 5), pool("gs", 2), pool("codes", 2)
+        opool, wp = pool("ost", 3), pool("wsetup", 1)
         pslr = ctx.enter_context(tc.psum_pool(name="pslr", bufs=6))
         psx = ctx.enter_context(tc.psum_pool(name="psx", bufs=1))
         psa = ctx.enter_context(tc.psum_pool(name="psa", bufs=1))
@@ -52,111 +76,121 @@ def tile_bsplinekanlayer_t_kernel(tc, x, base_weight, spline_weight, spline_scal
 
         def load_chunk(c):
             xraw = xpool.tile([P, CHT, IN], BF16, name="xraw")
-            nc.sync.dma_start(
-                out=xraw[:], in_=x[c * CHT * P:(c + 1) * CHT * P, :].rearrange("(p n) i -> p n i", n=CHT)
-            )
+            rows = x[c * CHT * P:(c + 1) * CHT * P, :].rearrange("(p n) i -> p n i", n=CHT)
+            pieces = UPC if c == 0 else 1
+            w = CHT // pieces
+            for q in range(pieces):
+                nc.sync.dma_start(out=xraw[:, q * w:(q + 1) * w, :], in_=rows[:, q * w:(q + 1) * w, :])
             loaded[c] = xraw
 
-        g_bf = const.tile([P, NK], BF16)
+        g_bf = const.tile([P, NK], BF16, name="g_bf")
         nc.sync.dma_start(out=g_bf[:], in_=grid[0, :].partition_broadcast(P))
         load_chunk(0)
-        sw = wp.tile([P, IN * NB], BF16)
-        sc = wp.tile([P, IN], BF16)
-        bw = wp.tile([P, IN], BF16)
+        sw = wp.tile([P, IN * NB], BF16, name="sw")
+        sc = wp.tile([P, IN], BF16, name="sc")
+        bw = wp.tile([P, IN], BF16, name="bw")
         nc.sync.dma_start(out=sc[:], in_=spline_scaler)
         nc.sync.dma_start(out=sw[:], in_=spline_weight.rearrange("o i j -> o (i j)"))
         nc.sync.dma_start(out=bw[:], in_=base_weight)
 
-        ident = const.tile([P, P], BF16)
+        ident = const.tile([P, P], BF16, name="ident")
         make_identity(nc, ident[:])
-        ident_f = const.tile([P, P], F32)
+        ident_f = const.tile([P, P], F32, name="ident_f")
         make_identity(nc, ident_f[:])
 
-        T = const.tile([P, NK], F32)
+        T = const.tile([P, NK], F32, name="T")
         nc.vector.tensor_copy(out=T[:], in_=g_bf[:])
-        negT = const.tile([P, NK], F32)
-        nc.vector.tensor_scalar(out=negT[:], in0=T[:], scalar1=-1.0, scalar2=None, op0=ALU.mult)
-        D = {}
-        for d in (1, 2, 3, 4):
-            D[d] = const.tile([P, NK - d], F32, name="D%d" % d)
-            nc.vector.tensor_tensor(out=D[d][:], in0=T[:, d:NK], in1=T[:, 0:NK - d], op=ALU.subtract)
+        S2 = const.tile([P, NQ], F32, name="S2")
+        nc.vector.tensor_tensor(out=S2[:], in0=T[:, 0:NQ], in1=T[:, NQ:NK], op=ALU.add)
+        negC = const.tile([P, NQ], F32, name="negC")
+        nc.vector.tensor_scalar(out=negC[:], in0=S2[:], scalar1=-0.5, scalar2=None, op0=ALU.mult)
+        D2x = const.tile([P, NQ], F32, name="D2x")
+        nc.vector.tensor_tensor(out=D2x[:], in0=T[:, NQ:NK], in1=T[:, 0:NQ], op=ALU.subtract)
+        H = const.tile([P, NQ], F32, name="H")
+        nc.vector.tensor_scalar(out=H[:], in0=D2x[:], scalar1=0.5, scalar2=None, op0=ALU.mult)
+        negH = const.tile([P, NQ], F32, name="negH")
+        nc.vector.tensor_scalar(out=negH[:], in0=D2x[:], scalar1=-0.5, scalar2=None, op0=ALU.mult)
 
-        def prod(name, factors):
-            acc = const.tile([P, NB], F32, name=name)
-            nc.vector.tensor_tensor(out=acc[:], in0=factors[0], in1=factors[1], op=ALU.mult)
-            for f in factors[2:]:
-                nc.vector.tensor_tensor(out=acc[:], in0=acc[:], in1=f, op=ALU.mult)
-            return acc
+        COEF = {}
 
-        def diff(d, j0):
-            return D[d][:, j0:j0 + NB]
+        def coefficients():
+            D = {}
+            for d in (1, 2, 3, 4):
+                D[d] = const.tile([P, NK - d], F32, name="D%d" % d)
+                nc.vector.tensor_tensor(out=D[d][:], in0=T[:, d:NK], in1=T[:, 0:NK - d], op=ALU.subtract)
 
-        def inverse(name, t):
-            r = const.tile([P, NB], F32, name=name)
-            nc.vector.reciprocal(out=r[:], in_=t[:])
-            return r
+            def diff(d, j0):
+                return D[d][:, j0:j0 + NB]
 
-        def negated(name, t):
-            r = const.tile([P, NB], F32, name=name)
-            nc.vector.tensor_scalar(out=r[:], in0=t[:], scalar1=-1.0, scalar2=None, op0=ALU.mult)
-            return r
+            def prod(name, factors):
+                acc = const.tile([P, NB], F32, name=name)
+                nc.vector.tensor_tensor(out=acc[:], in0=factors[0], in1=factors[1], op=ALU.mult)
+                for f in factors[2:]:
+                    nc.vector.tensor_tensor(out=acc[:], in0=acc[:], in1=f, op=ALU.mult)
+                return acc
 
-        aL = inverse("aL", prod("aLd", [diff(1, 0), diff(2, 0), diff(3, 0)]))
-        naR = negated("naR", inverse("aR", prod("aRd", [diff(3, 1), diff(2, 2), diff(1, 3)])))
-        rLi = inverse("rLi", prod("rLd", [diff(1, 1), diff(2, 1), diff(3, 1)]))
-        nrL = negated("nrL", prod("rL", [diff(4, 0), diff(2, 0), diff(3, 0), rLi[:]]))
-        rRi = inverse("rRi", prod("rRd", [diff(3, 0), diff(2, 1), diff(1, 2)]))
-        nrR = negated("nrR", prod("rR", [diff(4, 0), diff(3, 1), diff(2, 2), rRi[:]]))
+            def inverse(name, t):
+                r = const.tile([P, NB], F32, name=name)
+                nc.vector.reciprocal(out=r[:], in_=t[:])
+                return r
 
-        def times(name, p, q):
-            r = const.tile([P, NB], F32, name=name)
-            nc.vector.tensor_tensor(out=r[:], in0=p[:], in1=q[:], op=ALU.mult)
-            return r
+            def both_signs(key, name, t):
+                neg = const.tile([P, NB], F32, name=name + "_neg")
+                nc.vector.tensor_scalar(out=neg[:], in0=t[:], scalar1=-1.0, scalar2=None, op0=ALU.mult)
+                COEF[key, 1], COEF[key, -1] = t, neg
 
-        pIL = negated("pIL", times("nIL", aL, nrL))
-        nIR = negated("nIR", times("pIR", naR, nrR))
+            for side, den, rnum, rden in (
+                (LEFT, ((1, 0), (2, 0), (3, 0)), ((4, 0), (2, 0), (3, 0)), ((1, 1), (2, 1), (3, 1))),
+                (RIGHT, ((3, 1), (2, 2), (1, 3)), ((4, 0), (3, 1), (2, 2)), ((3, 0), (2, 1), (1, 2))),
+            ):
+                outer = inverse("outer_" + side, prod("den_" + side, [diff(d, j0) for d, j0 in den]))
+                rinv = inverse("rinv_" + side, prod("rden_" + side, [diff(d, j0) for d, j0 in rden]))
+                ratio = prod("ratio_" + side, [diff(d, j0) for d, j0 in rnum] + [rinv[:]])
+                both_signs((side, "outer"), "outerc_" + side, outer)
+                both_signs((side, "ratio"), "ratioc_" + side, ratio)
+                both_signs((side, "inner"), "innerc_" + side, prod("inner_" + side, [outer[:], ratio[:]]))
 
-        wcodes = const.tile([P, NPASS, OUT], U32, align_bytes=64)
-        wscales = const.tile([P, NPASS, OUT], U8, align_bytes=64)
+        def coef(side, kind, sign, j):
+            return COEF[(side, kind), sign][:, j:j + 1]
 
-        def prepare_weights():
-            ssw = wp.tile([P, NB, IN], BF16)
+        wcodes = const.tile([P, NPASS, OUT], U32, name="wcodes", align_bytes=64)
+        wscales = const.tile([P, NPASS, OUT], U8, name="wscales", align_bytes=64)
+        ssw = wp.tile([P, NPASS, IN], BF16, name="ssw")
+        wgrp = wp.tile([P, NPASS, OUT, PACK], BF16, name="wgrp", align_bytes=64)
+
+        def by_pairs(row):
+            return row.rearrange("o (h p e) -> o h e p", h=2, e=2)
+
+        def scale_weights(js):
             sw_j = sw[:].rearrange("o (i j) -> o j i", j=NB)
-            nc.vector.tensor_tensor(
-                out=ssw[:, 1:NB - 1, :], in0=sw_j[:, 1:NB - 1, :], in1=sc[:].unsqueeze(1).to_broadcast([P, NB - 2, IN]), op=ALU.mult
-            )
-            for j in NATURAL:
-                nc.vector.tensor_tensor(
-                    out=ssw[:, j, :].rearrange("o (u e p) -> o u e p", u=2, e=2),
-                    in0=sw_j[:, j, :].rearrange("o (u p e) -> o u e p", u=2, e=2),
-                    in1=sc[:].rearrange("o (u p e) -> o u e p", u=2, e=2),
-                    op=ALU.mult,
-                )
-            wgrp = wp.tile([P, NPASS, OUT, PACK], BF16, align_bytes=64)
-            for h in range(NB // 2):
-                ps_w = pslr.tile([P, 2, PACK, P], BF16, name="ps_w", tag="lr")
-                for jj in range(2):
-                    for t in range(PACK):
-                        nc.tensor.transpose(ps_w[:, jj, t, :], ssw[:, 2 * h + jj, t * P:(t + 1) * P], ident[:])
-                nc.vector.tensor_copy(
-                    out=wgrp[:, 2 * h:2 * h + 2, :, :], in_=ps_w[:].rearrange("p j t o -> p j o t")
-                )
-            ps_b = pslr.tile([P, PACK, P], BF16, name="ps_b", tag="lr")
-            for t in range(PACK):
-                nc.tensor.transpose(ps_b[:, t, :], bw[:, t * P:(t + 1) * P], ident[:])
-            nc.vector.tensor_copy(out=wgrp[:, NB, :, :], in_=ps_b[:].rearrange("p t o -> p o t"))
-            nc.vector.quantize_mx(
-                out=wcodes[:, 0:NB, :].rearrange("p a o -> p (a o)").bitcast(FP8X4),
-                scales=wscales[:, 0:NB, :].rearrange("p a o -> p (a o)"),
-                in_=wgrp[:, 0:NB, :, :].rearrange("p a o t -> p (a o t)"),
-            )
-            nc.vector.quantize_mx(
-                out=wcodes[:, NB, :].bitcast(FP8X4),
-                scales=wscales[:, NB, :],
-                in_=wgrp[:, NB, :, :].rearrange("p o t -> p (o t)"),
-            )
+            for j in js:
+                if j in NATURAL:
+                    nc.vector.tensor_tensor(
+                        out=ssw[:, j, :].rearrange("o (h e p) -> o h e p", h=2, e=2), in0=by_pairs(sw_j[:, j, :]),
+                        in1=by_pairs(sc[:]), op=ALU.mult,
+                    )
+                else:
+                    nc.vector.tensor_tensor(out=ssw[:, j, :], in0=sw_j[:, j, :], in1=sc[:], op=ALU.mult)
 
-        V, SQ, K, IL, IR, LPS, RPS, LB, GRP, CODES, SCALES, ACC, GS, XPS, LN, RN, NPS = ({} for i in range(17))
+        def order_base_weights():
+            nc.vector.tensor_copy(out=ssw[:, NB, :].rearrange("o (h e p) -> o h e p", h=2, e=2), in_=by_pairs(bw[:]))
+
+        def turn_weights(a0, a1):
+            ps_w = pslr.tile([P, 2, PACK, P], BF16, name="ps_w", tag="lr")
+            for a in range(a0, a1):
+                for t in range(PACK):
+                    nc.tensor.transpose(ps_w[:, a - a0, t, :], ssw[:, a, t * P:(t + 1) * P], ident[:])
+            nc.scalar.copy(out=wgrp[:, a0:a1, :, :], in_=ps_w[:, 0:a1 - a0, :, :].rearrange("p j t o -> p j o t"))
+
+        def quantize_weights():
+            for a0, a1 in ((0, NB), (NB, NPASS)):
+                nc.vector.quantize_mx(
+                    out=wcodes[:, a0:a1, :].rearrange("p a o -> p (a o)").bitcast(FP8X4),
+                    scales=wscales[:, a0:a1, :].rearrange("p a o -> p (a o)"),
+                    in_=wgrp[:, a0:a1, :, :].rearrange("p a o t -> p (a o t)"),
+                )
+
+        V, A, SQ, W, INNER, PS, FIRST, GRP, CODES, SCALES, ACC, GS, XPS, NAT, NPS = ({} for i in range(15))
 
         def raw(u):
             return loaded[u // UPC][:, (u % UPC) * UT:(u % UPC + 1) * UT, :]
@@ -169,92 +203,94 @@ def tile_bsplinekanlayer_t_kernel(tc, x, base_weight, spline_weight, spline_scal
             )
             V[u] = v
 
-        def square(u, m):
+        def distance(u, q):
+            a = apool.tile([P, UC], F32, name="a")
+            nc.scalar.activation(out=a[:], in_=V[u][:], func=ACT.Abs, bias=negC[:, q:q + 1], scale=1.0)
+            A[u, q] = a
+
+        def square(u, q):
             sq = sqpool.tile([P, UC], F32, name="sq")
-            nc.scalar.activation(out=sq[:], in_=V[u][:], func=ACT.Square, bias=negT[:, m:m + 1], scale=1.0)
-            SQ[u, m] = sq
+            nc.scalar.activation(out=sq[:], in_=A[u, q][:], func=ACT.Square, bias=negH[:, q:q + 1], scale=1.0)
+            SQ[u, q] = sq
 
-        def cube(u, m):
-            k = kpool.tile([P, UC], F32, name="k")
+        def cube(u, q):
+            w = (w0pool if q == 0 else kpool).tile([P, UC], F32, name="w")
             nc.vector.scalar_tensor_tensor(
-                out=k[:], in0=V[u][:], scalar=T[:, m:m + 1], in1=SQ[u, m][:], op0=ALU.subtract, op1=ALU.mult
+                out=w[:], in0=A[u, q][:], scalar=H[:, q:q + 1], in1=SQ[u, q][:], op0=ALU.subtract, op1=ALU.mult
             )
-            K[u, m] = k
+            W[u, q] = w
 
-        def inner_left(u, m):
-            j = m - 1
-            il = ilpool.tile([P, UC], F32, name="il")
-            IL[u, m] = il
+        def inner(u, side, j, scalar):
+            o, so, i, si = half(side, j)
+            t = ipool.tile([P, UC], F32, name="t")
+            INNER[u, side, j] = t
             if j in NATURAL:
-                nc.scalar.activation(out=il[:], in_=K[u, m][:], func=ACT.Relu, scale=pIL[:, j:j + 1])
-                return
-            nc.vector.tensor_scalar(
-                out=il[:], in0=K[u, m][:], scalar1=nrL[:, j:j + 1], scalar2=0.0, op0=ALU.mult, op1=ALU.min
-            )
-
-        def inner_right(u, m):
-            j = m - 3
-            ir = irpool.tile([P, UC], F32, name="ir")
-            scale = (nIR if j in NATURAL else nrR)[:, j:j + 1]
-            if m in INNER_ON_VECTOR:
-                nc.vector.tensor_scalar(
-                    out=ir[:], in0=K[u, m][:], scalar1=scale, scalar2=0.0, op0=ALU.mult, op1=ALU.max
-                )
+                scale, positive = coef(side, "inner", si, j), True
             else:
-                nc.scalar.activation(out=ir[:], in_=K[u, m][:], func=ACT.Relu, scale=scale)
-            IR[u, m] = ir
+                scale, positive = coef(side, "ratio", -so * si, j), so < 0
+            if scalar:
+                nc.scalar.activation(out=t[:], in_=W[u, i][:], func=ACT.Relu, scale=scale)
+            else:
+                nc.vector.tensor_scalar(
+                    out=t[:], in0=W[u, i][:], scalar1=scale, scalar2=0.0, op0=ALU.mult,
+                    op1=ALU.max if positive else ALU.min,
+                )
 
-        def add_transposed(first, second):
+        def on_scalar(side, j):
+            can = j in NATURAL or half(side, j)[1] < 0
+            return can and inner_step(side, j) < sum_step(side, j) and inner_step(side, j) in INNER_ON_SCALAR
+
+        def add_transposed(u, side, j):
+            outer = W[u, half(side, j)[0]]
+            second = INNER[u, side, j]
             sums = []
             for n in range(UT):
                 ps = pslr.tile([P, PACK, P], F32, name="ps", tag="lr")
                 for t in range(PACK):
                     cols = slice(n * IN + t * P, n * IN + (t + 1) * P)
-                    nc.tensor.matmul(ps[:, t, :], lhsT=first[:, cols], rhs=ident_f[:], start=True, stop=False, is_transpose=True)
+                    nc.tensor.matmul(ps[:, t, :], lhsT=outer[:, cols], rhs=ident_f[:], start=True, stop=False, is_transpose=True)
                     nc.tensor.matmul(ps[:, t, :], lhsT=second[:, cols], rhs=ident_f[:], start=False, stop=True, is_transpose=True)
                 sums.append(ps)
-            return sums
+            PS[u, side, j] = sums
 
-        def read_left(u, j):
-            lb = lpool.tile([P, UT, P, PACK], BF16, name="lb")
+        def read_first(u, side, j):
+            f = fpool.tile([P, UT, P, PACK], BF16, name="f")
             for n in range(UT):
                 nc.scalar.activation(
-                    out=lb[:, n, :, :], in_=LPS[u, j][n][:].rearrange("p t b -> p b t"), func=ACT.Relu,
-                    scale=aL[:, j:j + 1],
+                    out=f[:, n, :, :], in_=PS[u, side, j][n][:].rearrange("p t b -> p b t"), func=ACT.Relu,
+                    scale=coef(side, "outer", half(side, j)[1], j),
                 )
-            LB[u, j] = lb
+            FIRST[u, j] = f
 
-        def finish(u, j):
+        def finish(u, side, j):
             grp = gpool.tile([P, UT, P, PACK], BF16, name="grp", align_bytes=64)
             for n in range(UT):
                 nc.vector.scalar_tensor_tensor(
-                    out=grp[:, n, :, :], in0=RPS[u, j][n][:].rearrange("p t b -> p b t"), scalar=naR[:, j:j + 1],
-                    in1=LB[u, j][:, n, :, :], op0=ALU.mult, op1=ALU.max,
+                    out=grp[:, n, :, :], in0=PS[u, side, j][n][:].rearrange("p t b -> p b t"),
+                    scalar=coef(side, "outer", half(side, j)[1], j), in1=FIRST[u, j][:, n, :, :],
+                    op0=ALU.mult, op1=ALU.max,
                 )
             GRP[u, j] = grp
 
-        def natural_left(u, j):
-            ln = npool.tile([P, UC], BF16, name="ln", tag="ln%d" % j)
+        def natural_half(u, side, j):
+            o, so, i, si = half(side, j)
+            y = npool.tile([P, UC], BF16, name="y", tag="y%d%s" % (j, side))
             nc.vector.scalar_tensor_tensor(
-                out=ln[:], in0=K[u, j][:], scalar=aL[:, j:j + 1], in1=IL[u, j + 1][:], op0=ALU.mult, op1=ALU.subtract
+                out=y[:], in0=W[u, o][:], scalar=coef(side, "outer", so, j), in1=INNER[u, side, j][:],
+                op0=ALU.mult, op1=ALU.subtract,
             )
-            LN[u, j] = ln
-
-        def natural_right(u, j):
-            rn = npool.tile([P, UC], BF16, name="rn")
-            nc.vector.scalar_tensor_tensor(
-                out=rn[:], in0=K[u, j + 4][:], scalar=naR[:, j:j + 1], in1=IR[u, j + 3][:], op0=ALU.mult, op1=ALU.subtract
-            )
-            RN[u, j] = rn
+            NAT[u, side, j] = y
 
         def natural_join(u, j):
-            nc.vector.tensor_tensor(out=RN[u, j][:], in0=LN[u, j][:], in1=RN[u, j][:], op=ALU.max)
+            y = NAT[u, RIGHT, j]
+            nc.vector.tensor_tensor(out=y[:], in0=NAT[u, LEFT, j][:], in1=y[:], op=ALU.max)
 
         def natural_relu(u, j):
-            nc.vector.tensor_scalar(out=RN[u, j][:], in0=RN[u, j][:], scalar1=0.0, scalar2=None, op0=ALU.max)
+            y = NAT[u, RIGHT, j]
+            nc.vector.tensor_scalar(out=y[:], in0=y[:], scalar1=0.0, scalar2=None, op0=ALU.max)
 
         def natural_transpose(u, j):
-            words = RN[u, j][:].bitcast(F32)
+            words = NAT[u, RIGHT, j][:].bitcast(F32)
             ps_n = pslr.tile([P, UT, 2, P], F32, name="ps_n", tag="lr")
             for n in range(UT):
                 for h in range(2):
@@ -271,28 +307,34 @@ def tile_bsplinekanlayer_t_kernel(tc, x, base_weight, spline_weight, spline_scal
             GRP[u, j] = grp
 
         def quantize(u, a, src):
+            if u not in CODES:
+                codes = cpool.tile([P, NPASS, UT, P], U32, name="codes", align_bytes=64)
+                scales = cpool.tile([P, NPASS, UT, P], U8, name="scales", align_bytes=64)
+                CODES[u] = codes
+                SCALES[u] = scales
             nc.vector.quantize_mx(
                 out=CODES[u][:, a, :, :].rearrange("p n b -> p (n b)").bitcast(FP8X4),
                 scales=SCALES[u][:, a, :, :].rearrange("p n b -> p (n b)"),
                 in_=src[:].rearrange("p n b t -> p (n b t)"),
             )
 
-        def new_codes(u):
-            codes = cpool.tile([P, NPASS, UT, P], U32, name="codes", align_bytes=64)
-            scales = cpool.tile([P, NPASS, UT, P], U8, name="scales", align_bytes=64)
-            CODES[u] = codes
-            SCALES[u] = scales
-
         def transpose_raw(u):
-            ps_x = psx.tile([P, UT, PACK, P], BF16, name="ps_x")
+            ps_x = psx.tile([P, UT, 2, P], F32, name="ps_x")
             for n in range(UT):
-                for t in range(PACK):
-                    nc.tensor.transpose(ps_x[:, n, t, :], raw(u)[:, n, t * P:(t + 1) * P], ident[:])
+                words = raw(u)[:, n, :].bitcast(F32)
+                for h in range(2):
+                    nc.tensor.transpose(ps_x[:, n, h, :], words[:, h * P:(h + 1) * P], ident_f[:])
             XPS[u] = ps_x
 
         def silu(u):
             gs = gspool.tile([P, UT, P, PACK], BF16, name="gs", align_bytes=64)
-            nc.scalar.activation(out=gs[:], in_=XPS[u][:].rearrange("p n t b -> p n b t"), func=ACT.Silu)
+            values = XPS[u][:].rearrange("p n h b -> p (n h b)").bitcast(BF16).rearrange(
+                "p (n h b e) -> p n b h e", n=UT, h=2, e=2
+            )
+            for n in range(UT):
+                nc.scalar.activation(
+                    out=gs[:, n, :, :].rearrange("p b (h e) -> p b h e", e=2), in_=values[:, n, :, :, :], func=ACT.Silu
+                )
             GS[u] = gs
 
         def multiply(u):
@@ -317,82 +359,90 @@ def tile_bsplinekanlayer_t_kernel(tc, x, base_weight, spline_weight, spline_scal
             rows = out[c * CHT * P:(c + 1) * CHT * P, :].rearrange("(p n) o -> p n o", n=CHT)
             nc.sync.dma_start(out=rows[:, q * UT:(q + 1) * UT, :], in_=ost[:])
 
-        HALF = NK // 2
+        NS = NU * NQ
 
-        def stream(parity, tau):
-            i = tau // NK
-            return (2 * i + parity, tau % NK) if 0 <= i < NU // 2 else (-1, -1)
+        def at(s):
+            return (s // NQ, s % NQ) if 0 <= s < NS else None
 
-        for tau in range(-2, NU // 2 * NK + HALF + NK):
-            def both(lag):
-                return [stream(0, tau - lag), stream(1, tau - HALF - lag)]
+        def due(step_of, s, lag, halves):
+            found = []
+            for side, j in halves:
+                start = s - lag - step_of(side, j)
+                if start % NQ == 0 and 0 <= start < NS:
+                    found.append((start // NQ, side, j))
+            return found
 
-            ahead, now, before, two_ago, three_ago, four_ago = (both(lag) for lag in range(-1, 5))
-            for u, m in both(-2):
-                if m == 0:
-                    clamp(u)
-                    new_codes(u)
-                    if u % UPC == 1 and u // UPC + 1 < NCH:
-                        load_chunk(u // UPC + 1)
-            for u, m in ahead:
-                if m >= 0:
-                    square(u, m)
-            for u, m in now:
-                if 1 <= m <= NB:
-                    inner_left(u, m)
-            for u, m in now:
-                if 3 <= m <= NB + 2:
-                    inner_right(u, m)
-            for u, m in before:
-                if 1 <= m <= NB and m - 1 not in NATURAL:
-                    read_left(u, m - 1)
-                if m == 6:
-                    silu(u)
-            for u, m in before:
-                if m >= 4 and m - 4 not in NATURAL:
-                    finish(u, m - 4)
-            for u, m in now:
-                if m >= 4 and m - 4 in NATURAL:
-                    natural_right(u, m - 4)
-            for u, m in before:
-                if m >= 1 and m - 1 in NATURAL:
-                    natural_left(u, m - 1)
-            for u, m in four_ago:
-                if m >= 4 and m - 4 in NATURAL:
-                    quantize(u, m - 4, GRP[u, m - 4])
-            for u, m in before:
-                if m >= 4 and m - 4 in NATURAL:
-                    natural_join(u, m - 4)
-            for u, m in two_ago:
-                if m >= 4 and m - 4 not in NATURAL:
-                    quantize(u, m - 4, GRP[u, m - 4])
-                if m == 6:
-                    quantize(u, NB, GS[u])
-            for u, m in before:
-                if m >= 4 and m - 4 in NATURAL:
-                    natural_relu(u, m - 4)
-            for u, m in three_ago:
-                if m >= 4 and m - 4 in NATURAL:
-                    natural_copy(u, m - 4)
-            for u, m in ahead:
-                if m >= 0:
-                    cube(u, m)
-            for u, m in now:
-                if m >= 4 and m - 4 not in NATURAL:
-                    RPS[u, m - 4] = add_transposed(K[u, m], IR[u, m - 1])
-            for u, m in two_ago:
-                if m >= 4 and m - 4 in NATURAL:
-                    natural_transpose(u, m - 4)
-            for u, m in now:
-                if 1 <= m <= NB and m - 1 not in NATURAL:
-                    LPS[u, m - 1] = add_transposed(K[u, m - 1], IL[u, m])
-                if m == 6:
-                    transpose_raw(u)
-            if tau == 5:
-                prepare_weights()
-            for u, m in both(5):
-                if m == NK - 1:
-                    multiply(u)
-            for u, m in both(6):
-                if m == NK - 1:
-                    store(u)
+        SUMS = [(side, j) for side, j in HALVES if j not in NATURAL]
+        FIRSTS = [(side, j) for side, j in SUMS if sum_step(side, j) < sum_step(other(side), j)]
+        SECONDS = [(side, j) for side, j in SUMS if (side, j) not in FIRSTS]
+        NATS = [(side, j) for side, j in HALVES if j in NATURAL]
+        NLAST = [(RIGHT, j) for j in NATURAL]
+
+        for s in range(-3, NS + 2 * NQ):
+            nxt = at(s + 3)
+            if nxt and nxt[1] == 0:
+                clamp(nxt[0])
+                if nxt[0] % UPC == 1 and nxt[0] // UPC + 1 < NCH:
+                    load_chunk(nxt[0] // UPC + 1)
+            if at(s + 1):
+                square(*at(s + 1))
+            for u, side, j in due(inner_step, s, 0, HALVES):
+                if not on_scalar(side, j):
+                    inner(u, side, j, False)
+            for u, side, j in due(sum_step, s, 1, FIRSTS):
+                read_first(u, side, j)
+            for u, side, j in due(inner_step, s, 0, HALVES):
+                if on_scalar(side, j):
+                    inner(u, side, j, True)
+            for u, side, j in due(sum_step, s, 1, SECONDS):
+                finish(u, side, j)
+            for u, side, j in due(sum_step, s, 0, NATS):
+                if side == RIGHT:
+                    natural_half(u, side, j)
+            for u, side, j in due(sum_step, s, 1, NATS):
+                if side == LEFT:
+                    natural_half(u, side, j)
+            if at(s + 1):
+                cube(*at(s + 1))
+            for u, side, j in due(sum_step, s, 1, NLAST):
+                natural_join(u, j)
+            for u, side, j in due(sum_step, s, 2, SECONDS):
+                quantize(u, j, GRP[u, j])
+            for u, side, j in due(sum_step, s, 4, NLAST):
+                quantize(u, j, GRP[u, j])
+            for u, side, j in due(sum_step, s, 1, NLAST):
+                natural_relu(u, j)
+            if at(s + 2):
+                distance(*at(s + 2))
+            for u, side, j in due(sum_step, s, 3, NLAST):
+                natural_copy(u, j)
+            for u, side, j in due(sum_step, s, 0, SUMS):
+                if inner_step(side, j) < sum_step(side, j):
+                    add_transposed(u, side, j)
+            for u, side, j in due(sum_step, s, 2, NLAST):
+                natural_transpose(u, j)
+            for u, side, j in due(sum_step, s, 0, SUMS):
+                if inner_step(side, j) == sum_step(side, j):
+                    add_transposed(u, side, j)
+            if at(s) and at(s)[1] == 0:
+                transpose_raw(at(s)[0])
+            if at(s - 1) and at(s - 1)[1] == 0:
+                silu(at(s - 1)[0])
+            if at(s - 8) and at(s - 8)[1] == 0:
+                quantize(at(s - 8)[0], NB, GS[at(s - 8)[0]])
+            if s == -2:
+                coefficients()
+            if 1 <= s <= 4:
+                scale_weights((2 * s - 2, 2 * s - 1))
+            if s == 5:
+                order_base_weights()
+            if 2 <= s <= 5:
+                turn_weights(2 * s - 4, 2 * s - 2)
+            if s == 6:
+                turn_weights(NB, NPASS)
+            if s == 8:
+                quantize_weights()
+            if at(s - 10) and at(s - 10)[1] == 0:
+                multiply(at(s - 10)[0])
+            if at(s - 11) and at(s - 11)[1] == 0:
+                store(at(s - 11)[0])

@@ -22,9 +22,15 @@ NU = NCH * UPC
 UC = UT * IN
 NPASS = NB + 1
 FLOPS = 2 * B * (IN + IN * NB) * OUT
-NQ = NK // 2
-NATURAL = (0, 7)
-INNER_ON_SCALAR = (0, 1, 4, 5)
+NQ = 5
+TRIPLE = NK - 2 * NQ
+NATURAL = (6, 7)
+EXTRA = 3
+EVERY = 4
+SHARED = (0, 1, 2)
+SHIFT = 3
+LAG = 10
+INNER_ON_SCALAR = (1, 4)
 LEFT, RIGHT = "left", "right"
 
 
@@ -33,7 +39,7 @@ def half(side, j):
         outer, inner, up = j, j + 1, 1
     else:
         outer, inner, up = j + 4, j + 3, -1
-    return outer % NQ, up if outer >= NQ else -up, inner % NQ, up if inner >= NQ else -up
+    return outer % NQ, up if outer // NQ % 2 else -up, inner % NQ, up if inner // NQ % 2 else -up
 
 
 def wraps(side, j):
@@ -50,7 +56,23 @@ def inner_step(side, j):
     return NQ - 1 if wraps(side, j) else half(side, j)[2]
 
 
+def natural_step(side, j):
+    return sum_step(side, j) + (1 if inner_step(side, j) == sum_step(side, j) else 0)
+
+
+def join_step(side, j):
+    return 1 + max(natural_step(LEFT, j), natural_step(RIGHT, j))
+
+
 HALVES = [(side, j) for j in range(NB) for side in (LEFT, RIGHT)]
+
+
+def natural(u, j):
+    return j in NATURAL or (j == EXTRA and u % EVERY == EVERY - 1)
+
+
+def shared(u, j):
+    return j in SHARED and not natural(u, j) and not natural(u, j + SHIFT)
 
 
 def other(side):
@@ -63,13 +85,11 @@ def tile_bsplinekanlayer_t_kernel(tc, x, base_weight, spline_weight, spline_scal
         def pool(name, bufs):
             return ctx.enter_context(tc.tile_pool(name=name, bufs=bufs))
 
-        const, xpool, vpool, apool, sqpool = pool("const", 1), pool("xraw", 2), pool("v", 2), pool("a", 3), pool("sq", 3)
-        kpool, w0pool, ipool, fpool = pool("w", 6), pool("w0", 2), pool("inner", 9), pool("first", 9)
+        const, xpool, vpool, apool, sqpool = pool("const", 1), pool("xraw", 2), pool("v", 2), pool("a", 4), pool("sq", 3)
+        kpool, w0pool, ipool, fpool = pool("w", 6), pool("w0", 2), pool("inner", 9), pool("first", 8)
         npool, gpool, gspool, cpool = pool("nat", 2), pool("grp", 5), pool("gs", 2), pool("codes", 2)
         opool, wp = pool("ost", 3), pool("wsetup", 1)
-        pslr = ctx.enter_context(tc.psum_pool(name="pslr", bufs=6))
-        psx = ctx.enter_context(tc.psum_pool(name="psx", bufs=1))
-        psa = ctx.enter_context(tc.psum_pool(name="psa", bufs=1))
+        pslr = ctx.enter_context(tc.psum_pool(name="pslr", bufs=8))
         ctx.enter_context(tc.manual_schedule())
 
         loaded = {}
@@ -100,16 +120,25 @@ def tile_bsplinekanlayer_t_kernel(tc, x, base_weight, spline_weight, spline_scal
 
         T = const.tile([P, NK], F32, name="T")
         nc.vector.tensor_copy(out=T[:], in_=g_bf[:])
-        S2 = const.tile([P, NQ], F32, name="S2")
-        nc.vector.tensor_tensor(out=S2[:], in0=T[:, 0:NQ], in1=T[:, NQ:NK], op=ALU.add)
-        negC = const.tile([P, NQ], F32, name="negC")
-        nc.vector.tensor_scalar(out=negC[:], in0=S2[:], scalar1=-0.5, scalar2=None, op0=ALU.mult)
-        D2x = const.tile([P, NQ], F32, name="D2x")
-        nc.vector.tensor_tensor(out=D2x[:], in0=T[:, NQ:NK], in1=T[:, 0:NQ], op=ALU.subtract)
-        H = const.tile([P, NQ], F32, name="H")
-        nc.vector.tensor_scalar(out=H[:], in0=D2x[:], scalar1=0.5, scalar2=None, op0=ALU.mult)
-        negH = const.tile([P, NQ], F32, name="negH")
-        nc.vector.tensor_scalar(out=negH[:], in0=D2x[:], scalar1=-0.5, scalar2=None, op0=ALU.mult)
+        def small(name, in0, in1, op, scale=None):
+            r = const.tile([P, in0.shape[1]], F32, name=name)
+            nc.vector.tensor_tensor(out=r[:], in0=in0, in1=in1, op=op)
+            if scale is not None:
+                nc.vector.tensor_scalar(out=r[:], in0=r[:], scalar1=scale, scalar2=None, op0=ALU.mult)
+            return r
+
+        C = small("C", T[:, 0:NQ], T[:, NQ:2 * NQ], ALU.add, 0.5)
+        H = small("H", T[:, NQ:2 * NQ], T[:, 0:NQ], ALU.subtract, 0.5)
+        far = small("far", T[:, 2 * NQ:NK], H[:, 0:TRIPLE], ALU.add)
+        E = small("E", far[:], C[:, 0:TRIPLE], ALU.subtract, 0.5)
+        nc.vector.tensor_tensor(out=C[:, 0:TRIPLE], in0=C[:, 0:TRIPLE], in1=E[:], op=ALU.add)
+
+        def negative(name, t):
+            r = const.tile([P, t.shape[1]], F32, name=name)
+            nc.vector.tensor_scalar(out=r[:], in0=t[:], scalar1=-1.0, scalar2=None, op0=ALU.mult)
+            return r
+
+        negC, negE, negH = negative("negC", C), negative("negE", E), negative("negH", H)
 
         COEF = {}
 
@@ -139,6 +168,7 @@ def tile_bsplinekanlayer_t_kernel(tc, x, base_weight, spline_weight, spline_scal
                 nc.vector.tensor_scalar(out=neg[:], in0=t[:], scalar1=-1.0, scalar2=None, op0=ALU.mult)
                 COEF[key, 1], COEF[key, -1] = t, neg
 
+            found = {}
             for side, den, rnum, rden in (
                 (LEFT, ((1, 0), (2, 0), (3, 0)), ((4, 0), (2, 0), (3, 0)), ((1, 1), (2, 1), (3, 1))),
                 (RIGHT, ((3, 1), (2, 2), (1, 3)), ((4, 0), (3, 1), (2, 2)), ((3, 0), (2, 1), (1, 2))),
@@ -146,6 +176,39 @@ def tile_bsplinekanlayer_t_kernel(tc, x, base_weight, spline_weight, spline_scal
                 outer = inverse("outer_" + side, prod("den_" + side, [diff(d, j0) for d, j0 in den]))
                 rinv = inverse("rinv_" + side, prod("rden_" + side, [diff(d, j0) for d, j0 in rden]))
                 ratio = prod("ratio_" + side, [diff(d, j0) for d, j0 in rnum] + [rinv[:]])
+                found[side] = outer, ratio
+            G = const.tile([P, NQ], F32, name="G")
+            nc.vector.memset(G[:], 1.0)
+            n = len(SHARED)
+            rinv = inverse("rinv", found[RIGHT][1])
+            q0 = SHARED[0] + 2
+            nc.vector.tensor_tensor(
+                out=G[:, q0:q0 + n], in0=found[LEFT][1][:, SHARED[0]:SHARED[0] + n],
+                in1=rinv[:, SHARED[0] + SHIFT:SHARED[0] + SHIFT + n], op=ALU.mult,
+            )
+            for k in range(q0 + 2, q0 + n):
+                nc.vector.tensor_tensor(out=G[:, k:k + 1], in0=G[:, k:k + 1], in1=G[:, k - 2:k - 1], op=ALU.mult)
+            y = const.tile([P, NQ], F32, name="root")
+            nc.vector.tensor_scalar(out=y[:], in0=G[:], scalar1=0.5, scalar2=0.5, op0=ALU.mult, op1=ALU.add)
+            for k in range(4):
+                yi = const.tile([P, NQ], F32, name="yi%d" % k)
+                nc.vector.reciprocal(out=yi[:], in_=y[:])
+                nc.vector.tensor_tensor(out=yi[:], in0=yi[:], in1=G[:], op=ALU.mult)
+                nc.vector.tensor_tensor(out=y[:], in0=y[:], in1=yi[:], op=ALU.add)
+                nc.vector.tensor_scalar(out=y[:], in0=y[:], scalar1=0.5, scalar2=None, op0=ALU.mult)
+            nrH = const.tile([P, NQ], F32, name="nrH")
+            nc.vector.tensor_tensor(out=nrH[:], in0=y[:], in1=negH[:], op=ALU.mult)
+            COEF["root"], COEF["nrH"] = y, nrH
+            knotG = const.tile([P, NK], F32, name="knotG")
+            for k in range(0, NK, NQ):
+                w = min(NQ, NK - k)
+                nc.vector.tensor_copy(out=knotG[:, k:k + w], in_=G[:, 0:w])
+            invG = const.tile([P, NK], F32, name="invG")
+            nc.vector.reciprocal(out=invG[:], in_=knotG[:])
+            for side, o0, i0 in ((LEFT, 0, 1), (RIGHT, 4, 3)):
+                outer, ratio = found[side]
+                outer = prod("outer2_" + side, [outer[:], invG[:, o0:o0 + NB]])
+                ratio = prod("ratio2_" + side, [ratio[:], knotG[:, o0:o0 + NB], invG[:, i0:i0 + NB]])
                 both_signs((side, "outer"), "outerc_" + side, outer)
                 both_signs((side, "ratio"), "ratioc_" + side, ratio)
                 both_signs((side, "inner"), "innerc_" + side, prod("inner_" + side, [outer[:], ratio[:]]))
@@ -153,10 +216,10 @@ def tile_bsplinekanlayer_t_kernel(tc, x, base_weight, spline_weight, spline_scal
         def coef(side, kind, sign, j):
             return COEF[(side, kind), sign][:, j:j + 1]
 
-        wcodes = const.tile([P, NPASS, OUT], U32, name="wcodes", align_bytes=64)
-        wscales = const.tile([P, NPASS, OUT], U8, name="wscales", align_bytes=64)
-        ssw = wp.tile([P, NPASS, IN], BF16, name="ssw")
-        wgrp = wp.tile([P, NPASS, OUT, PACK], BF16, name="wgrp", align_bytes=64)
+        wcodes = const.tile([P, NPASS + 1, OUT], U32, name="wcodes", align_bytes=64)
+        wscales = const.tile([P, NPASS + 1, OUT], U8, name="wscales", align_bytes=64)
+        ssw = wp.tile([P, NPASS + 1, IN], BF16, name="ssw")
+        wgrp = wp.tile([P, NPASS + 1, OUT, PACK], BF16, name="wgrp", align_bytes=64)
 
         def by_pairs(row):
             return row.rearrange("o (h p e) -> o h e p", h=2, e=2)
@@ -172,7 +235,11 @@ def tile_bsplinekanlayer_t_kernel(tc, x, base_weight, spline_weight, spline_scal
                 else:
                     nc.vector.tensor_tensor(out=ssw[:, j, :], in0=sw_j[:, j, :], in1=sc[:], op=ALU.mult)
 
-        def order_base_weights():
+        def order_other_weights():
+            nc.vector.tensor_tensor(
+                out=ssw[:, NPASS, :].rearrange("o (h e p) -> o h e p", h=2, e=2),
+                in0=by_pairs(sw[:].rearrange("o (i j) -> o j i", j=NB)[:, EXTRA, :]), in1=by_pairs(sc[:]), op=ALU.mult,
+            )
             nc.vector.tensor_copy(out=ssw[:, NB, :].rearrange("o (h e p) -> o h e p", h=2, e=2), in_=by_pairs(bw[:]))
 
         def turn_weights(a0, a1):
@@ -183,7 +250,7 @@ def tile_bsplinekanlayer_t_kernel(tc, x, base_weight, spline_weight, spline_scal
             nc.scalar.copy(out=wgrp[:, a0:a1, :, :], in_=ps_w[:, 0:a1 - a0, :, :].rearrange("p j t o -> p j o t"))
 
         def quantize_weights():
-            for a0, a1 in ((0, NB), (NB, NPASS)):
+            for a0, a1 in ((0, NB), (NB, NPASS + 1)):
                 nc.vector.quantize_mx(
                     out=wcodes[:, a0:a1, :].rearrange("p a o -> p (a o)").bitcast(FP8X4),
                     scales=wscales[:, a0:a1, :].rearrange("p a o -> p (a o)"),
@@ -196,21 +263,28 @@ def tile_bsplinekanlayer_t_kernel(tc, x, base_weight, spline_weight, spline_scal
             return loaded[u // UPC][:, (u % UPC) * UT:(u % UPC + 1) * UT, :]
 
         def clamp(u):
-            v = vpool.tile([P, UC], BF16, name="v")
-            nc.vector.tensor_scalar(
-                out=v[:], in0=raw(u).rearrange("p n i -> p (n i)"), scalar1=T[:, 0:1], scalar2=T[:, NK - 1:NK],
-                op0=ALU.max, op1=ALU.min,
-            )
-            V[u] = v
+            for k in range(TRIPLE):
+                v = vpool.tile([P, UC], BF16, name="v", tag="v%d" % k)
+                nc.vector.tensor_scalar(
+                    out=v[:], in0=raw(u).rearrange("p n i -> p (n i)"), scalar1=T[:, k:k + 1],
+                    scalar2=T[:, 2 * NQ + k:2 * NQ + k + 1], op0=ALU.max, op1=ALU.min,
+                )
+                V[u, k] = v
 
         def distance(u, q):
             a = apool.tile([P, UC], F32, name="a")
-            nc.scalar.activation(out=a[:], in_=V[u][:], func=ACT.Abs, bias=negC[:, q:q + 1], scale=1.0)
+            v = V[u, 1 if q == 1 else 0]
+            nc.scalar.activation(out=a[:], in_=v[:], func=ACT.Abs, bias=negC[:, q:q + 1], scale=1.0)
+            A[u, q] = a
+
+        def fold(u, q):
+            a = apool.tile([P, UC], F32, name="a")
+            nc.scalar.activation(out=a[:], in_=A[u, q][:], func=ACT.Abs, bias=negE[:, q:q + 1], scale=1.0)
             A[u, q] = a
 
         def square(u, q):
             sq = sqpool.tile([P, UC], F32, name="sq")
-            nc.scalar.activation(out=sq[:], in_=A[u, q][:], func=ACT.Square, bias=negH[:, q:q + 1], scale=1.0)
+            nc.scalar.activation(out=sq[:], in_=A[u, q][:], func=ACT.Square, bias=COEF["nrH"][:, q:q + 1], scale=COEF["root"][:, q:q + 1])
             SQ[u, q] = sq
 
         def cube(u, q):
@@ -224,7 +298,9 @@ def tile_bsplinekanlayer_t_kernel(tc, x, base_weight, spline_weight, spline_scal
             o, so, i, si = half(side, j)
             t = ipool.tile([P, UC], F32, name="t")
             INNER[u, side, j] = t
-            if j in NATURAL:
+            if side == LEFT and shared(u, j):
+                INNER[u, RIGHT, j + SHIFT] = t
+            if natural(u, j):
                 scale, positive = coef(side, "inner", si, j), True
             else:
                 scale, positive = coef(side, "ratio", -so * si, j), so < 0
@@ -236,8 +312,8 @@ def tile_bsplinekanlayer_t_kernel(tc, x, base_weight, spline_weight, spline_scal
                     op1=ALU.max if positive else ALU.min,
                 )
 
-        def on_scalar(side, j):
-            can = j in NATURAL or half(side, j)[1] < 0
+        def on_scalar(u, side, j):
+            can = natural(u, j) or half(side, j)[1] < 0
             return can and inner_step(side, j) < sum_step(side, j) and inner_step(side, j) in INNER_ON_SCALAR
 
         def add_transposed(u, side, j):
@@ -319,7 +395,7 @@ def tile_bsplinekanlayer_t_kernel(tc, x, base_weight, spline_weight, spline_scal
             )
 
         def transpose_raw(u):
-            ps_x = psx.tile([P, UT, 2, P], F32, name="ps_x")
+            ps_x = pslr.tile([P, UT, 2, P], F32, name="ps_x", tag="lr")
             for n in range(UT):
                 words = raw(u)[:, n, :].bitcast(F32)
                 for h in range(2):
@@ -338,15 +414,16 @@ def tile_bsplinekanlayer_t_kernel(tc, x, base_weight, spline_weight, spline_scal
             GS[u] = gs
 
         def multiply(u):
-            acc = psa.tile([P, UT, OUT], F32, name="acc")
+            w = [NPASS if a == EXTRA and natural(u, a) else a for a in range(NPASS)]
+            acc = pslr.tile([P, UT, OUT], F32, name="acc", tag="lr")
             for n in range(UT):
                 for a in range(NPASS):
                     nc.tensor.matmul_mx(
                         out=acc[:, n, :],
                         lhsT=CODES[u][:, a, n, :].bitcast(FP8X4),
                         lhsT_scale=SCALES[u][:, a, n, :],
-                        rhs=wcodes[:, a, :].bitcast(FP8X4),
-                        rhs_scale=wscales[:, a, :],
+                        rhs=wcodes[:, w[a], :].bitcast(FP8X4),
+                        rhs_scale=wscales[:, w[a], :],
                         start=(a == 0),
                         stop=(a == NPASS - 1),
                     )
@@ -372,77 +449,82 @@ def tile_bsplinekanlayer_t_kernel(tc, x, base_weight, spline_weight, spline_scal
                     found.append((start // NQ, side, j))
             return found
 
-        SUMS = [(side, j) for side, j in HALVES if j not in NATURAL]
-        FIRSTS = [(side, j) for side, j in SUMS if sum_step(side, j) < sum_step(other(side), j)]
-        SECONDS = [(side, j) for side, j in SUMS if (side, j) not in FIRSTS]
-        NATS = [(side, j) for side, j in HALVES if j in NATURAL]
-        NLAST = [(RIGHT, j) for j in NATURAL]
+        FIRSTS = [(side, j) for side, j in HALVES if sum_step(side, j) < sum_step(other(side), j)]
+        SECONDS = [(side, j) for side, j in HALVES if (side, j) not in FIRSTS]
+        JOINS = [(LEFT, j) for j in range(NB)]
+
+        def summed(step_of, s, lag, halves):
+            return [h for h in due(step_of, s, lag, halves) if not natural(h[0], h[2])]
+
+        def joined(step_of, s, lag, halves):
+            return [h for h in due(step_of, s, lag, halves) if natural(h[0], h[2])]
+
+        def ranked(s):
+            return at(s) and at(s)[1] == 0
 
         for s in range(-3, NS + 2 * NQ):
-            nxt = at(s + 3)
-            if nxt and nxt[1] == 0:
-                clamp(nxt[0])
-                if nxt[0] % UPC == 1 and nxt[0] // UPC + 1 < NCH:
-                    load_chunk(nxt[0] // UPC + 1)
+            if ranked(s + 3):
+                u = at(s + 3)[0]
+                clamp(u)
+                if u % UPC == 1 and u // UPC + 1 < NCH:
+                    load_chunk(u // UPC + 1)
+            if s == -1:
+                coefficients()
             if at(s + 1):
                 square(*at(s + 1))
             for u, side, j in due(inner_step, s, 0, HALVES):
-                if not on_scalar(side, j):
+                if not on_scalar(u, side, j) and not (side == RIGHT and shared(u, j - SHIFT)):
                     inner(u, side, j, False)
-            for u, side, j in due(sum_step, s, 1, FIRSTS):
-                read_first(u, side, j)
-            for u, side, j in due(inner_step, s, 0, HALVES):
-                if on_scalar(side, j):
-                    inner(u, side, j, True)
-            for u, side, j in due(sum_step, s, 1, SECONDS):
-                finish(u, side, j)
-            for u, side, j in due(sum_step, s, 0, NATS):
-                if side == RIGHT:
-                    natural_half(u, side, j)
-            for u, side, j in due(sum_step, s, 1, NATS):
-                if side == LEFT:
-                    natural_half(u, side, j)
-            if at(s + 1):
-                cube(*at(s + 1))
-            for u, side, j in due(sum_step, s, 1, NLAST):
-                natural_join(u, j)
-            for u, side, j in due(sum_step, s, 2, SECONDS):
-                quantize(u, j, GRP[u, j])
-            for u, side, j in due(sum_step, s, 4, NLAST):
-                quantize(u, j, GRP[u, j])
-            for u, side, j in due(sum_step, s, 1, NLAST):
-                natural_relu(u, j)
             if at(s + 2):
                 distance(*at(s + 2))
-            for u, side, j in due(sum_step, s, 3, NLAST):
+            for u, side, j in summed(sum_step, s, 1, FIRSTS):
+                read_first(u, side, j)
+            for u, side, j in due(inner_step, s, 0, HALVES):
+                if on_scalar(u, side, j) and not (side == RIGHT and shared(u, j - SHIFT)):
+                    inner(u, side, j, True)
+            for u, side, j in summed(sum_step, s, 1, SECONDS):
+                finish(u, side, j)
+            for u, side, j in joined(natural_step, s, 0, HALVES):
+                natural_half(u, side, j)
+            if at(s + 1):
+                cube(*at(s + 1))
+            for u, side, j in joined(join_step, s, 0, JOINS):
+                natural_join(u, j)
+            for u, side, j in summed(sum_step, s, 2, SECONDS):
+                quantize(u, j, GRP[u, j])
+            for u, side, j in joined(join_step, s, 3, JOINS):
+                quantize(u, j, GRP[u, j])
+            for u, side, j in joined(join_step, s, 0, JOINS):
+                natural_relu(u, j)
+            if at(s + 2) and at(s + 2)[1] < TRIPLE:
+                fold(*at(s + 2))
+            for u, side, j in joined(join_step, s, 2, JOINS):
                 natural_copy(u, j)
-            for u, side, j in due(sum_step, s, 0, SUMS):
+            if ranked(s):
+                transpose_raw(at(s)[0])
+            for u, side, j in summed(sum_step, s, 0, HALVES):
                 if inner_step(side, j) < sum_step(side, j):
                     add_transposed(u, side, j)
-            for u, side, j in due(sum_step, s, 2, NLAST):
+            for u, side, j in joined(join_step, s, 1, JOINS):
                 natural_transpose(u, j)
-            for u, side, j in due(sum_step, s, 0, SUMS):
+            for u, side, j in summed(sum_step, s, 0, HALVES):
                 if inner_step(side, j) == sum_step(side, j):
                     add_transposed(u, side, j)
-            if at(s) and at(s)[1] == 0:
-                transpose_raw(at(s)[0])
-            if at(s - 1) and at(s - 1)[1] == 0:
+            if ranked(s - 1):
                 silu(at(s - 1)[0])
-            if at(s - 8) and at(s - 8)[1] == 0:
+            if ranked(s - 8):
                 quantize(at(s - 8)[0], NB, GS[at(s - 8)[0]])
-            if s == -2:
-                coefficients()
-            if 1 <= s <= 4:
-                scale_weights((2 * s - 2, 2 * s - 1))
-            if s == 5:
-                order_base_weights()
             if 2 <= s <= 5:
-                turn_weights(2 * s - 4, 2 * s - 2)
+                scale_weights((2 * s - 4, 2 * s - 3))
             if s == 6:
-                turn_weights(NB, NPASS)
-            if s == 8:
+                order_other_weights()
+            if 3 <= s <= 6:
+                turn_weights(2 * s - 6, 2 * s - 4)
+            if s == 7:
+                turn_weights(NB, NPASS + 1)
+            if s == 9:
                 quantize_weights()
-            if at(s - 10) and at(s - 10)[1] == 0:
-                multiply(at(s - 10)[0])
-            if at(s - 11) and at(s - 11)[1] == 0:
-                store(at(s - 11)[0])
+            if ranked(s - LAG):
+                multiply(at(s - LAG)[0])
+            if ranked(s - LAG - 1):
+                store(at(s - LAG - 1)[0])

@@ -14,23 +14,20 @@ ACT = mybir.ActivationFunctionType
 P = 128
 B, IN, OUT, NB, NK = 8192, 512, 128, 8, 12
 PACK = IN // P
-CHT = 8
-NCH = B // (P * CHT)
 UT = 2
-UPC = CHT // UT
-NU = NCH * UPC
-UC = UT * IN
+UNITS = [1] + [UT] * (B // P // UT - 1) + [1]
+NU = len(UNITS)
+AHEAD = 3
 NPASS = NB + 1
 FLOPS = 2 * B * (IN + IN * NB) * OUT
 NQ = 5
 TRIPLE = NK - 2 * NQ
 NATURAL = (6, 7)
 EXTRA = 3
-EVERY = 4
-SHARED = (0, 1, 2)
+EVERY = 2
 SHIFT = 3
 LAG = 10
-INNER_ON_SCALAR = (1, 4)
+INNER_ON_SCALAR = (0, 1)
 LEFT, RIGHT = "left", "right"
 
 
@@ -72,7 +69,15 @@ def natural(u, j):
 
 
 def shared(u, j):
-    return j in SHARED and not natural(u, j) and not natural(u, j + SHIFT)
+    return 0 <= j < NB - SHIFT and not natural(u, j) and not (j + SHIFT == EXTRA and natural(u, j + SHIFT))
+
+
+def leads(u, side, j):
+    left = j if side == LEFT else j - SHIFT
+    if not shared(u, left):
+        return True
+    first = LEFT if inner_step(LEFT, left) <= inner_step(RIGHT, left + SHIFT) else RIGHT
+    return side == first
 
 
 def other(side):
@@ -85,33 +90,36 @@ def tile_bsplinekanlayer_t_kernel(tc, x, base_weight, spline_weight, spline_scal
         def pool(name, bufs):
             return ctx.enter_context(tc.tile_pool(name=name, bufs=bufs))
 
-        const, xpool, vpool, apool, sqpool = pool("const", 1), pool("xraw", 2), pool("v", 2), pool("a", 4), pool("sq", 3)
+        const, xpool, vpool, apool, sqpool = pool("const", 1), pool("xraw", 4), pool("v", 2), pool("a", 4), pool("sq", 3)
         kpool, w0pool, ipool, fpool = pool("w", 6), pool("w0", 2), pool("inner", 9), pool("first", 8)
         npool, gpool, gspool, cpool = pool("nat", 2), pool("grp", 5), pool("gs", 2), pool("codes", 2)
-        opool, wp = pool("ost", 3), pool("wsetup", 1)
+        opool, wp, wpair = pool("ost", 3), pool("wsetup", 1), pool("wpair", 2)
+        hold = pool("hold", 2)
         pslr = ctx.enter_context(tc.psum_pool(name="pslr", bufs=8))
         ctx.enter_context(tc.manual_schedule())
 
-        loaded = {}
+        def rows_of(dram, u):
+            r0 = sum(UNITS[:u]) * P
+            return dram[r0:r0 + UNITS[u] * P, :].rearrange("(p n) i -> p n i", n=UNITS[u])
 
-        def load_chunk(c):
-            xraw = xpool.tile([P, CHT, IN], BF16, name="xraw")
-            rows = x[c * CHT * P:(c + 1) * CHT * P, :].rearrange("(p n) i -> p n i", n=CHT)
-            pieces = UPC if c == 0 else 1
-            w = CHT // pieces
-            for q in range(pieces):
-                nc.sync.dma_start(out=xraw[:, q * w:(q + 1) * w, :], in_=rows[:, q * w:(q + 1) * w, :])
-            loaded[c] = xraw
+        RAW = {}
+
+        def load(u):
+            xraw = xpool.tile([P, UT, IN], BF16, name="xraw")
+            RAW[u] = xraw[:, 0:UNITS[u], :]
+            nc.sync.dma_start(out=RAW[u], in_=rows_of(x, u))
 
         g_bf = const.tile([P, NK], BF16, name="g_bf")
         nc.sync.dma_start(out=g_bf[:], in_=grid[0, :].partition_broadcast(P))
-        load_chunk(0)
+        load(0)
+        load(1)
         sw = wp.tile([P, IN * NB], BF16, name="sw")
         sc = wp.tile([P, IN], BF16, name="sc")
         bw = wp.tile([P, IN], BF16, name="bw")
         nc.sync.dma_start(out=sc[:], in_=spline_scaler)
         nc.sync.dma_start(out=sw[:], in_=spline_weight.rearrange("o i j -> o (i j)"))
         nc.sync.dma_start(out=bw[:], in_=base_weight)
+        load(2)
 
         ident = const.tile([P, P], BF16, name="ident")
         make_identity(nc, ident[:])
@@ -143,152 +151,150 @@ def tile_bsplinekanlayer_t_kernel(tc, x, base_weight, spline_weight, spline_scal
         COEF = {}
 
         def coefficients():
-            D = {}
-            for d in (1, 2, 3, 4):
-                D[d] = const.tile([P, NK - d], F32, name="D%d" % d)
-                nc.vector.tensor_tensor(out=D[d][:], in0=T[:, d:NK], in1=T[:, 0:NK - d], op=ALU.subtract)
-
-            def diff(d, j0):
-                return D[d][:, j0:j0 + NB]
-
-            def prod(name, factors):
-                acc = const.tile([P, NB], F32, name=name)
-                nc.vector.tensor_tensor(out=acc[:], in0=factors[0], in1=factors[1], op=ALU.mult)
-                for f in factors[2:]:
-                    nc.vector.tensor_tensor(out=acc[:], in0=acc[:], in1=f, op=ALU.mult)
-                return acc
-
-            def inverse(name, t):
-                r = const.tile([P, NB], F32, name=name)
-                nc.vector.reciprocal(out=r[:], in_=t[:])
+            def stacked(name, dl, jl, dr, jr):
+                r = const.tile([P, 2, NB], F32, name=name)
+                for k, (d, j0) in enumerate(((dl, jl), (dr, jr))):
+                    nc.vector.tensor_tensor(
+                        out=r[:, k, :], in0=T[:, j0 + d:j0 + d + NB], in1=T[:, j0:j0 + NB], op=ALU.subtract
+                    )
                 return r
 
-            def both_signs(key, name, t):
-                neg = const.tile([P, NB], F32, name=name + "_neg")
-                nc.vector.tensor_scalar(out=neg[:], in0=t[:], scalar1=-1.0, scalar2=None, op0=ALU.mult)
-                COEF[key, 1], COEF[key, -1] = t, neg
+            def times(name, p, q):
+                r = const.tile([P] + list(p.shape[1:]), F32, name=name)
+                nc.vector.tensor_tensor(out=r[:], in0=p, in1=q, op=ALU.mult)
+                return r
 
-            found = {}
-            for side, den, rnum, rden in (
-                (LEFT, ((1, 0), (2, 0), (3, 0)), ((4, 0), (2, 0), (3, 0)), ((1, 1), (2, 1), (3, 1))),
-                (RIGHT, ((3, 1), (2, 2), (1, 3)), ((4, 0), (3, 1), (2, 2)), ((3, 0), (2, 1), (1, 2))),
-            ):
-                outer = inverse("outer_" + side, prod("den_" + side, [diff(d, j0) for d, j0 in den]))
-                rinv = inverse("rinv_" + side, prod("rden_" + side, [diff(d, j0) for d, j0 in rden]))
-                ratio = prod("ratio_" + side, [diff(d, j0) for d, j0 in rnum] + [rinv[:]])
-                found[side] = outer, ratio
+            def inverse(name, p):
+                r = const.tile([P] + list(p.shape[1:]), F32, name=name)
+                nc.vector.reciprocal(out=r[:], in_=p)
+                return r
+
+            d1, d2, d3 = stacked("d1", 1, 0, 1, 3), stacked("d2", 2, 0, 2, 2), stacked("d3", 3, 0, 3, 1)
+            e1, e2, e3 = stacked("e1", 1, 1, 1, 2), stacked("e2", 2, 1, 2, 1), stacked("e3", 3, 1, 3, 0)
+            d4 = stacked("d4", 4, 0, 4, 0)
+            d23 = times("d23", d2[:], d3[:])
+            e12 = times("e12", e1[:], e2[:])
+            d123 = times("d123", d23[:], d1[:])
+            e123 = times("e123", e12[:], e3[:])
+            num = times("num", d23[:], d4[:])
+            iout = inverse("iout", d123[:])
+            irat = inverse("irat", e123[:])
+            ratio = times("ratio", num[:], irat[:])
+            iright = inverse("iright", ratio[:, 1, :])
+            quot = times("quot", ratio[:, 0, 0:NB - SHIFT], iright[:, SHIFT:NB])
+            full = times("full", iout[:, 1, :], ratio[:, 1, :])
+            ileft = inverse("ileft", ratio[:, 0, :])
+            iquot = inverse("iquot", quot[:])
             G = const.tile([P, NQ], F32, name="G")
-            nc.vector.memset(G[:], 1.0)
-            n = len(SHARED)
-            rinv = inverse("rinv", found[RIGHT][1])
-            q0 = SHARED[0] + 2
-            nc.vector.tensor_tensor(
-                out=G[:, q0:q0 + n], in0=found[LEFT][1][:, SHARED[0]:SHARED[0] + n],
-                in1=rinv[:, SHARED[0] + SHIFT:SHARED[0] + SHIFT + n], op=ALU.mult,
-            )
-            for k in range(q0 + 2, q0 + n):
-                nc.vector.tensor_tensor(out=G[:, k:k + 1], in0=G[:, k:k + 1], in1=G[:, k - 2:k - 1], op=ALU.mult)
-            y = const.tile([P, NQ], F32, name="root")
-            nc.vector.tensor_scalar(out=y[:], in0=G[:], scalar1=0.5, scalar2=0.5, op0=ALU.mult, op1=ALU.add)
-            for k in range(4):
-                yi = const.tile([P, NQ], F32, name="yi%d" % k)
-                nc.vector.reciprocal(out=yi[:], in_=y[:])
-                nc.vector.tensor_tensor(out=yi[:], in0=yi[:], in1=G[:], op=ALU.mult)
-                nc.vector.tensor_tensor(out=y[:], in0=y[:], in1=yi[:], op=ALU.add)
-                nc.vector.tensor_scalar(out=y[:], in0=y[:], scalar1=0.5, scalar2=None, op0=ALU.mult)
-            nrH = const.tile([P, NQ], F32, name="nrH")
-            nc.vector.tensor_tensor(out=nrH[:], in0=y[:], in1=negH[:], op=ALU.mult)
-            COEF["root"], COEF["nrH"] = y, nrH
+            nc.vector.tensor_tensor(out=G[:, 3:5], in0=full[:, 6:8], in1=ileft[:, 3:5], op=ALU.mult)
+            nc.vector.tensor_tensor(out=G[:, 1:3], in0=G[:, 3:5], in1=iquot[:, 1:3], op=ALU.mult)
+            nc.vector.tensor_tensor(out=G[:, 0:1], in0=G[:, 2:3], in1=iquot[:, 0:1], op=ALU.mult)
+            half_g = const.tile([P, NQ], F32, name="half_g")
+            nc.vector.tensor_scalar(out=half_g[:], in0=G[:], scalar1=0.5, scalar2=None, op0=ALU.mult)
+            y = const.tile([P, NQ], F32, name="y0")
+            nc.scalar.activation(out=y[:], in_=G[:], func=ACT.Sqrt)
+            yi = inverse("yi", y[:])
+            yg = times("yg", yi[:], half_g[:])
+            root = const.tile([P, NQ], F32, name="root")
+            nc.vector.scalar_tensor_tensor(out=root[:], in0=y[:], scalar=0.5, in1=yg[:], op0=ALU.mult, op1=ALU.add)
+            nrH = times("nrH", root[:], negH[:])
+            COEF["root"], COEF["nrH"] = root, nrH
+            return iout, ratio, G
+
+        def more_coefficients(iout, ratio, G):
             knotG = const.tile([P, NK], F32, name="knotG")
             for k in range(0, NK, NQ):
                 w = min(NQ, NK - k)
                 nc.vector.tensor_copy(out=knotG[:, k:k + w], in_=G[:, 0:w])
             invG = const.tile([P, NK], F32, name="invG")
             nc.vector.reciprocal(out=invG[:], in_=knotG[:])
-            for side, o0, i0 in ((LEFT, 0, 1), (RIGHT, 4, 3)):
-                outer, ratio = found[side]
-                outer = prod("outer2_" + side, [outer[:], invG[:, o0:o0 + NB]])
-                ratio = prod("ratio2_" + side, [ratio[:], knotG[:, o0:o0 + NB], invG[:, i0:i0 + NB]])
-                both_signs((side, "outer"), "outerc_" + side, outer)
-                both_signs((side, "ratio"), "ratioc_" + side, ratio)
-                both_signs((side, "inner"), "innerc_" + side, prod("inner_" + side, [outer[:], ratio[:]]))
+            for k, (side, o0, i0) in enumerate(((LEFT, 0, 1), (RIGHT, 4, 3))):
+                c = const.tile([P, 3, NB], F32, name="coef_" + side)
+                nc.vector.tensor_tensor(out=c[:, 0, :], in0=iout[:, k, :], in1=invG[:, o0:o0 + NB], op=ALU.mult)
+                nc.vector.tensor_tensor(out=c[:, 1, :], in0=ratio[:, k, :], in1=knotG[:, o0:o0 + NB], op=ALU.mult)
+                nc.vector.tensor_tensor(out=c[:, 1, :], in0=c[:, 1, :], in1=invG[:, i0:i0 + NB], op=ALU.mult)
+                nc.vector.tensor_tensor(out=c[:, 2, :], in0=c[:, 0, :], in1=c[:, 1, :], op=ALU.mult)
+                n = const.tile([P, 3, NB], F32, name="ncoef_" + side)
+                nc.vector.tensor_scalar(out=n[:], in0=c[:], scalar1=-1.0, scalar2=None, op0=ALU.mult)
+                for i, kind in enumerate(("outer", "ratio", "inner")):
+                    COEF[(side, kind), 1], COEF[(side, kind), -1] = c[:, i, :], n[:, i, :]
 
         def coef(side, kind, sign, j):
             return COEF[(side, kind), sign][:, j:j + 1]
 
         wcodes = const.tile([P, NPASS + 1, OUT], U32, name="wcodes", align_bytes=64)
         wscales = const.tile([P, NPASS + 1, OUT], U8, name="wscales", align_bytes=64)
-        ssw = wp.tile([P, NPASS + 1, IN], BF16, name="ssw")
-        wgrp = wp.tile([P, NPASS + 1, OUT, PACK], BF16, name="wgrp", align_bytes=64)
+        sw_j = sw[:].rearrange("o (i j) -> o j i", j=NB)
+        SSW, WGRP = {}, {}
 
         def by_pairs(row):
             return row.rearrange("o (h p e) -> o h e p", h=2, e=2)
 
-        def scale_weights(js):
-            sw_j = sw[:].rearrange("o (i j) -> o j i", j=NB)
-            for j in js:
-                if j in NATURAL:
-                    nc.vector.tensor_tensor(
-                        out=ssw[:, j, :].rearrange("o (h e p) -> o h e p", h=2, e=2), in0=by_pairs(sw_j[:, j, :]),
-                        in1=by_pairs(sc[:]), op=ALU.mult,
-                    )
+        def scale_weights(k):
+            ssw = wpair.tile([P, 2, IN], BF16, name="ssw")
+            for i in range(2):
+                a = 2 * k + i
+                pairs = ssw[:, i, :].rearrange("o (h e p) -> o h e p", h=2, e=2)
+                if a == NB:
+                    nc.vector.tensor_copy(out=pairs, in_=by_pairs(bw[:]))
+                elif a in NATURAL or a == NPASS:
+                    j = EXTRA if a == NPASS else a
+                    nc.vector.tensor_tensor(out=pairs, in0=by_pairs(sw_j[:, j, :]), in1=by_pairs(sc[:]), op=ALU.mult)
                 else:
-                    nc.vector.tensor_tensor(out=ssw[:, j, :], in0=sw_j[:, j, :], in1=sc[:], op=ALU.mult)
+                    nc.vector.tensor_tensor(out=ssw[:, i, :], in0=sw_j[:, a, :], in1=sc[:], op=ALU.mult)
+            SSW[k] = ssw
 
-        def order_other_weights():
-            nc.vector.tensor_tensor(
-                out=ssw[:, NPASS, :].rearrange("o (h e p) -> o h e p", h=2, e=2),
-                in0=by_pairs(sw[:].rearrange("o (i j) -> o j i", j=NB)[:, EXTRA, :]), in1=by_pairs(sc[:]), op=ALU.mult,
-            )
-            nc.vector.tensor_copy(out=ssw[:, NB, :].rearrange("o (h e p) -> o h e p", h=2, e=2), in_=by_pairs(bw[:]))
-
-        def turn_weights(a0, a1):
+        def turn_weights(k):
             ps_w = pslr.tile([P, 2, PACK, P], BF16, name="ps_w", tag="lr")
-            for a in range(a0, a1):
+            for i in range(2):
                 for t in range(PACK):
-                    nc.tensor.transpose(ps_w[:, a - a0, t, :], ssw[:, a, t * P:(t + 1) * P], ident[:])
-            nc.scalar.copy(out=wgrp[:, a0:a1, :, :], in_=ps_w[:, 0:a1 - a0, :, :].rearrange("p j t o -> p j o t"))
+                    nc.tensor.transpose(ps_w[:, i, t, :], SSW[k][:, i, t * P:(t + 1) * P], ident[:])
+            wgrp = wpair.tile([P, 2, OUT, PACK], BF16, name="wgrp", align_bytes=64)
+            nc.scalar.copy(out=wgrp[:], in_=ps_w[:].rearrange("p j t o -> p j o t"))
+            WGRP[k] = wgrp
 
-        def quantize_weights():
-            for a0, a1 in ((0, NB), (NB, NPASS + 1)):
-                nc.vector.quantize_mx(
-                    out=wcodes[:, a0:a1, :].rearrange("p a o -> p (a o)").bitcast(FP8X4),
-                    scales=wscales[:, a0:a1, :].rearrange("p a o -> p (a o)"),
-                    in_=wgrp[:, a0:a1, :, :].rearrange("p a o t -> p (a o t)"),
-                )
+        def quantize_weights(k):
+            nc.vector.quantize_mx(
+                out=wcodes[:, 2 * k:2 * k + 2, :].rearrange("p a o -> p (a o)").bitcast(FP8X4),
+                scales=wscales[:, 2 * k:2 * k + 2, :].rearrange("p a o -> p (a o)"),
+                in_=WGRP[k][:].rearrange("p a o t -> p (a o t)"),
+            )
 
         V, A, SQ, W, INNER, PS, FIRST, GRP, CODES, SCALES, ACC, GS, XPS, NAT, NPS = ({} for i in range(15))
 
-        def raw(u):
-            return loaded[u // UPC][:, (u % UPC) * UT:(u % UPC + 1) * UT, :]
+        def columns(u, tile):
+            return tile[:, 0:UNITS[u] * IN]
+
+        def packed(u, tile):
+            return tile[:, 0:UNITS[u], :, :]
 
         def clamp(u):
             for k in range(TRIPLE):
-                v = vpool.tile([P, UC], BF16, name="v", tag="v%d" % k)
+                v = columns(u, vpool.tile([P, UT * IN], BF16, name="v", tag="v%d" % k))
                 nc.vector.tensor_scalar(
-                    out=v[:], in0=raw(u).rearrange("p n i -> p (n i)"), scalar1=T[:, k:k + 1],
+                    out=v[:], in0=RAW[u].rearrange("p n i -> p (n i)"), scalar1=T[:, k:k + 1],
                     scalar2=T[:, 2 * NQ + k:2 * NQ + k + 1], op0=ALU.max, op1=ALU.min,
                 )
                 V[u, k] = v
 
         def distance(u, q):
-            a = apool.tile([P, UC], F32, name="a")
+            a = columns(u, apool.tile([P, UT * IN], F32, name="a"))
             v = V[u, 1 if q == 1 else 0]
             nc.scalar.activation(out=a[:], in_=v[:], func=ACT.Abs, bias=negC[:, q:q + 1], scale=1.0)
             A[u, q] = a
 
         def fold(u, q):
-            a = apool.tile([P, UC], F32, name="a")
+            a = columns(u, apool.tile([P, UT * IN], F32, name="a"))
             nc.scalar.activation(out=a[:], in_=A[u, q][:], func=ACT.Abs, bias=negE[:, q:q + 1], scale=1.0)
             A[u, q] = a
 
         def square(u, q):
-            sq = sqpool.tile([P, UC], F32, name="sq")
+            sq = columns(u, sqpool.tile([P, UT * IN], F32, name="sq"))
             nc.scalar.activation(out=sq[:], in_=A[u, q][:], func=ACT.Square, bias=COEF["nrH"][:, q:q + 1], scale=COEF["root"][:, q:q + 1])
             SQ[u, q] = sq
 
         def cube(u, q):
-            w = (w0pool if q == 0 else kpool).tile([P, UC], F32, name="w")
+            w = columns(u, (w0pool if q == 0 else kpool).tile([P, UT * IN], F32, name="w"))
             nc.vector.scalar_tensor_tensor(
                 out=w[:], in0=A[u, q][:], scalar=H[:, q:q + 1], in1=SQ[u, q][:], op0=ALU.subtract, op1=ALU.mult
             )
@@ -296,10 +302,14 @@ def tile_bsplinekanlayer_t_kernel(tc, x, base_weight, spline_weight, spline_scal
 
         def inner(u, side, j, scalar):
             o, so, i, si = half(side, j)
-            t = ipool.tile([P, UC], F32, name="t")
+            left = j if side == LEFT else j - SHIFT
+            if side == RIGHT and shared(u, left):
+                t = columns(u, hold.tile([P, UT * IN], F32, name="t"))
+            else:
+                t = columns(u, ipool.tile([P, UT * IN], F32, name="t"))
             INNER[u, side, j] = t
-            if side == LEFT and shared(u, j):
-                INNER[u, RIGHT, j + SHIFT] = t
+            if shared(u, left):
+                INNER[u, other(side), left if side == RIGHT else left + SHIFT] = t
             if natural(u, j):
                 scale, positive = coef(side, "inner", si, j), True
             else:
@@ -314,13 +324,14 @@ def tile_bsplinekanlayer_t_kernel(tc, x, base_weight, spline_weight, spline_scal
 
         def on_scalar(u, side, j):
             can = natural(u, j) or half(side, j)[1] < 0
-            return can and inner_step(side, j) < sum_step(side, j) and inner_step(side, j) in INNER_ON_SCALAR
+            spare = natural(u, EXTRA) and j in NATURAL
+            return can and inner_step(side, j) < sum_step(side, j) and (inner_step(side, j) in INNER_ON_SCALAR or spare)
 
         def add_transposed(u, side, j):
             outer = W[u, half(side, j)[0]]
             second = INNER[u, side, j]
             sums = []
-            for n in range(UT):
+            for n in range(UNITS[u]):
                 ps = pslr.tile([P, PACK, P], F32, name="ps", tag="lr")
                 for t in range(PACK):
                     cols = slice(n * IN + t * P, n * IN + (t + 1) * P)
@@ -330,8 +341,8 @@ def tile_bsplinekanlayer_t_kernel(tc, x, base_weight, spline_weight, spline_scal
             PS[u, side, j] = sums
 
         def read_first(u, side, j):
-            f = fpool.tile([P, UT, P, PACK], BF16, name="f")
-            for n in range(UT):
+            f = packed(u, fpool.tile([P, UT, P, PACK], BF16, name="f"))
+            for n in range(UNITS[u]):
                 nc.scalar.activation(
                     out=f[:, n, :, :], in_=PS[u, side, j][n][:].rearrange("p t b -> p b t"), func=ACT.Relu,
                     scale=coef(side, "outer", half(side, j)[1], j),
@@ -339,8 +350,8 @@ def tile_bsplinekanlayer_t_kernel(tc, x, base_weight, spline_weight, spline_scal
             FIRST[u, j] = f
 
         def finish(u, side, j):
-            grp = gpool.tile([P, UT, P, PACK], BF16, name="grp", align_bytes=64)
-            for n in range(UT):
+            grp = packed(u, gpool.tile([P, UT, P, PACK], BF16, name="grp", align_bytes=64))
+            for n in range(UNITS[u]):
                 nc.vector.scalar_tensor_tensor(
                     out=grp[:, n, :, :], in0=PS[u, side, j][n][:].rearrange("p t b -> p b t"),
                     scalar=coef(side, "outer", half(side, j)[1], j), in1=FIRST[u, j][:, n, :, :],
@@ -348,9 +359,14 @@ def tile_bsplinekanlayer_t_kernel(tc, x, base_weight, spline_weight, spline_scal
                 )
             GRP[u, j] = grp
 
+        def unpacked(ps):
+            return ps[:].rearrange("p n h b -> p (n h b)").bitcast(BF16).rearrange(
+                "p (n h b e) -> p n b h e", n=UT, h=2, e=2
+            )
+
         def natural_half(u, side, j):
             o, so, i, si = half(side, j)
-            y = npool.tile([P, UC], BF16, name="y", tag="y%d%s" % (j, side))
+            y = columns(u, npool.tile([P, UT * IN], BF16, name="y", tag="y%d%s" % (j, side)))
             nc.vector.scalar_tensor_tensor(
                 out=y[:], in0=W[u, o][:], scalar=coef(side, "outer", so, j), in1=INNER[u, side, j][:],
                 op0=ALU.mult, op1=ALU.subtract,
@@ -361,25 +377,22 @@ def tile_bsplinekanlayer_t_kernel(tc, x, base_weight, spline_weight, spline_scal
             y = NAT[u, RIGHT, j]
             nc.vector.tensor_tensor(out=y[:], in0=NAT[u, LEFT, j][:], in1=y[:], op=ALU.max)
 
-        def natural_relu(u, j):
-            y = NAT[u, RIGHT, j]
-            nc.vector.tensor_scalar(out=y[:], in0=y[:], scalar1=0.0, scalar2=None, op0=ALU.max)
-
         def natural_transpose(u, j):
             words = NAT[u, RIGHT, j][:].bitcast(F32)
             ps_n = pslr.tile([P, UT, 2, P], F32, name="ps_n", tag="lr")
-            for n in range(UT):
+            for n in range(UNITS[u]):
                 for h in range(2):
                     q = 2 * n + h
                     nc.tensor.transpose(ps_n[:, n, h, :], words[:, q * P:(q + 1) * P], ident_f[:])
             NPS[u, j] = ps_n
 
         def natural_copy(u, j):
-            grp = gpool.tile([P, UT, P, PACK], BF16, name="grp", align_bytes=64)
-            nc.scalar.copy(
-                out=grp[:].rearrange("p n b t -> p (n b t)").bitcast(F32).rearrange("p (n b h) -> p n b h", n=UT, h=2),
-                in_=NPS[u, j][:].rearrange("p n h b -> p n b h"),
-            )
+            grp = packed(u, gpool.tile([P, UT, P, PACK], BF16, name="grp", align_bytes=64))
+            values = unpacked(NPS[u, j])
+            for n in range(UNITS[u]):
+                nc.scalar.activation(
+                    out=grp[:, n, :, :].rearrange("p b (h e) -> p b h e", e=2), in_=values[:, n, :, :, :], func=ACT.Relu
+                )
             GRP[u, j] = grp
 
         def quantize(u, a, src):
@@ -389,25 +402,23 @@ def tile_bsplinekanlayer_t_kernel(tc, x, base_weight, spline_weight, spline_scal
                 CODES[u] = codes
                 SCALES[u] = scales
             nc.vector.quantize_mx(
-                out=CODES[u][:, a, :, :].rearrange("p n b -> p (n b)").bitcast(FP8X4),
-                scales=SCALES[u][:, a, :, :].rearrange("p n b -> p (n b)"),
+                out=CODES[u][:, a, 0:UNITS[u], :].rearrange("p n b -> p (n b)").bitcast(FP8X4),
+                scales=SCALES[u][:, a, 0:UNITS[u], :].rearrange("p n b -> p (n b)"),
                 in_=src[:].rearrange("p n b t -> p (n b t)"),
             )
 
         def transpose_raw(u):
             ps_x = pslr.tile([P, UT, 2, P], F32, name="ps_x", tag="lr")
-            for n in range(UT):
-                words = raw(u)[:, n, :].bitcast(F32)
+            for n in range(UNITS[u]):
+                words = RAW[u][:, n, :].bitcast(F32)
                 for h in range(2):
                     nc.tensor.transpose(ps_x[:, n, h, :], words[:, h * P:(h + 1) * P], ident_f[:])
             XPS[u] = ps_x
 
         def silu(u):
-            gs = gspool.tile([P, UT, P, PACK], BF16, name="gs", align_bytes=64)
-            values = XPS[u][:].rearrange("p n h b -> p (n h b)").bitcast(BF16).rearrange(
-                "p (n h b e) -> p n b h e", n=UT, h=2, e=2
-            )
-            for n in range(UT):
+            gs = packed(u, gspool.tile([P, UT, P, PACK], BF16, name="gs", align_bytes=64))
+            values = unpacked(XPS[u])
+            for n in range(UNITS[u]):
                 nc.scalar.activation(
                     out=gs[:, n, :, :].rearrange("p b (h e) -> p b h e", e=2), in_=values[:, n, :, :, :], func=ACT.Silu
                 )
@@ -416,7 +427,7 @@ def tile_bsplinekanlayer_t_kernel(tc, x, base_weight, spline_weight, spline_scal
         def multiply(u):
             w = [NPASS if a == EXTRA and natural(u, a) else a for a in range(NPASS)]
             acc = pslr.tile([P, UT, OUT], F32, name="acc", tag="lr")
-            for n in range(UT):
+            for n in range(UNITS[u]):
                 for a in range(NPASS):
                     nc.tensor.matmul_mx(
                         out=acc[:, n, :],
@@ -431,10 +442,9 @@ def tile_bsplinekanlayer_t_kernel(tc, x, base_weight, spline_weight, spline_scal
 
         def store(u):
             ost = opool.tile([P, UT, OUT], F32, name="ost")
-            nc.scalar.copy(out=ost[:], in_=ACC[u][:])
-            c, q = u // UPC, u % UPC
-            rows = out[c * CHT * P:(c + 1) * CHT * P, :].rearrange("(p n) o -> p n o", n=CHT)
-            nc.sync.dma_start(out=rows[:, q * UT:(q + 1) * UT, :], in_=ost[:])
+            part = ost[:, 0:UNITS[u], :]
+            nc.scalar.copy(out=part, in_=ACC[u][:, 0:UNITS[u], :])
+            nc.sync.dma_start(out=rows_of(out, u), in_=part)
 
         NS = NU * NQ
 
@@ -466,21 +476,23 @@ def tile_bsplinekanlayer_t_kernel(tc, x, base_weight, spline_weight, spline_scal
             if ranked(s + 3):
                 u = at(s + 3)[0]
                 clamp(u)
-                if u % UPC == 1 and u // UPC + 1 < NCH:
-                    load_chunk(u // UPC + 1)
+                if u + AHEAD < NU:
+                    load(u + AHEAD)
+            if at(s + 2):
+                distance(*at(s + 2))
             if s == -1:
-                coefficients()
+                first_coefficients = coefficients()
+            if s == 0:
+                more_coefficients(*first_coefficients)
             if at(s + 1):
                 square(*at(s + 1))
             for u, side, j in due(inner_step, s, 0, HALVES):
-                if not on_scalar(u, side, j) and not (side == RIGHT and shared(u, j - SHIFT)):
+                if not on_scalar(u, side, j) and leads(u, side, j):
                     inner(u, side, j, False)
-            if at(s + 2):
-                distance(*at(s + 2))
             for u, side, j in summed(sum_step, s, 1, FIRSTS):
                 read_first(u, side, j)
             for u, side, j in due(inner_step, s, 0, HALVES):
-                if on_scalar(u, side, j) and not (side == RIGHT and shared(u, j - SHIFT)):
+                if on_scalar(u, side, j) and leads(u, side, j):
                     inner(u, side, j, True)
             for u, side, j in summed(sum_step, s, 1, SECONDS):
                 finish(u, side, j)
@@ -494,8 +506,6 @@ def tile_bsplinekanlayer_t_kernel(tc, x, base_weight, spline_weight, spline_scal
                 quantize(u, j, GRP[u, j])
             for u, side, j in joined(join_step, s, 3, JOINS):
                 quantize(u, j, GRP[u, j])
-            for u, side, j in joined(join_step, s, 0, JOINS):
-                natural_relu(u, j)
             if at(s + 2) and at(s + 2)[1] < TRIPLE:
                 fold(*at(s + 2))
             for u, side, j in joined(join_step, s, 2, JOINS):
@@ -514,16 +524,12 @@ def tile_bsplinekanlayer_t_kernel(tc, x, base_weight, spline_weight, spline_scal
                 silu(at(s - 1)[0])
             if ranked(s - 8):
                 quantize(at(s - 8)[0], NB, GS[at(s - 8)[0]])
-            if 2 <= s <= 5:
-                scale_weights((2 * s - 4, 2 * s - 3))
-            if s == 6:
-                order_other_weights()
-            if 3 <= s <= 6:
-                turn_weights(2 * s - 6, 2 * s - 4)
-            if s == 7:
-                turn_weights(NB, NPASS + 1)
-            if s == 9:
-                quantize_weights()
+            if 2 <= s < 7:
+                scale_weights(s - 2)
+            if 3 <= s < 8:
+                turn_weights(s - 3)
+            if 5 <= s < 10:
+                quantize_weights(s - 5)
             if ranked(s - LAG):
                 multiply(at(s - LAG)[0])
             if ranked(s - LAG - 1):

@@ -27,7 +27,7 @@ EXTRA = 3
 EVERY = 2
 SHIFT = 3
 LAG = 10
-INNER_ON_SCALAR = (0, 1)
+INNER_ON_SCALAR = (0, 1, 4)
 LEFT, RIGHT = "left", "right"
 
 
@@ -377,6 +377,10 @@ def tile_bsplinekanlayer_t_kernel(tc, x, base_weight, spline_weight, spline_scal
             y = NAT[u, RIGHT, j]
             nc.vector.tensor_tensor(out=y[:], in0=NAT[u, LEFT, j][:], in1=y[:], op=ALU.max)
 
+        def natural_relu(u, j):
+            y = NAT[u, RIGHT, j]
+            nc.vector.tensor_scalar(out=y[:], in0=y[:], scalar1=0.0, scalar2=None, op0=ALU.max)
+
         def natural_transpose(u, j):
             words = NAT[u, RIGHT, j][:].bitcast(F32)
             ps_n = pslr.tile([P, UT, 2, P], F32, name="ps_n", tag="lr")
@@ -388,11 +392,10 @@ def tile_bsplinekanlayer_t_kernel(tc, x, base_weight, spline_weight, spline_scal
 
         def natural_copy(u, j):
             grp = packed(u, gpool.tile([P, UT, P, PACK], BF16, name="grp", align_bytes=64))
-            values = unpacked(NPS[u, j])
-            for n in range(UNITS[u]):
-                nc.scalar.activation(
-                    out=grp[:, n, :, :].rearrange("p b (h e) -> p b h e", e=2), in_=values[:, n, :, :, :], func=ACT.Relu
-                )
+            nc.scalar.copy(
+                out=grp.rearrange("p n b t -> p (n b t)").bitcast(F32).rearrange("p (n b h) -> p n b h", n=UNITS[u], h=2),
+                in_=NPS[u, j][:, 0:UNITS[u], :, :].rearrange("p n h b -> p n b h"),
+            )
             GRP[u, j] = grp
 
         def quantize(u, a, src):
@@ -508,6 +511,8 @@ def tile_bsplinekanlayer_t_kernel(tc, x, base_weight, spline_weight, spline_scal
                 quantize(u, j, GRP[u, j])
             if at(s + 2) and at(s + 2)[1] < TRIPLE:
                 fold(*at(s + 2))
+            for u, side, j in joined(join_step, s, 0, JOINS):
+                natural_relu(u, j)
             for u, side, j in joined(join_step, s, 2, JOINS):
                 natural_copy(u, j)
             if ranked(s):

@@ -23,11 +23,10 @@ FLOPS = 2 * B * (IN + IN * NB) * OUT
 NQ = 5
 TRIPLE = NK - 2 * NQ
 NATURAL = (6, 7)
-EXTRA = 3
+EXTRA = 0
 EVERY = 2
 SHIFT = 3
 LAG = 10
-INNER_ON_SCALAR = (0, 1, 4)
 LEFT, RIGHT = "left", "right"
 
 
@@ -148,17 +147,20 @@ def tile_bsplinekanlayer_t_kernel(tc, x, base_weight, spline_weight, spline_scal
 
         negC, negE, negH = negative("negC", C), negative("negE", E), negative("negH", H)
 
+        def stacked(name, dl, jl, dr, jr):
+            r = const.tile([P, 2, NB], F32, name=name)
+            for k, (d, j0) in enumerate(((dl, jl), (dr, jr))):
+                nc.vector.tensor_tensor(
+                    out=r[:, k, :], in0=T[:, j0 + d:j0 + d + NB], in1=T[:, j0:j0 + NB], op=ALU.subtract
+                )
+            return r
+
+        d1, d2, d3 = stacked("d1", 1, 0, 1, 3), stacked("d2", 2, 0, 2, 2), stacked("d3", 3, 0, 3, 1)
+        e1, e2, e3 = stacked("e1", 1, 1, 1, 2), stacked("e2", 2, 1, 2, 1), stacked("e3", 3, 1, 3, 0)
+        d4 = stacked("d4", 4, 0, 4, 0)
         COEF = {}
 
         def coefficients():
-            def stacked(name, dl, jl, dr, jr):
-                r = const.tile([P, 2, NB], F32, name=name)
-                for k, (d, j0) in enumerate(((dl, jl), (dr, jr))):
-                    nc.vector.tensor_tensor(
-                        out=r[:, k, :], in0=T[:, j0 + d:j0 + d + NB], in1=T[:, j0:j0 + NB], op=ALU.subtract
-                    )
-                return r
-
             def times(name, p, q):
                 r = const.tile([P] + list(p.shape[1:]), F32, name=name)
                 nc.vector.tensor_tensor(out=r[:], in0=p, in1=q, op=ALU.mult)
@@ -169,9 +171,6 @@ def tile_bsplinekanlayer_t_kernel(tc, x, base_weight, spline_weight, spline_scal
                 nc.vector.reciprocal(out=r[:], in_=p)
                 return r
 
-            d1, d2, d3 = stacked("d1", 1, 0, 1, 3), stacked("d2", 2, 0, 2, 2), stacked("d3", 3, 0, 3, 1)
-            e1, e2, e3 = stacked("e1", 1, 1, 1, 2), stacked("e2", 2, 1, 2, 1), stacked("e3", 3, 1, 3, 0)
-            d4 = stacked("d4", 4, 0, 4, 0)
             d23 = times("d23", d2[:], d3[:])
             e12 = times("e12", e1[:], e2[:])
             d123 = times("d123", d23[:], d1[:])
@@ -323,9 +322,7 @@ def tile_bsplinekanlayer_t_kernel(tc, x, base_weight, spline_weight, spline_scal
                 )
 
         def on_scalar(u, side, j):
-            can = natural(u, j) or half(side, j)[1] < 0
-            spare = natural(u, EXTRA) and j in NATURAL
-            return can and inner_step(side, j) < sum_step(side, j) and (inner_step(side, j) in INNER_ON_SCALAR or spare)
+            return (natural(u, j) or half(side, j)[1] < 0) and inner_step(side, j) < sum_step(side, j)
 
         def add_transposed(u, side, j):
             outer = W[u, half(side, j)[0]]

from contextlib import ExitStack

import concourse.mybir as mybir
from concourse.masks import make_identity

F32 = mybir.dt.float32
BF16 = mybir.dt.bfloat16
U32 = mybir.dt.uint32
U8 = mybir.dt.uint8
FP8X4 = mybir.dt.float8_e4m3fn_x4
ALU = mybir.AluOpType
ACT = mybir.ActivationFunctionType

P = 128
B, IN, OUT, NB, NK = 8192, 512, 128, 8, 12
PACK = IN // P
UT = 2
UNITS = [1] + [UT] * (B // P // UT - 1) + [1]
NU = len(UNITS)
AHEAD = 3
NPASS = NB + 1
FLOPS = 2 * B * (IN + IN * NB) * OUT
NQ = 5
TRIPLE = NK - 2 * NQ
NATURAL = (6, 7)
EXTRA = 0
EVERY = 2
SHIFT = 3
LAG = 10
LEFT, RIGHT = "left", "right"


def half(side, j):
    if side == LEFT:
        outer, inner, up = j, j + 1, 1
    else:
        outer, inner, up = j + 4, j + 3, -1
    return outer % NQ, up if outer // NQ % 2 else -up, inner % NQ, up if inner // NQ % 2 else -up


def wraps(side, j):
    o, so, i, si = half(side, j)
    return abs(o - i) == NQ - 1


def sum_step(side, j):
    o, so, i, si = half(side, j)
    return NQ if wraps(side, j) else max(o, i)


def inner_step(side, j):
    return NQ - 1 if wraps(side, j) else half(side, j)[2]


def natural_step(side, j):
    return sum_step(side, j) + (1 if inner_step(side, j) == sum_step(side, j) else 0)


def join_step(side, j):
    return 1 + max(natural_step(LEFT, j), natural_step(RIGHT, j))


HALVES = [(side, j) for j in range(NB) for side in (LEFT, RIGHT)]


def natural(u, j):
    return j in NATURAL or (j == EXTRA and u % EVERY == EVERY - 1)


def shared(u, j):
    return 0 <= j < NB - SHIFT and not natural(u, j) and not (j + SHIFT == EXTRA and natural(u, j + SHIFT))


def leads(u, side, j):
    left = j if side == LEFT else j - SHIFT
    if not shared(u, left):
        return True
    first = LEFT if inner_step(LEFT, left) <= inner_step(RIGHT, left + SHIFT) else RIGHT
    return side == first


def other(side):
    return RIGHT if side == LEFT else LEFT


def tile_bsplinekanlayer_t_kernel(tc, x, base_weight, spline_weight, spline_scaler, grid, out):
    nc = tc.nc
    with ExitStack() as ctx:
        def pool(name, bufs):
            return ctx.enter_context(tc.tile_pool(name=name, bufs=bufs))

        const, xpool, vpool, apool, sqpool = pool("const", 1), pool("xraw", 4), pool("v", 2), pool("a", 4), pool("sq", 3)
        kpool, w0pool, ipool, fpool = pool("w", 6), pool("w0", 2), pool("inner", 9), pool("first", 8)
        npool, gpool, gspool, cpool = pool("nat", 2), pool("grp", 5), pool("gs", 2), pool("codes", 2)
        opool, wp, wpair = pool("ost", 3), pool("wsetup", 1), pool("wpair", 2)
        hold = pool("hold", 2)
        pslr = ctx.enter_context(tc.psum_pool(name="pslr", bufs=8))
        ctx.enter_context(tc.manual_schedule())

        def rows_of(dram, u):
            r0 = sum(UNITS[:u]) * P
            return dram[r0:r0 + UNITS[u] * P, :].rearrange("(p n) i -> p n i", n=UNITS[u])

        RAW = {}

        def load(u):
            xraw = xpool.tile([P, UT, IN], BF16, name="xraw")
            RAW[u] = xraw[:, 0:UNITS[u], :]
            nc.sync.dma_start(out=RAW[u], in_=rows_of(x, u))

        g_bf = const.tile([P, NK], BF16, name="g_bf")
        nc.sync.dma_start(out=g_bf[:], in_=grid[0, :].partition_broadcast(P))
        load(0)
        load(1)
        sw = wp.tile([P, IN * NB], BF16, name="sw")
        sc = wp.tile([P, IN], BF16, name="sc")
        bw = wp.tile([P, IN], BF16, name="bw")
        nc.sync.dma_start(out=sc[:], in_=spline_scaler)
        nc.sync.dma_start(out=sw[:], in_=spline_weight.rearrange("o i j -> o (i j)"))
        nc.sync.dma_start(out=bw[:], in_=base_weight)
        load(2)

        ident = const.tile([P, P], BF16, name="ident")
        make_identity(nc, ident[:])
        ident_f = const.tile([P, P], F32, name="ident_f")
        make_identity(nc, ident_f[:])

        T = const.tile([P, NK], F32, name="T")
        nc.vector.tensor_copy(out=T[:], in_=g_bf[:])
        def small(name, in0, in1, op, scale=None):
            r = const.tile([P, in0.shape[1]], F32, name=name)
            nc.vector.tensor_tensor(out=r[:], in0=in0, in1=in1, op=op)
            if scale is not None:
                nc.vector.tensor_scalar(out=r[:], in0=r[:], scalar1=scale, scalar2=None, op0=ALU.mult)
            return r

        C = small("C", T[:, 0:NQ], T[:, NQ:2 * NQ], ALU.add, 0.5)
        H = small("H", T[:, NQ:2 * NQ], T[:, 0:NQ], ALU.subtract, 0.5)
        far = small("far", T[:, 2 * NQ:NK], H[:, 0:TRIPLE], ALU.add)
        E = small("E", far[:], C[:, 0:TRIPLE], ALU.subtract, 0.5)
        nc.vector.tensor_tensor(out=C[:, 0:TRIPLE], in0=C[:, 0:TRIPLE], in1=E[:], op=ALU.add)

        def negative(name, t):
            r = const.tile([P, t.shape[1]], F32, name=name)
            nc.vector.tensor_scalar(out=r[:], in0=t[:], scalar1=-1.0, scalar2=None, op0=ALU.mult)
            return r

        negC, negE, negH = negative("negC", C), negative("negE", E), negative("negH", H)

        def stacked(name, dl, jl, dr, jr):
            r = const.tile([P, 2, NB], F32, name=name)
            for k, (d, j0) in enumerate(((dl, jl), (dr, jr))):
                nc.vector.tensor_tensor(
                    out=r[:, k, :], in0=T[:, j0 + d:j0 + d + NB], in1=T[:, j0:j0 + NB], op=ALU.subtract
                )
            return r

        d1, d2, d3 = stacked("d1", 1, 0, 1, 3), stacked("d2", 2, 0, 2, 2), stacked("d3", 3, 0, 3, 1)
        e1, e2, e3 = stacked("e1", 1, 1, 1, 2), stacked("e2", 2, 1, 2, 1), stacked("e3", 3, 1, 3, 0)
        d4 = stacked("d4", 4, 0, 4, 0)
        COEF = {}

        def coefficients():
            def times(name, p, q):
                r = const.tile([P] + list(p.shape[1:]), F32, name=name)
                nc.vector.tensor_tensor(out=r[:], in0=p, in1=q, op=ALU.mult)
                return r

            def inverse(name, p):
                r = const.tile([P] + list(p.shape[1:]), F32, name=name)
                nc.vector.reciprocal(out=r[:], in_=p)
                return r

            d23 = times("d23", d2[:], d3[:])
            e12 = times("e12", e1[:], e2[:])
            d123 = times("d123", d23[:], d1[:])
            e123 = times("e123", e12[:], e3[:])
            num = times("num", d23[:], d4[:])
            iout = inverse("iout", d123[:])
            irat = inverse("irat", e123[:])
            ratio = times("ratio", num[:], irat[:])
            iright = inverse("iright", ratio[:, 1, :])
            quot = times("quot", ratio[:, 0, 0:NB - SHIFT], iright[:, SHIFT:NB])
            full = times("full", iout[:, 1, :], ratio[:, 1, :])
            ileft = inverse("ileft", ratio[:, 0, :])
            iquot = inverse("iquot", quot[:])
            G = const.tile([P, NQ], F32, name="G")
            nc.vector.tensor_tensor(out=G[:, 3:5], in0=full[:, 6:8], in1=ileft[:, 3:5], op=ALU.mult)
            nc.vector.tensor_tensor(out=G[:, 1:3], in0=G[:, 3:5], in1=iquot[:, 1:3], op=ALU.mult)
            nc.vector.tensor_tensor(out=G[:, 0:1], in0=G[:, 2:3], in1=iquot[:, 0:1], op=ALU.mult)
            half_g = const.tile([P, NQ], F32, name="half_g")
            nc.vector.tensor_scalar(out=half_g[:], in0=G[:], scalar1=0.5, scalar2=None, op0=ALU.mult)
            y = const.tile([P, NQ], F32, name="y0")
            nc.scalar.activation(out=y[:], in_=G[:], func=ACT.Sqrt)
            yi = inverse("yi", y[:])
            yg = times("yg", yi[:], half_g[:])
            root = const.tile([P, NQ], F32, name="root")
            nc.vector.scalar_tensor_tensor(out=root[:], in0=y[:], scalar=0.5, in1=yg[:], op0=ALU.mult, op1=ALU.add)
            nrH = times("nrH", root[:], negH[:])
            COEF["root"], COEF["nrH"] = root, nrH
            return iout, ratio, G

        def more_coefficients(iout, ratio, G):
            knotG = const.tile([P, NK], F32, name="knotG")
            for k in range(0, NK, NQ):
                w = min(NQ, NK - k)
                nc.vector.tensor_copy(out=knotG[:, k:k + w], in_=G[:, 0:w])
            invG = const.tile([P, NK], F32, name="invG")
            nc.vector.reciprocal(out=invG[:], in_=knotG[:])
            for k, (side, o0, i0) in enumerate(((LEFT, 0, 1), (RIGHT, 4, 3))):
                c = const.tile([P, 3, NB], F32, name="coef_" + side)
                nc.vector.tensor_tensor(out=c[:, 0, :], in0=iout[:, k, :], in1=invG[:, o0:o0 + NB], op=ALU.mult)
                nc.vector.tensor_tensor(out=c[:, 1, :], in0=ratio[:, k, :], in1=knotG[:, o0:o0 + NB], op=ALU.mult)
                nc.vector.tensor_tensor(out=c[:, 1, :], in0=c[:, 1, :], in1=invG[:, i0:i0 + NB], op=ALU.mult)
                nc.vector.tensor_tensor(out=c[:, 2, :], in0=c[:, 0, :], in1=c[:, 1, :], op=ALU.mult)
                n = const.tile([P, 3, NB], F32, name="ncoef_" + side)
                nc.vector.tensor_scalar(out=n[:], in0=c[:], scalar1=-1.0, scalar2=None, op0=ALU.mult)
                for i, kind in enumerate(("outer", "ratio", "inner")):
                    COEF[(side, kind), 1], COEF[(side, kind), -1] = c[:, i, :], n[:, i, :]

        def coef(side, kind, sign, j):
            return COEF[(side, kind), sign][:, j:j + 1]

        wcodes = const.tile([P, NPASS + 1, OUT], U32, name="wcodes", align_bytes=64)
        wscales = const.tile([P, NPASS + 1, OUT], U8, name="wscales", align_bytes=64)
        sw_j = sw[:].rearrange("o (i j) -> o j i", j=NB)
        SSW, WGRP = {}, {}

        def by_pairs(row):
            return row.rearrange("o (h p e) -> o h e p", h=2, e=2)

        def scale_weights(k):
            ssw = wpair.tile([P, 2, IN], BF16, name="ssw")
            for i in range(2):
                a = 2 * k + i
                pairs = ssw[:, i, :].rearrange("o (h e p) -> o h e p", h=2, e=2)
                if a == NB:
                    nc.vector.tensor_copy(out=pairs, in_=by_pairs(bw[:]))
                elif a in NATURAL or a == NPASS:
                    j = EXTRA if a == NPASS else a
                    nc.vector.tensor_tensor(out=pairs, in0=by_pairs(sw_j[:, j, :]), in1=by_pairs(sc[:]), op=ALU.mult)
                else:
                    nc.vector.tensor_tensor(out=ssw[:, i, :], in0=sw_j[:, a, :], in1=sc[:], op=ALU.mult)
            SSW[k] = ssw

        def turn_weights(k):
            ps_w = pslr.tile([P, 2, PACK, P], BF16, name="ps_w", tag="lr")
            for i in range(2):
                for t in range(PACK):
                    nc.tensor.transpose(ps_w[:, i, t, :], SSW[k][:, i, t * P:(t + 1) * P], ident[:])
            wgrp = wpair.tile([P, 2, OUT, PACK], BF16, name="wgrp", align_bytes=64)
            nc.scalar.copy(out=wgrp[:], in_=ps_w[:].rearrange("p j t o -> p j o t"))
            WGRP[k] = wgrp

        def quantize_weights(k):
            nc.vector.quantize_mx(
                out=wcodes[:, 2 * k:2 * k + 2, :].rearrange("p a o -> p (a o)").bitcast(FP8X4),
                scales=wscales[:, 2 * k:2 * k + 2, :].rearrange("p a o -> p (a o)"),
                in_=WGRP[k][:].rearrange("p a o t -> p (a o t)"),
            )

        V, A, SQ, W, INNER, PS, FIRST, GRP, CODES, SCALES, ACC, GS, XPS, NAT, NPS = ({} for i in range(15))

        def columns(u, tile):
            return tile[:, 0:UNITS[u] * IN]

        def packed(u, tile):
            return tile[:, 0:UNITS[u], :, :]

        def clamp(u):
            for k in range(TRIPLE):
                v = columns(u, vpool.tile([P, UT * IN], BF16, name="v", tag="v%d" % k))
                nc.vector.tensor_scalar(
                    out=v[:], in0=RAW[u].rearrange("p n i -> p (n i)"), scalar1=T[:, k:k + 1],
                    scalar2=T[:, 2 * NQ + k:2 * NQ + k + 1], op0=ALU.max, op1=ALU.min,
                )
                V[u, k] = v

        def distance(u, q):
            a = columns(u, apool.tile([P, UT * IN], F32, name="a"))
            v = V[u, 1 if q == 1 else 0]
            nc.scalar.activation(out=a[:], in_=v[:], func=ACT.Abs, bias=negC[:, q:q + 1], scale=1.0)
            A[u, q] = a

        def fold(u, q):
            a = columns(u, apool.tile([P, UT * IN], F32, name="a"))
            nc.scalar.activation(out=a[:], in_=A[u, q][:], func=ACT.Abs, bias=negE[:, q:q + 1], scale=1.0)
            A[u, q] = a

        def square(u, q):
            sq = columns(u, sqpool.tile([P, UT * IN], F32, name="sq"))
            nc.scalar.activation(out=sq[:], in_=A[u, q][:], func=ACT.Square, bias=COEF["nrH"][:, q:q + 1], scale=COEF["root"][:, q:q + 1])
            SQ[u, q] = sq

        def cube(u, q):
            w = columns(u, (w0pool if q == 0 else kpool).tile([P, UT * IN], F32, name="w"))
            nc.vector.scalar_tensor_tensor(
                out=w[:], in0=A[u, q][:], scalar=H[:, q:q + 1], in1=SQ[u, q][:], op0=ALU.subtract, op1=ALU.mult
            )
            W[u, q] = w

        def inner(u, side, j, scalar):
            o, so, i, si = half(side, j)
            left = j if side == LEFT else j - SHIFT
            if side == RIGHT and shared(u, left):
                t = columns(u, hold.tile([P, UT * IN], F32, name="t"))
            else:
                t = columns(u, ipool.tile([P, UT * IN], F32, name="t"))
            INNER[u, side, j] = t
            if shared(u, left):
                INNER[u, other(side), left if side == RIGHT else left + SHIFT] = t
            if natural(u, j):
                scale, positive = coef(side, "inner", si, j), True
            else:
                scale, positive = coef(side, "ratio", -so * si, j), so < 0
            if scalar:
                nc.scalar.activation(out=t[:], in_=W[u, i][:], func=ACT.Relu, scale=scale)
            else:
                nc.vector.tensor_scalar(
                    out=t[:], in0=W[u, i][:], scalar1=scale, scalar2=0.0, op0=ALU.mult,
                    op1=ALU.max if positive else ALU.min,
                )

        def on_scalar(u, side, j):
            return (natural(u, j) or half(side, j)[1] < 0) and inner_step(side, j) < sum_step(side, j)

        def add_transposed(u, side, j):
            outer = W[u, half(side, j)[0]]
            second = INNER[u, side, j]
            sums = []
            for n in range(UNITS[u]):
                ps = pslr.tile([P, PACK, P], F32, name="ps", tag="lr")
                for t in range(PACK):
                    cols = slice(n * IN + t * P, n * IN + (t + 1) * P)
                    nc.tensor.matmul(ps[:, t, :], lhsT=outer[:, cols], rhs=ident_f[:], start=True, stop=False, is_transpose=True)
                    nc.tensor.matmul(ps[:, t, :], lhsT=second[:, cols], rhs=ident_f[:], start=False, stop=True, is_transpose=True)
                sums.append(ps)
            PS[u, side, j] = sums

        def read_first(u, side, j):
            f = packed(u, fpool.tile([P, UT, P, PACK], BF16, name="f"))
            for n in range(UNITS[u]):
                nc.scalar.activation(
                    out=f[:, n, :, :], in_=PS[u, side, j][n][:].rearrange("p t b -> p b t"), func=ACT.Relu,
                    scale=coef(side, "outer", half(side, j)[1], j),
                )
            FIRST[u, j] = f

        def finish(u, side, j):
            grp = packed(u, gpool.tile([P, UT, P, PACK], BF16, name="grp", align_bytes=64))
            for n in range(UNITS[u]):
                nc.vector.scalar_tensor_tensor(
                    out=grp[:, n, :, :], in0=PS[u, side, j][n][:].rearrange("p t b -> p b t"),
                    scalar=coef(side, "outer", half(side, j)[1], j), in1=FIRST[u, j][:, n, :, :],
                    op0=ALU.mult, op1=ALU.max,
                )
            GRP[u, j] = grp

        def unpacked(ps):
            return ps[:].rearrange("p n h b -> p (n h b)").bitcast(BF16).rearrange(
                "p (n h b e) -> p n b h e", n=UT, h=2, e=2
            )

        def natural_half(u, side, j):
            o, so, i, si = half(side, j)
            y = columns(u, npool.tile([P, UT * IN], BF16, name="y", tag="y%d%s" % (j, side)))
            nc.vector.scalar_tensor_tensor(
                out=y[:], in0=W[u, o][:], scalar=coef(side, "outer", so, j), in1=INNER[u, side, j][:],
                op0=ALU.mult, op1=ALU.subtract,
            )
            NAT[u, side, j] = y

        def natural_join(u, j):
            y = NAT[u, RIGHT, j]
            nc.vector.tensor_tensor(out=y[:], in0=NAT[u, LEFT, j][:], in1=y[:], op=ALU.max)

        def natural_relu(u, j):
            y = NAT[u, RIGHT, j]
            nc.vector.tensor_scalar(out=y[:], in0=y[:], scalar1=0.0, scalar2=None, op0=ALU.max)

        def natural_transpose(u, j):
            words = NAT[u, RIGHT, j][:].bitcast(F32)
            ps_n = pslr.tile([P, UT, 2, P], F32, name="ps_n", tag="lr")
            for n in range(UNITS[u]):
                for h in range(2):
                    q = 2 * n + h
                    nc.tensor.transpose(ps_n[:, n, h, :], words[:, q * P:(q + 1) * P], ident_f[:])
            NPS[u, j] = ps_n

        def natural_copy(u, j):
            grp = packed(u, gpool.tile([P, UT, P, PACK], BF16, name="grp", align_bytes=64))
            nc.scalar.copy(
                out=grp.rearrange("p n b t -> p (n b t)").bitcast(F32).rearrange("p (n b h) -> p n b h", n=UNITS[u], h=2),
                in_=NPS[u, j][:, 0:UNITS[u], :, :].rearrange("p n h b -> p n b h"),
            )
            GRP[u, j] = grp

        def quantize(u, a, src):
            if u not in CODES:
                codes = cpool.tile([P, NPASS, UT, P], U32, name="codes", align_bytes=64)
                scales = cpool.tile([P, NPASS, UT, P], U8, name="scales", align_bytes=64)
                CODES[u] = codes
                SCALES[u] = scales
            nc.vector.quantize_mx(
                out=CODES[u][:, a, 0:UNITS[u], :].rearrange("p n b -> p (n b)").bitcast(FP8X4),
                scales=SCALES[u][:, a, 0:UNITS[u], :].rearrange("p n b -> p (n b)"),
                in_=src[:].rearrange("p n b t -> p (n b t)"),
            )

        def transpose_raw(u):
            ps_x = pslr.tile([P, UT, 2, P], F32, name="ps_x", tag="lr")
            for n in range(UNITS[u]):
                words = RAW[u][:, n, :].bitcast(F32)
                for h in range(2):
                    nc.tensor.transpose(ps_x[:, n, h, :], words[:, h * P:(h + 1) * P], ident_f[:])
            XPS[u] = ps_x

        def silu(u):
            gs = packed(u, gspool.tile([P, UT, P, PACK], BF16, name="gs", align_bytes=64))
            values = unpacked(XPS[u])
            for n in range(UNITS[u]):
                nc.scalar.activation(
                    out=gs[:, n, :, :].rearrange("p b (h e) -> p b h e", e=2), in_=values[:, n, :, :, :], func=ACT.Silu
                )
            GS[u] = gs

        def multiply(u):
            w = [NPASS if a == EXTRA and natural(u, a) else a for a in range(NPASS)]
            acc = pslr.tile([P, UT, OUT], F32, name="acc", tag="lr")
            for n in range(UNITS[u]):
                for a in range(NPASS):
                    nc.tensor.matmul_mx(
                        out=acc[:, n, :],
                        lhsT=CODES[u][:, a, n, :].bitcast(FP8X4),
                        lhsT_scale=SCALES[u][:, a, n, :],
                        rhs=wcodes[:, w[a], :].bitcast(FP8X4),
                        rhs_scale=wscales[:, w[a], :],
                        start=(a == 0),
                        stop=(a == NPASS - 1),
                    )
            ACC[u] = acc

        def store(u):
            ost = opool.tile([P, UT, OUT], F32, name="ost")
            part = ost[:, 0:UNITS[u], :]
            nc.scalar.copy(out=part, in_=ACC[u][:, 0:UNITS[u], :])
            nc.sync.dma_start(out=rows_of(out, u), in_=part)

        NS = NU * NQ

        def at(s):
            return (s // NQ, s % NQ) if 0 <= s < NS else None

        def due(step_of, s, lag, halves):
            found = []
            for side, j in halves:
                start = s - lag - step_of(side, j)
                if start % NQ == 0 and 0 <= start < NS:
                    found.append((start // NQ, side, j))
            return found

        FIRSTS = [(side, j) for side, j in HALVES if sum_step(side, j) < sum_step(other(side), j)]
        SECONDS = [(side, j) for side, j in HALVES if (side, j) not in FIRSTS]
        JOINS = [(LEFT, j) for j in range(NB)]

        def summed(step_of, s, lag, halves):
            return [h for h in due(step_of, s, lag, halves) if not natural(h[0], h[2])]

        def joined(step_of, s, lag, halves):
            return [h for h in due(step_of, s, lag, halves) if natural(h[0], h[2])]

        def ranked(s):
            return at(s) and at(s)[1] == 0

        for s in range(-3, NS + 2 * NQ):
            if ranked(s + 3):
                u = at(s + 3)[0]
                clamp(u)
                if u + AHEAD < NU:
                    load(u + AHEAD)
            if at(s + 2):
                distance(*at(s + 2))
            if s == -1:
                first_coefficients = coefficients()
            if s == 0:
                more_coefficients(*first_coefficients)
            if at(s + 1):
                square(*at(s + 1))
            for u, side, j in due(inner_step, s, 0, HALVES):
                if not on_scalar(u, side, j) and leads(u, side, j):
                    inner(u, side, j, False)
            for u, side, j in summed(sum_step, s, 1, FIRSTS):
                read_first(u, side, j)
            for u, side, j in due(inner_step, s, 0, HALVES):
                if on_scalar(u, side, j) and leads(u, side, j):
                    inner(u, side, j, True)
            for u, side, j in summed(sum_step, s, 1, SECONDS):
                finish(u, side, j)
            for u, side, j in joined(natural_step, s, 0, HALVES):
                natural_half(u, side, j)
            if at(s + 1):
                cube(*at(s + 1))
            for u, side, j in joined(join_step, s, 0, JOINS):
                natural_join(u, j)
            for u, side, j in summed(sum_step, s, 2, SECONDS):
                quantize(u, j, GRP[u, j])
            for u, side, j in joined(join_step, s, 3, JOINS):
                quantize(u, j, GRP[u, j])
            if at(s + 2) and at(s + 2)[1] < TRIPLE:
                fold(*at(s + 2))
            for u, side, j in joined(join_step, s, 0, JOINS):
                natural_relu(u, j)
            for u, side, j in joined(join_step, s, 2, JOINS):
                natural_copy(u, j)
            if ranked(s):
                transpose_raw(at(s)[0])
            for u, side, j in summed(sum_step, s, 0, HALVES):
                if inner_step(side, j) < sum_step(side, j):
                    add_transposed(u, side, j)
            for u, side, j in joined(join_step, s, 1, JOINS):
                natural_transpose(u, j)
            for u, side, j in summed(sum_step, s, 0, HALVES):
                if inner_step(side, j) == sum_step(side, j):
                    add_transposed(u, side, j)
            if ranked(s - 1):
                silu(at(s - 1)[0])
            if ranked(s - 8):
                quantize(at(s - 8)[0], NB, GS[at(s - 8)[0]])
            if 2 <= s < 7:
                scale_weights(s - 2)
            if 3 <= s < 8:
                turn_weights(s - 3)
            if 5 <= s < 10:
                quantize_weights(s - 5)
            if ranked(s - LAG):
                multiply(at(s - LAG)[0])
            if ranked(s - LAG - 1):
                store(at(s - LAG - 1)[0])
